import numpy as np
import ml_dtypes


def mxq(x, axis, fmt="e4m3"):
    dtype, down = {"e4m3": (ml_dtypes.float8_e4m3fn, 7), "e5m2": (ml_dtypes.float8_e5m2, 14)}[fmt]
    v = np.moveaxis(np.asarray(x, np.float32).astype(ml_dtypes.bfloat16).astype(np.float64), axis, -1)
    blocks = v.reshape(v.shape[:-1] + (-1, 32))
    amax = np.abs(blocks).max(-1, keepdims=True)
    byte = np.maximum(np.where(amax > 0, np.frexp(amax)[1] - 1 + 127, 0) - down, 1)
    scale = np.exp2(byte - 127.0)
    codes = (blocks / scale).astype(np.float32).astype(dtype).astype(np.float64)
    return np.moveaxis((codes * scale).reshape(v.shape), -1, axis)


WIDE = False


def mx_kscale(k):
    if not WIDE:
        return np.ones(k)
    levels = np.array([10, -10, 5, -5, 0])
    if k % 512:
        return np.exp2(np.random.permutation(np.resize(levels, k // 32))).repeat(32)
    a = np.empty((k // 512, 16))
    for p in range(k // 512):
        a[p, :8] = np.random.permutation(np.resize(levels, 8))
        for g in range(8):
            far = levels[np.abs(levels - a[p, g]) >= 10]
            a[p, g + 8] = far[np.random.randint(len(far))]
    return np.exp2(a.ravel()).repeat(32)


BF16 = ml_dtypes.bfloat16


def bf(x):
    return np.asarray(x, np.float32).astype(BF16)


def f64(x):
    return np.asarray(x).astype(np.float64)


E2M1 = np.array([0.0, 0.5, 1.0, 1.5, 2.0, 3.0, 4.0, 6.0, -0.0, -0.5, -1.0, -1.5, -2.0, -3.0, -4.0, -6.0])


def pack_weight(w, fmt):
    k, n = w.shape
    w = f64(bf(w)).reshape(k // 32, 32, n)
    amax = np.abs(w).max(1)
    if fmt == "e4m3":
        byte = np.frexp(amax)[1] - 1 + 127 - 7
    else:
        mant, ex = np.frexp(amax / 6.0)
        byte = np.where(mant > 0.5, ex, ex - 1) + 127
    byte = np.clip(np.where(amax > 0, byte, 1), 1, 254)
    scaled = (w * np.exp2(127.0 - byte)[:, None, :]).reshape(k, n).astype(np.float32)
    by_word = np.ascontiguousarray(scaled.reshape(k // 512, 128, 4, n).transpose(0, 1, 3, 2))
    if fmt == "e4m3":
        words = by_word.astype(ml_dtypes.float8_e4m3fn).view(np.uint8)
    else:
        c = by_word.astype(ml_dtypes.float4_e2m1fn).view(np.uint8) & 0xF
        words = c[..., 0::2] | (c[..., 1::2] << 4)
    return np.ascontiguousarray(words), np.ascontiguousarray(byte.astype(np.uint8).reshape(k // 512, 16, n))


def unpack_weight(words, scales, fmt):
    g, p, n, _ = words.shape
    if fmt == "e4m3":
        vals = np.ascontiguousarray(words).view(ml_dtypes.float8_e4m3fn).astype(np.float64)
    else:
        nib = np.empty((g, p, n, 4), np.uint8)
        nib[..., 0::2] = words & 0xF
        nib[..., 1::2] = words >> 4
        vals = E2M1[nib]
    vals = vals * np.repeat(np.exp2(scales.astype(np.float64) - 127.0), 8, axis=1)[..., None]
    return vals.transpose(0, 1, 3, 2).reshape(g * 512, n)
def pack4(w):
    words, scales = pack_weight(w, "e2m1")
    return words.reshape(words.shape[0], 128, -1), scales


def unpack4(words, scales):
    return unpack_weight(words.reshape(words.shape[0], 128, -1, 2), scales, "e2m1")


NU, NI, D = 1024, 1024, 512
N = NU + NI


def draw0():
    s, t = mx_kscale(N), mx_kscale(D)
    A = bf(np.random.uniform(0.0, 2.0 / np.sqrt(N), (N, N)) * s)
    features = bf(np.random.standard_normal((N, D)) / s[:, None] * t)
    Wg_words, Wg_scales = pack4(np.random.standard_normal((D, D)) / np.sqrt(D) / t[:, None])
    return {"A": A,
            "features": features,
            "Wg_words": Wg_words,
            "Wg_scales": Wg_scales,
            "bg": bf(np.random.standard_normal(D) * 0.1)}


def core(A, features, Wg_words, Wg_scales, bg):
    agg = mxq(f64(A), 1, "e4m3") @ mxq(f64(features), 0, "e4m3")
    return np.maximum((mxq(agg, 1, "e4m3") @ unpack4(Wg_words, Wg_scales)) + f64(bg), 0.0)


def e4m3fn_bytes(y):
    return np.clip(np.asarray(y, np.float64), -448.0, 448.0).astype(np.float32).astype(ml_dtypes.float8_e4m3fn).view(np.uint8)


def e4m3fn_values(b):
    return np.asarray(b, np.uint8).view(ml_dtypes.float8_e4m3fn).astype(np.float64)


def setup_inputs():
    d = draw0()
    x0 = np.asarray(d['A']).astype(np.float64)
    s = (np.max(np.abs(x0), axis=(0,), keepdims=True) / 448.0).astype(np.float32)
    out = {}
    for k, v in d.items():
        if k == 'A':
            out['A_bytes'] = e4m3fn_bytes(x0 / s.astype(np.float64))
            out['A_scale'] = s
        else:
            out[k] = v
    return out


def reference(A_bytes, A_scale, features, Wg_words, Wg_scales, bg):
    return core(e4m3fn_values(A_bytes) * A_scale.astype(np.float64), features, Wg_words, Wg_scales, bg)

@@ -1,0 +1,512 @@
+from contextlib import ExitStack
+
+import concourse.mybir as mybir
+from concourse.masks import make_identity
+
+F32 = mybir.dt.float32
+BF16 = mybir.dt.bfloat16
+U32 = mybir.dt.uint32
+I32 = mybir.dt.int32
+U8 = mybir.dt.uint8
+FP8 = mybir.dt.float8_e4m3fn
+FP8X4 = mybir.dt.float8_e4m3fn_x4
+FP4X4 = mybir.dt.float4_e2m1fn_x4
+ALU = mybir.AluOpType
+ACT = mybir.ActivationFunctionType
+
+NODES = 2048
+D = 512
+P = 128
+PASSES = NODES // 512
+TILES = NODES // P
+FLOPS = 2 * NODES * NODES * D + 2 * NODES * D * D
+
+
+def tile_net_pa_w4_kernel(tc, A_bytes, A_scale, features, Wg_words, Wg_scales, bg, out):
+    nc = tc.nc
+    with ExitStack() as ctx:
+        keep = ctx.enter_context(tc.tile_pool(name="keep", bufs=1))
+        flow = ctx.enter_context(tc.tile_pool(name="flow", bufs=3))
+        psum = ctx.enter_context(tc.psum_pool(name="psum", bufs=1))
+        ctx.enter_context(tc.manual_schedule())
+
+        codes_in = [keep.tile([P, NODES], U8, name="abytes%d" % r, align_bytes=64) for r in range(TILES)]
+        vecs = keep.tile([P, PASSES + 1, 4], F32, name="vecs")
+        bias_raw = keep.tile([P, 4], BF16, name="biasraw")
+        spread = keep.tile([P, PASSES + 1, D], F32, name="spread", align_bytes=64)
+        bias = spread[:, PASSES, :]
+        f_raw = [keep.tile([P, 4, D], BF16, name="fraw%d" % g, align_bytes=64) for g in range(PASSES)]
+        f_grp = [keep.tile([P, 4, P, 4], BF16, name="fgrp%d" % g, align_bytes=64) for g in range(PASSES)]
+        f_codes = [keep.tile([P, D], U32, name="fcodes%d" % g, align_bytes=64) for g in range(PASSES)]
+        f_scales = [keep.tile([P, D], U8, name="fscales%d" % g, align_bytes=64) for g in range(PASSES)]
+        w_words = keep.tile([P, 2 * D], U8, name="wwords", align_bytes=64)
+        w_scales = keep.tile([P, D], U8, name="wscales", align_bytes=64)
+        bias_col = keep.tile([P, 4], F32, name="biascol")
+        ident = keep.tile([P, P], F32, name="ident", align_bytes=64)
+        dummy = keep.tile([P, 1], F32, name="dummy")
+        dummy2 = keep.tile([P, 1], F32, name="dummy2")
+
+        def load_a(r):
+            nc.sync.dma_start(out=codes_in[r][:], in_=A_bytes[r * P : (r + 1) * P, :])
+
+        def load_f(g):
+            nc.sync.dma_start(out=f_raw[g][:], in_=features.rearrange("(g p j) c -> g p j c", p=P, j=4)[g])
+
+        def load_scale():
+            nc.sync.dma_start(out=vecs[:, 0:PASSES, :], in_=A_scale.rearrange("o (g p t) -> p (o g) t", p=P, t=4))
+
+        def spread_turn(g):
+            bank = psum.tile([P, 4, P], F32, name="spreadbank", tag="turn", bufs=4)
+            banks["s", g] = bank
+            for t in range(4):
+                nc.tensor.transpose(bank[:, t, :], vecs[:, g, t : t + 1].to_broadcast([P, P]), ident[:])
+
+        def spread_out(g, engine):
+            dst = spread[:, g, :].rearrange("p (n t) -> p n t", t=4)
+            src = banks["s", g][:].rearrange("p t n -> p n t")
+            if engine == "v":
+                nc.vector.tensor_copy(out=dst, in_=src)
+            else:
+                nc.scalar.copy(out=dst, in_=src)
+
+        def load_bias():
+            nc.sync.dma_start(out=bias_raw[:], in_=bg.rearrange("(p t) -> p t", t=4))
+
+        def bias_cast():
+            nc.vector.tensor_copy(out=vecs[:, PASSES, :], in_=bias_raw[:])
+
+        def load_w():
+            nc.sync.dma_start(out=w_words[:], in_=Wg_words.rearrange("g p w -> p (g w)"))
+            for q in range(4):
+                nc.sync.dma_start(
+                    out=w_scales[32 * q : 32 * q + 4, :].bitcast(I32),
+                    in_=Wg_scales.rearrange("g q n -> (g q) n")[4 * q : 4 * q + 4, :].bitcast(I32),
+                )
+
+        nc.vector.memset(dummy[:], 0.0)
+        nc.scalar.copy(out=dummy2[:], in_=dummy[:])
+        nc.vector.memset(w_scales[:].bitcast(I32), 0)
+        make_identity(nc, ident[:])
+
+        banks = {}
+        load_scale()
+        load_bias()
+        load_f(0)
+        load_a(0)
+        load_f(1)
+        load_a(1)
+        load_f(2)
+        load_f(3)
+        load_a(2)
+        load_w()
+        load_a(3)
+        load_a(4)
+        load_a(5)
+        load_a(6)
+        load_a(7)
+        load_a(8)
+        load_a(9)
+        load_a(10)
+        load_a(11)
+        load_a(12)
+        load_a(13)
+        load_a(14)
+        load_a(15)
+
+        wide = {}
+        grouped = {}
+        a_codes = {}
+        a_scales = {}
+        acc = {}
+        g_bf = {}
+        g_codes = {}
+        g_scales = {}
+        mid = {}
+        t1 = {}
+        t2 = {}
+
+        def scaled(r, half):
+            if r not in wide:
+                wide[r] = flow.tile([P, NODES], BF16, name="wide", bufs=5, align_bytes=64)
+            cols = slice(half * 1024, (half + 1) * 1024)
+            nc.vector.tensor_tensor(
+                out=wide[r][:, cols], in0=codes_in[r][:, cols].bitcast(FP8), in1=spread[:, 2 * half : 2 * half + 2, :].rearrange("p g k -> p (g k)"), op=ALU.mult
+            )
+
+        def turn(r, b):
+            words = wide[r][:].bitcast(F32)
+            bank = psum.tile([P, 2, 2, P], F32, name="turn", tag="turn", bufs=4)
+            banks[r, b] = bank
+            for gl in range(2):
+                for u in range(2):
+                    w0 = 256 * (2 * b + gl)
+                    nc.tensor.transpose(bank[:, u, gl, :], words[:, w0 + u : w0 + 256 : 2], ident[:])
+
+        def turned(r, b, engine):
+            if r not in grouped:
+                grouped[r] = flow.tile([P, PASSES, P, 4], BF16, name="grouped", bufs=4, align_bytes=64)
+            dst = grouped[r][:, 2 * b : 2 * b + 2].bitcast(F32)
+            src = banks[r, b][:].rearrange("p u g i -> p g i u")
+            if engine == "v":
+                nc.vector.tensor_copy(out=dst, in_=src)
+            else:
+                nc.scalar.copy(out=dst, in_=src)
+
+        def quant_a(r):
+            a_codes[r] = flow.tile([P, PASSES, P], U32, name="acodes", bufs=4, align_bytes=64)
+            a_scales[r] = flow.tile([P, PASSES, P], U8, name="ascales", bufs=4, align_bytes=64)
+            nc.vector.quantize_mx(
+                out=a_codes[r][:].rearrange("p g i -> p (g i)").bitcast(FP8X4),
+                scales=a_scales[r][:].rearrange("p g i -> p (g i)"),
+                in_=grouped[r][:].rearrange("p g i t -> p (g i t)"),
+            )
+
+        def first_matmul(r):
+            acc[r] = psum.tile([P, 4, P], F32, name="acc", bufs=1)
+            for t in range(4):
+                for g in range(PASSES):
+                    nc.tensor.matmul_mx(
+                        out=acc[r][:, t, :],
+                        lhsT=f_codes[g][:, t * P : (t + 1) * P].bitcast(FP8X4),
+                        lhsT_scale=f_scales[g][:, t * P : (t + 1) * P],
+                        rhs=a_codes[r][:, g, :].bitcast(FP8X4),
+                        rhs_scale=a_scales[r][:, g, :],
+                        start=(g == 0),
+                        stop=(g == PASSES - 1),
+                    )
+
+        def agg_out(r, engine="s"):
+            g_bf[r] = flow.tile([P, P, 4], BF16, name="gbf", bufs=3, align_bytes=64)
+            src = acc[r][:].rearrange("p t i -> p i t")
+            if engine == "v":
+                nc.vector.tensor_copy(out=g_bf[r][:], in_=src)
+            else:
+                nc.scalar.copy(out=g_bf[r][:], in_=src)
+
+        def quant_agg(r):
+            g_codes[r] = flow.tile([P, P], U32, name="gcodes", bufs=3, align_bytes=64)
+            g_scales[r] = flow.tile([P, P], U8, name="gscales", bufs=3, align_bytes=64)
+            nc.vector.quantize_mx(
+                out=g_codes[r][:].bitcast(FP8X4),
+                scales=g_scales[r][:],
+                in_=g_bf[r][:].rearrange("p i t -> p (i t)"),
+            )
+
+        def second_matmul(r):
+            mid[r] = psum.tile([P, D], F32, name="mid", bufs=2)
+            nc.tensor.matmul_mx(
+                out=mid[r][:],
+                lhsT=g_codes[r][:].bitcast(FP8X4),
+                lhsT_scale=g_scales[r][:],
+                rhs=w_words[:].bitcast(FP4X4),
+                rhs_scale=w_scales[:],
+                start=True,
+                stop=True,
+            )
+
+        def second_matmul_t(r):
+            mid[r] = psum.tile([P, D], F32, name="mid", bufs=2)
+            for c in range(4):
+                nc.tensor.matmul_mx(
+                    out=mid[r][:, c * P : (c + 1) * P],
+                    lhsT=w_words[:, 2 * c * P : 2 * (c + 1) * P].bitcast(FP4X4),
+                    lhsT_scale=w_scales[:, c * P : (c + 1) * P],
+                    rhs=g_codes[r][:].bitcast(FP8X4),
+                    rhs_scale=g_scales[r][:],
+                    start=True,
+                    stop=True,
+                )
+
+        def relu_t(r, cs, engine="s"):
+            if r not in t1:
+                t1[r] = flow.tile([P, 4, P], F32, name="t1", bufs=3, align_bytes=64)
+            for c in cs:
+                nc.scalar.activation(
+                    out=t1[r][:, c, :], in_=mid[r][:, c * P : (c + 1) * P], func=ACT.Relu, bias=bias_col[:, c : c + 1]
+                )
+
+        def turn_back(r):
+            t2[r] = psum.tile([P, 4, P], F32, name="t2", bufs=1)
+            for c in range(4):
+                nc.tensor.transpose(t2[r][:, c, :], t1[r][:, c, :], ident[:])
+
+        def back_out(r, engine="s"):
+            fin = flow.tile([P, D], F32, name="fin", bufs=4, align_bytes=64)
+            src = t2[r][:].rearrange("p c n -> p (c n)")
+            if engine == "v":
+                nc.vector.tensor_copy(out=fin[:], in_=src)
+            else:
+                nc.scalar.copy(out=fin[:], in_=src)
+            nc.sync.dma_start(out=out[r * P : (r + 1) * P, :], in_=fin[:])
+
+        def bias_column():
+            bank = psum.tile([P, 4, P], F32, name="biasbank", tag="t2", bufs=1)
+            for c in range(4):
+                nc.tensor.transpose(bank[:, c, :], bias[:, c * P : (c + 1) * P], ident[:])
+            nc.vector.tensor_copy(out=bias_col[:].rearrange("p (c o) -> p c o", o=1), in_=bank[:, :, 0:1])
+
+        def f_interleave(g, engine):
+            src = f_raw[g][:].rearrange("p j (m t) -> p t m j", t=4)
+            if engine == "v":
+                nc.vector.tensor_copy(out=f_grp[g][:], in_=src)
+            elif engine == "s":
+                nc.scalar.copy(out=f_grp[g][:], in_=src)
+            else:
+                nc.gpsimd.tensor_scalar(out=f_grp[g][:], in0=src, scalar1=1.0, scalar2=0.0, op0=ALU.mult, op1=ALU.add)
+
+        def f_quant(g):
+            nc.vector.quantize_mx(
+                out=f_codes[g][:].bitcast(FP8X4),
+                scales=f_scales[g][:],
+                in_=f_grp[g][:].rearrange("p t m j -> p (t m j)"),
+            )
+
+        summed = {}
+
+        def add_v(r):
+            summed[r] = flow.tile([P, D], F32, name="summed", bufs=4, align_bytes=64)
+            nc.vector.tensor_tensor(out=summed[r][:], in0=mid[r][:], in1=bias, op=ALU.add)
+
+        def relu(r, engine):
+            fin = flow.tile([P, D], F32, name="fin", bufs=4, align_bytes=64)
+            if engine == "v":
+                nc.vector.tensor_scalar(out=fin[:], in0=summed[r][:], scalar1=0.0, scalar2=None, op0=ALU.max)
+            else:
+                nc.scalar.activation(out=fin[:], in_=summed[r][:], func=ACT.Relu)
+            nc.sync.dma_start(out=out[r * P : (r + 1) * P, :], in_=fin[:])
+
+        bias_cast()
+        spread_turn(1)
+        spread_turn(0)
+        spread_out(1, "s")
+        spread_turn(3)
+        spread_out(0, "s")
+        f_interleave(0, "v")
+        spread_turn(2)
+        spread_out(3, "s")
+        f_interleave(1, "s")
+        f_quant(0)
+        spread_out(2, "s")
+        spread_turn(4)
+        spread_out(4, "s")
+        f_interleave(3, "s")
+        scaled(1, 0)
+        f_interleave(2, "s")
+        scaled(0, 0)
+        scaled(0, 1)
+        turn(0, 0)
+        scaled(3, 0)
+        turned(0, 0, "s")
+        turn(0, 1)
+        turned(0, 1, "s")
+        turn(1, 0)
+        scaled(1, 1)
+        scaled(2, 0)
+        f_quant(3)
+        f_quant(1)
+        f_quant(2)
+        quant_a(0)
+        turn(1, 1)
+        scaled(2, 1)
+        turn(2, 0)
+        first_matmul(0)
+        scaled(5, 0)
+        turned(1, 0, "s")
+        turned(1, 1, "s")
+        turned(2, 0, "s")
+        agg_out(0, "s")
+        quant_a(1)
+        turn(2, 1)
+        turned(2, 1, "s")
+        turn(3, 0)
+        first_matmul(1)
+        scaled(3, 1)
+        scaled(4, 0)
+        agg_out(1, "s")
+        quant_a(2)
+        turn(3, 1)
+        scaled(4, 1)
+        turn(4, 0)
+        quant_agg(1)
+        first_matmul(2)
+        scaled(7, 0)
+        turned(3, 0, "s")
+        quant_agg(0)
+        turned(3, 1, "s")
+        turned(4, 0, "s")
+        agg_out(2, "s")
+        quant_a(3)
+        turn(4, 1)
+        turned(4, 1, "s")
+        turn(5, 0)
+        bias_column()
+        second_matmul_t(1)
+        second_matmul(0)
+        first_matmul(3)
+        scaled(5, 1)
+        scaled(6, 0)
+        relu_t(1, range(4))
+        turn_back(1)
+        agg_out(3, "s")
+        quant_a(4)
+        turn(5, 1)
+        scaled(6, 1)
+        turn(6, 0)
+        quant_agg(3)
+        first_matmul(4)
+        scaled(9, 0)
+        turned(5, 0, "s")
+        add_v(0)
+        quant_agg(2)
+        turned(5, 1, "s")
+        back_out(1, "s")
+        turned(6, 0, "s")
+        agg_out(4, "s")
+        relu(0, "s")
+        quant_a(5)
+        turn(6, 1)
+        turned(6, 1, "s")
+        turn(7, 0)
+        second_matmul_t(3)
+        second_matmul(2)
+        first_matmul(5)
+        scaled(7, 1)
+        scaled(8, 0)
+        relu_t(3, range(4))
+        turn_back(3)
+        agg_out(5, "s")
+        quant_a(6)
+        turn(7, 1)
+        scaled(8, 1)
+        turn(8, 0)
+        quant_agg(5)
+        first_matmul(6)
+        scaled(11, 0)
+        turned(7, 0, "s")
+        add_v(2)
+        quant_agg(4)
+        turned(7, 1, "s")
+        back_out(3, "s")
+        turned(8, 0, "s")
+        agg_out(6, "s")
+        relu(2, "s")
+        quant_a(7)
+        turn(8, 1)
+        turned(8, 1, "s")
+        turn(9, 0)
+        second_matmul_t(5)
+        second_matmul(4)
+        first_matmul(7)
+        scaled(9, 1)
+        scaled(10, 0)
+        relu_t(5, range(4))
+        turn_back(5)
+        agg_out(7, "s")
+        quant_a(8)
+        turn(9, 1)
+        scaled(10, 1)
+        turn(10, 0)
+        quant_agg(7)
+        first_matmul(8)
+        scaled(13, 0)
+        turned(9, 0, "s")
+        add_v(4)
+        quant_agg(6)
+        turned(9, 1, "s")
+        back_out(5, "s")
+        turned(10, 0, "s")
+        agg_out(8, "s")
+        relu(4, "s")
+        quant_a(9)
+        turn(10, 1)
+        turned(10, 1, "s")
+        turn(11, 0)
+        second_matmul_t(7)
+        second_matmul(6)
+        first_matmul(9)
+        scaled(11, 1)
+        scaled(12, 0)
+        relu_t(7, range(4))
+        turn_back(7)
+        agg_out(9, "s")
+        quant_a(10)
+        turn(11, 1)
+        scaled(12, 1)
+        turn(12, 0)
+        quant_agg(9)
+        first_matmul(10)
+        turned(11, 0, "s")
+        add_v(6)
+        quant_agg(8)
+        turned(11, 1, "s")
+        back_out(7, "s")
+        turned(12, 0, "s")
+        agg_out(10, "s")
+        relu(6, "s")
+        quant_a(11)
+        turn(12, 1)
+        turned(12, 1, "s")
+        turn(13, 0)
+        second_matmul_t(9)
+        second_matmul(8)
+        first_matmul(11)
+        scaled(13, 1)
+        scaled(14, 0)
+        relu_t(9, range(4))
+        turn_back(9)
+        agg_out(11, "s")
+        quant_a(12)
+        turn(13, 1)
+        scaled(14, 1)
+        turn(14, 0)
+        quant_agg(11)
+        first_matmul(12)
+        turned(13, 0, "s")
+        scaled(15, 0)
+        add_v(8)
+        quant_agg(10)
+        turned(13, 1, "s")
+        back_out(9, "s")
+        turned(14, 0, "s")
+        agg_out(12, "s")
+        relu(8, "s")
+        quant_a(13)
+        turn(14, 1)
+        scaled(15, 1)
+        turn(15, 0)
+        turned(14, 1, "s")
+        second_matmul_t(11)
+        second_matmul(10)
+        first_matmul(13)
+        relu_t(11, range(4))
+        turned(15, 0, "s")
+        turn_back(11)
+        agg_out(13, "s")
+        turn(15, 1)
+        quant_a(14)
+        turned(15, 1, "s")
+        quant_agg(13)
+        first_matmul(14)
+        add_v(10)
+        quant_agg(12)
+        back_out(11, "s")
+        agg_out(14, "s")
+        relu(10, "s")
+        quant_a(15)
+        second_matmul_t(13)
+        second_matmul(12)
+        first_matmul(15)
+        relu_t(13, range(4))
+        turn_back(13)
+        agg_out(15, "s")
+        add_v(12)
+        quant_agg(14)
+        back_out(13, "s")
+        relu(12, "s")
+        second_matmul(14)
+        quant_agg(15)
+        second_matmul(15)
+        add_v(14)
+        relu(14, "s")
+        add_v(15)
+        relu(15, "s")

@@ -19,6 +19,8 @@ D = 512
 P = 128
 PASSES = NODES // 512
 TILES = NODES // P
+BANKS = 8
+TURNED = [0, 1, 2, 3, 5, 6, 8, 9]
 FLOPS = 2 * NODES * NODES * D + 2 * NODES * D * D
 
 
@@ -26,54 +28,40 @@ def tile_net_pa_w4_kernel(tc, A_bytes, A_scale, features, Wg_words, Wg_scales, b
     nc = tc.nc
     with ExitStack() as ctx:
         keep = ctx.enter_context(tc.tile_pool(name="keep", bufs=1))
-        flow = ctx.enter_context(tc.tile_pool(name="flow", bufs=3))
         psum = ctx.enter_context(tc.psum_pool(name="psum", bufs=1))
         ctx.enter_context(tc.manual_schedule())
 
-        codes_in = [keep.tile([P, NODES], U8, name="abytes%d" % r, align_bytes=64) for r in range(TILES)]
-        vecs = keep.tile([P, PASSES + 1, 4], F32, name="vecs")
+        a_bytes = [keep.tile([P, NODES], U8, name="abytes%d" % r, align_bytes=64) for r in range(TILES)]
+        scale_cols = keep.tile([P, PASSES, 4], F32, name="scalecols")
         bias_raw = keep.tile([P, 4], BF16, name="biasraw")
-        spread = keep.tile([P, PASSES + 1, D], F32, name="spread", align_bytes=64)
-        bias = spread[:, PASSES, :]
+        bias_cols = keep.tile([P, 4], F32, name="biascols")
+        scale_row = keep.tile([P, NODES], F32, name="scalerow", align_bytes=64)
+        bias_row = keep.tile([P, D], F32, name="biasrow", align_bytes=64)
+        bias_chunks = keep.tile([P, 4], F32, name="biaschunks")
         f_raw = [keep.tile([P, 4, D], BF16, name="fraw%d" % g, align_bytes=64) for g in range(PASSES)]
-        f_grp = [keep.tile([P, 4, P, 4], BF16, name="fgrp%d" % g, align_bytes=64) for g in range(PASSES)]
+        f_grouped = [keep.tile([P, 4, P, 4], BF16, name="fgrouped%d" % g, align_bytes=64) for g in range(PASSES)]
         f_codes = [keep.tile([P, D], U32, name="fcodes%d" % g, align_bytes=64) for g in range(PASSES)]
         f_scales = [keep.tile([P, D], U8, name="fscales%d" % g, align_bytes=64) for g in range(PASSES)]
         w_words = keep.tile([P, 2 * D], U8, name="wwords", align_bytes=64)
         w_scales = keep.tile([P, D], U8, name="wscales", align_bytes=64)
-        bias_col = keep.tile([P, 4], F32, name="biascol")
         ident = keep.tile([P, P], F32, name="ident", align_bytes=64)
-        dummy = keep.tile([P, 1], F32, name="dummy")
-        dummy2 = keep.tile([P, 1], F32, name="dummy2")
+        ident_bf = keep.tile([P, P], BF16, name="identbf", align_bytes=64)
+
+        banks_taken = []
+
+        def next_bank(shape, dtype):
+            bank = psum.tile(shape, dtype, name="bank%d" % (len(banks_taken) % BANKS))
+            banks_taken.append(bank)
+            return bank
+
+        def ring(name, index, depth, shape, dtype):
+            return keep.tile(shape, dtype, name="%s%d" % (name, index % depth), align_bytes=64)
 
         def load_a(r):
-            nc.sync.dma_start(out=codes_in[r][:], in_=A_bytes[r * P : (r + 1) * P, :])
+            nc.sync.dma_start(out=a_bytes[r][:], in_=A_bytes[r * P : (r + 1) * P, :])
 
         def load_f(g):
             nc.sync.dma_start(out=f_raw[g][:], in_=features.rearrange("(g p j) c -> g p j c", p=P, j=4)[g])
-
-        def load_scale():
-            nc.sync.dma_start(out=vecs[:, 0:PASSES, :], in_=A_scale.rearrange("o (g p t) -> p (o g) t", p=P, t=4))
-
-        def spread_turn(g):
-            bank = psum.tile([P, 4, P], F32, name="spreadbank", tag="turn", bufs=4)
-            banks["s", g] = bank
-            for t in range(4):
-                nc.tensor.transpose(bank[:, t, :], vecs[:, g, t : t + 1].to_broadcast([P, P]), ident[:])
-
-        def spread_out(g, engine):
-            dst = spread[:, g, :].rearrange("p (n t) -> p n t", t=4)
-            src = banks["s", g][:].rearrange("p t n -> p n t")
-            if engine == "v":
-                nc.vector.tensor_copy(out=dst, in_=src)
-            else:
-                nc.scalar.copy(out=dst, in_=src)
-
-        def load_bias():
-            nc.sync.dma_start(out=bias_raw[:], in_=bg.rearrange("(p t) -> p t", t=4))
-
-        def bias_cast():
-            nc.vector.tensor_copy(out=vecs[:, PASSES, :], in_=bias_raw[:])
 
         def load_w():
             nc.sync.dma_start(out=w_words[:], in_=Wg_words.rearrange("g p w -> p (g w)"))
@@ -83,14 +71,211 @@ def tile_net_pa_w4_kernel(tc, A_bytes, A_scale, features, Wg_words, Wg_scales, b
                     in_=Wg_scales.rearrange("g q n -> (g q) n")[4 * q : 4 * q + 4, :].bitcast(I32),
                 )
 
-        nc.vector.memset(dummy[:], 0.0)
-        nc.scalar.copy(out=dummy2[:], in_=dummy[:])
-        nc.vector.memset(w_scales[:].bitcast(I32), 0)
-        make_identity(nc, ident[:])
+        def copy_on(engine, dst, src):
+            if engine == "vector":
+                nc.vector.tensor_copy(out=dst, in_=src)
+            else:
+                nc.scalar.copy(out=dst, in_=src)
 
-        banks = {}
-        load_scale()
-        load_bias()
+        def spread(cols, row, engine):
+            bank = next_bank([P, 4, P], F32)
+            for t in range(4):
+                nc.tensor.transpose(bank[:, t, :], cols[:, t : t + 1].to_broadcast([P, P]), ident[:])
+            copy_on(engine, row.rearrange("p (n t) -> p n t", t=4), bank[:].rearrange("p t n -> p n t"))
+
+        def spread_scale(g, engine):
+            spread(scale_cols[:, g, :], scale_row[:, g * 512 : (g + 1) * 512], engine)
+
+        def bias_to_partitions():
+            bank = next_bank([P, 4, P], F32)
+            for c in range(4):
+                nc.tensor.transpose(bank[:, c, :], bias_row[:, c * P : (c + 1) * P], ident[:])
+            nc.scalar.copy(out=bias_chunks[:].rearrange("p (c o) -> p c o", o=1), in_=bank[:, :, 0:1])
+
+        def group_features(g):
+            src = f_raw[g][:].rearrange("p j (m t) -> p t m j", t=4)
+            for half in range(2):
+                bank = next_bank([P, 2, 4 * P], BF16)
+                for tl in range(2):
+                    nc.tensor.matmul(bank[:, tl, :], lhsT=ident_bf[:], rhs=src[:, 2 * half + tl], start=True, stop=True)
+                nc.scalar.copy(
+                    out=f_grouped[g][:, 2 * half : 2 * half + 2].rearrange("p t m j -> p (t m j)"),
+                    in_=bank[:].rearrange("p t n -> p (t n)"),
+                )
+
+        def group_features_on_vector(g):
+            nc.vector.tensor_copy(out=f_grouped[g][:], in_=f_raw[g][:].rearrange("p j (m t) -> p t m j", t=4))
+
+        def quantize_features(g):
+            nc.vector.quantize_mx(
+                out=f_codes[g][:].bitcast(FP8X4),
+                scales=f_scales[g][:],
+                in_=f_grouped[g][:].rearrange("p t m j -> p (t m j)"),
+            )
+
+        wide, grouped, a_codes, a_scales = {}, {}, {}, {}
+        agg_bf, agg_codes, agg_scales = {}, {}, {}
+        product, relu_turned, summed, unscaled = {}, {}, {}, {}
+
+        def scale_rows(r, parts=1):
+            wide[r] = ring("wide", r, 4, [P, NODES], BF16)
+            width = NODES // parts
+            for part in range(parts):
+                cols = slice(part * width, (part + 1) * width)
+                nc.vector.tensor_tensor(
+                    out=wide[r][:, cols], in0=a_bytes[r][:, cols].bitcast(FP8), in1=scale_row[:, cols], op=ALU.mult
+                )
+
+        def turn_rows(r):
+            words = wide[r][:].bitcast(F32)
+            grouped[r] = ring("grouped", r, 4, [P, PASSES, P, 4], BF16)
+            for half in range(2):
+                bank = next_bank([P, 2, 2, P], F32)
+                for gl in range(2):
+                    w0 = 256 * (2 * half + gl)
+                    for u in range(2):
+                        nc.tensor.transpose(bank[:, u, gl, :], words[:, w0 + u : w0 + 256 : 2], ident[:])
+                nc.scalar.copy(
+                    out=grouped[r][:, 2 * half : 2 * half + 2].bitcast(F32),
+                    in_=bank[:].rearrange("p u g i -> p g i u"),
+                )
+
+        def widen_rows(r, half):
+            if half == 0:
+                wide[r] = keep.tile([P, NODES], BF16, name="widelate%d" % r, align_bytes=64)
+            cols = slice(half * 1024, (half + 1) * 1024)
+            nc.scalar.copy(out=wide[r][:, cols], in_=a_bytes[r][:, cols].bitcast(FP8))
+
+        def turn_unscaled(r):
+            words = wide[r][:].bitcast(F32)
+            for half in range(2):
+                bank = next_bank([P, 2, 2, P], F32)
+                unscaled[r, half] = bank
+                for gl in range(2):
+                    w0 = 256 * (2 * half + gl)
+                    for u in range(2):
+                        nc.tensor.transpose(bank[:, u, gl, :], words[:, w0 + u : w0 + 256 : 2], ident[:])
+
+        def scale_turned(r, half):
+            if half == 0:
+                grouped[r] = ring("grouped", r, 4, [P, PASSES, P, 4], BF16)
+            passes = slice(2 * half, 2 * half + 2)
+            nc.vector.tensor_tensor(
+                out=grouped[r][:, passes].rearrange("p g i (u e) -> p g i u e", u=2),
+                in0=unscaled[r, half][:].bitcast(BF16).rearrange("p u g (i e) -> p g i u e", e=2),
+                in1=scale_cols[:, passes, :].rearrange("p g (u e) -> p g u e", u=2).unsqueeze(2).to_broadcast([P, 2, P, 2, 2]),
+                op=ALU.mult,
+            )
+
+        def quantize_rows(r, first=0, count=PASSES):
+            if first == 0:
+                a_codes[r] = ring("acodes", r, 4, [P, PASSES, P], U32)
+                a_scales[r] = ring("ascales", r, 4, [P, PASSES, P], U8)
+            passes = slice(first, first + count)
+            nc.vector.quantize_mx(
+                out=a_codes[r][:, passes].rearrange("p g i -> p (g i)").bitcast(FP8X4),
+                scales=a_scales[r][:, passes].rearrange("p g i -> p (g i)"),
+                in_=grouped[r][:, passes].rearrange("p g i t -> p (g i t)"),
+            )
+
+        def aggregate(r):
+            bank = next_bank([P, 4, P], F32)
+            for g in range(PASSES):
+                for t in range(4):
+                    nc.tensor.matmul_mx(
+                        out=bank[:, t, :],
+                        lhsT=f_codes[g][:, t * P : (t + 1) * P].bitcast(FP8X4),
+                        lhsT_scale=f_scales[g][:, t * P : (t + 1) * P],
+                        rhs=a_codes[r][:, g, :].bitcast(FP8X4),
+                        rhs_scale=a_scales[r][:, g, :],
+                        start=(g == 0 and t == 0),
+                        stop=(g == PASSES - 1 and t == 3),
+                    )
+            first = first_of(r)
+            if first == r:
+                width = 2 * P if turned(r) else P
+                agg_bf[r] = ring("aggbf", r, 6, [P, width, 4], BF16)
+                agg_codes[r] = ring("aggcodes", r, 6, [P, width], U32)
+                agg_scales[r] = ring("aggscales", r, 6, [P, width], U8)
+            nc.scalar.copy(
+                out=agg_bf[first][:, (r - first) * P : (r - first + 1) * P], in_=bank[:].rearrange("p t i -> p i t")
+            )
+
+        def quantize_agg(r):
+            nc.vector.quantize_mx(
+                out=agg_codes[r][:].bitcast(FP8X4),
+                scales=agg_scales[r][:],
+                in_=agg_bf[r][:].rearrange("p i t -> p (i t)"),
+            )
+
+        def project(r):
+            product[r] = next_bank([P, D], F32)
+            nc.tensor.matmul_mx(
+                out=product[r][:],
+                lhsT=agg_codes[r][:].bitcast(FP8X4),
+                lhsT_scale=agg_scales[r][:],
+                rhs=w_words[:].bitcast(FP4X4),
+                rhs_scale=w_scales[:],
+                start=True,
+                stop=True,
+            )
+
+        def add_bias(r):
+            summed[r] = ring("summed", r, 6, [P, D], F32)
+            nc.vector.tensor_tensor(out=summed[r][:], in0=product[r][:], in1=bias_row[:], op=ALU.add)
+
+        def relu_store(r, engine="scalar"):
+            rows = ring("rows", r, 8, [P, D], F32)
+            if engine == "vector":
+                nc.vector.tensor_scalar(out=rows[:], in0=summed[r][:], scalar1=0.0, scalar2=None, op0=ALU.max)
+            else:
+                nc.scalar.activation(out=rows[:], in_=summed[r][:], func=ACT.Relu)
+            nc.sync.dma_start(out=out[r * P : (r + 1) * P, :], in_=rows[:])
+
+        def project_turned(first, half):
+            if half == 0:
+                relu_turned[first] = ring("reluturned", TURNED.index(first) // 2, 2, [P, 4, 2 * P], F32)
+            bank = next_bank([P, 2, 2 * P], F32)
+            for cl in range(2):
+                c = 2 * half + cl
+                nc.tensor.matmul_mx(
+                    out=bank[:, cl, :],
+                    lhsT=w_words[:, 2 * c * P : 2 * (c + 1) * P].bitcast(FP4X4),
+                    lhsT_scale=w_scales[:, c * P : (c + 1) * P],
+                    rhs=agg_codes[first][:].bitcast(FP8X4),
+                    rhs_scale=agg_scales[first][:],
+                    start=True,
+                    stop=True,
+                )
+            for cl in range(2):
+                c = 2 * half + cl
+                nc.scalar.activation(
+                    out=relu_turned[first][:, c, :], in_=bank[:, cl, :], func=ACT.Relu, bias=bias_chunks[:, c : c + 1]
+                )
+
+        def turn_back_store(r):
+            first = first_of(r)
+            bank = next_bank([P, 4, P], F32)
+            for c in range(4):
+                nc.tensor.transpose(bank[:, c, :], relu_turned[first][:, c, (r - first) * P : (r - first + 1) * P], ident[:])
+            rows = ring("rows", r, 8, [P, D], F32)
+            nc.scalar.copy(out=rows[:], in_=bank[:].rearrange("p c n -> p (c n)"))
+            nc.sync.dma_start(out=out[r * P : (r + 1) * P, :], in_=rows[:])
+
+        def turned(r):
+            return r in TURNED
+
+        def first_of(r):
+            return TURNED[TURNED.index(r) // 2 * 2] if turned(r) else r
+
+        def plain(r):
+            return 0 <= r < TILES and not turned(r)
+
+        make_identity(nc, ident[:])
+        nc.vector.memset(w_scales[:].bitcast(I32), 0)
+        nc.scalar.copy(out=ident_bf[:], in_=ident[:])
+
+        nc.sync.dma_start(out=scale_cols[:], in_=A_scale.rearrange("o (g p t) -> p (o g) t", p=P, t=4))
         load_f(0)
         load_a(0)
         load_f(1)
@@ -98,415 +283,76 @@ def tile_net_pa_w4_kernel(tc, A_bytes, A_scale, features, Wg_words, Wg_scales, b
         load_f(2)
         load_f(3)
         load_a(2)
-        load_w()
         load_a(3)
+        nc.sync.dma_start(out=bias_raw[:], in_=bg.rearrange("(p t) -> p t", t=4))
         load_a(4)
-        load_a(5)
-        load_a(6)
-        load_a(7)
-        load_a(8)
-        load_a(9)
-        load_a(10)
-        load_a(11)
-        load_a(12)
-        load_a(13)
-        load_a(14)
-        load_a(15)
+        load_w()
+        for r in range(5, TILES):
+            load_a(r)
 
-        wide = {}
-        grouped = {}
-        a_codes = {}
-        a_scales = {}
-        acc = {}
-        g_bf = {}
-        g_codes = {}
-        g_scales = {}
-        mid = {}
-        t1 = {}
-        t2 = {}
+        for g in range(PASSES):
+            spread_scale(g, "scalar")
+        group_features_on_vector(0)
+        scale_rows(0, parts=2)
+        quantize_features(0)
+        group_features(1)
+        group_features(2)
+        turn_rows(0)
+        group_features(3)
+        scale_rows(1)
+        quantize_features(1)
+        quantize_features(2)
+        quantize_rows(0)
+        quantize_features(3)
+        turn_rows(1)
+        aggregate(0)
 
-        def scaled(r, half):
-            if r not in wide:
-                wide[r] = flow.tile([P, NODES], BF16, name="wide", bufs=5, align_bytes=64)
-            cols = slice(half * 1024, (half + 1) * 1024)
-            nc.vector.tensor_tensor(
-                out=wide[r][:, cols], in0=codes_in[r][:, cols].bitcast(FP8), in1=spread[:, 2 * half : 2 * half + 2, :].rearrange("p g k -> p (g k)"), op=ALU.mult
-            )
+        for r in range(1, TILES - 1):
+            scale_rows(r + 1)
+            if r == 1:
+                nc.vector.tensor_copy(out=bias_cols[:], in_=bias_raw[:])
+            if plain(r - 4) and r < 13:
+                add_bias(r - 4)
+            quantize_rows(r)
+            if r <= 13 and (plain(r - 3) or (turned(r - 3) and first_of(r - 3) == r - 3)):
+                quantize_agg(r - 3)
+            if r >= 13:
+                quantize_agg(r - 2)
+            if r > 13:
+                add_bias(r - 4)
 
-        def turn(r, b):
-            words = wide[r][:].bitcast(F32)
-            bank = psum.tile([P, 2, 2, P], F32, name="turn", tag="turn", bufs=4)
-            banks[r, b] = bank
-            for gl in range(2):
-                for u in range(2):
-                    w0 = 256 * (2 * b + gl)
-                    nc.tensor.transpose(bank[:, u, gl, :], words[:, w0 + u : w0 + 256 : 2], ident[:])
+            turn_rows(r + 1)
+            if r == 1:
+                spread(bias_cols[:], bias_row[:], "scalar")
+            if r == 2:
+                bias_to_partitions()
+            if turned(r - 5):
+                turn_back_store(r - 5)
+            if turned(r - 3):
+                project_turned(first_of(r - 3), r - 3 - first_of(r - 3))
+            if plain(r - 3) and r <= 13:
+                project(r - 3)
+            if r >= 13:
+                project(r - 2)
+            aggregate(r)
+            if plain(r - 4) and r != 13:
+                relu_store(r - 4)
 
-        def turned(r, b, engine):
-            if r not in grouped:
-                grouped[r] = flow.tile([P, PASSES, P, 4], BF16, name="grouped", bufs=4, align_bytes=64)
-            dst = grouped[r][:, 2 * b : 2 * b + 2].bitcast(F32)
-            src = banks[r, b][:].rearrange("p u g i -> p g i u")
-            if engine == "v":
-                nc.vector.tensor_copy(out=dst, in_=src)
-            else:
-                nc.scalar.copy(out=dst, in_=src)
-
-        def quant_a(r):
-            a_codes[r] = flow.tile([P, PASSES, P], U32, name="acodes", bufs=4, align_bytes=64)
-            a_scales[r] = flow.tile([P, PASSES, P], U8, name="ascales", bufs=4, align_bytes=64)
-            nc.vector.quantize_mx(
-                out=a_codes[r][:].rearrange("p g i -> p (g i)").bitcast(FP8X4),
-                scales=a_scales[r][:].rearrange("p g i -> p (g i)"),
-                in_=grouped[r][:].rearrange("p g i t -> p (g i t)"),
-            )
-
-        def first_matmul(r):
-            acc[r] = psum.tile([P, 4, P], F32, name="acc", bufs=1)
-            for t in range(4):
-                for g in range(PASSES):
-                    nc.tensor.matmul_mx(
-                        out=acc[r][:, t, :],
-                        lhsT=f_codes[g][:, t * P : (t + 1) * P].bitcast(FP8X4),
-                        lhsT_scale=f_scales[g][:, t * P : (t + 1) * P],
-                        rhs=a_codes[r][:, g, :].bitcast(FP8X4),
-                        rhs_scale=a_scales[r][:, g, :],
-                        start=(g == 0),
-                        stop=(g == PASSES - 1),
-                    )
-
-        def agg_out(r, engine="s"):
-            g_bf[r] = flow.tile([P, P, 4], BF16, name="gbf", bufs=3, align_bytes=64)
-            src = acc[r][:].rearrange("p t i -> p i t")
-            if engine == "v":
-                nc.vector.tensor_copy(out=g_bf[r][:], in_=src)
-            else:
-                nc.scalar.copy(out=g_bf[r][:], in_=src)
-
-        def quant_agg(r):
-            g_codes[r] = flow.tile([P, P], U32, name="gcodes", bufs=3, align_bytes=64)
-            g_scales[r] = flow.tile([P, P], U8, name="gscales", bufs=3, align_bytes=64)
-            nc.vector.quantize_mx(
-                out=g_codes[r][:].bitcast(FP8X4),
-                scales=g_scales[r][:],
-                in_=g_bf[r][:].rearrange("p i t -> p (i t)"),
-            )
-
-        def second_matmul(r):
-            mid[r] = psum.tile([P, D], F32, name="mid", bufs=2)
-            nc.tensor.matmul_mx(
-                out=mid[r][:],
-                lhsT=g_codes[r][:].bitcast(FP8X4),
-                lhsT_scale=g_scales[r][:],
-                rhs=w_words[:].bitcast(FP4X4),
-                rhs_scale=w_scales[:],
-                start=True,
-                stop=True,
-            )
-
-        def second_matmul_t(r):
-            mid[r] = psum.tile([P, D], F32, name="mid", bufs=2)
-            for c in range(4):
-                nc.tensor.matmul_mx(
-                    out=mid[r][:, c * P : (c + 1) * P],
-                    lhsT=w_words[:, 2 * c * P : 2 * (c + 1) * P].bitcast(FP4X4),
-                    lhsT_scale=w_scales[:, c * P : (c + 1) * P],
-                    rhs=g_codes[r][:].bitcast(FP8X4),
-                    rhs_scale=g_scales[r][:],
-                    start=True,
-                    stop=True,
-                )
-
-        def relu_t(r, cs, engine="s"):
-            if r not in t1:
-                t1[r] = flow.tile([P, 4, P], F32, name="t1", bufs=3, align_bytes=64)
-            for c in cs:
-                nc.scalar.activation(
-                    out=t1[r][:, c, :], in_=mid[r][:, c * P : (c + 1) * P], func=ACT.Relu, bias=bias_col[:, c : c + 1]
-                )
-
-        def turn_back(r):
-            t2[r] = psum.tile([P, 4, P], F32, name="t2", bufs=1)
-            for c in range(4):
-                nc.tensor.transpose(t2[r][:, c, :], t1[r][:, c, :], ident[:])
-
-        def back_out(r, engine="s"):
-            fin = flow.tile([P, D], F32, name="fin", bufs=4, align_bytes=64)
-            src = t2[r][:].rearrange("p c n -> p (c n)")
-            if engine == "v":
-                nc.vector.tensor_copy(out=fin[:], in_=src)
-            else:
-                nc.scalar.copy(out=fin[:], in_=src)
-            nc.sync.dma_start(out=out[r * P : (r + 1) * P, :], in_=fin[:])
-
-        def bias_column():
-            bank = psum.tile([P, 4, P], F32, name="biasbank", tag="t2", bufs=1)
-            for c in range(4):
-                nc.tensor.transpose(bank[:, c, :], bias[:, c * P : (c + 1) * P], ident[:])
-            nc.vector.tensor_copy(out=bias_col[:].rearrange("p (c o) -> p c o", o=1), in_=bank[:, :, 0:1])
-
-        def f_interleave(g, engine):
-            src = f_raw[g][:].rearrange("p j (m t) -> p t m j", t=4)
-            if engine == "v":
-                nc.vector.tensor_copy(out=f_grp[g][:], in_=src)
-            elif engine == "s":
-                nc.scalar.copy(out=f_grp[g][:], in_=src)
-            else:
-                nc.gpsimd.tensor_scalar(out=f_grp[g][:], in0=src, scalar1=1.0, scalar2=0.0, op0=ALU.mult, op1=ALU.add)
-
-        def f_quant(g):
-            nc.vector.quantize_mx(
-                out=f_codes[g][:].bitcast(FP8X4),
-                scales=f_scales[g][:],
-                in_=f_grp[g][:].rearrange("p t m j -> p (t m j)"),
-            )
-
-        summed = {}
-
-        def add_v(r):
-            summed[r] = flow.tile([P, D], F32, name="summed", bufs=4, align_bytes=64)
-            nc.vector.tensor_tensor(out=summed[r][:], in0=mid[r][:], in1=bias, op=ALU.add)
-
-        def relu(r, engine):
-            fin = flow.tile([P, D], F32, name="fin", bufs=4, align_bytes=64)
-            if engine == "v":
-                nc.vector.tensor_scalar(out=fin[:], in0=summed[r][:], scalar1=0.0, scalar2=None, op0=ALU.max)
-            else:
-                nc.scalar.activation(out=fin[:], in_=summed[r][:], func=ACT.Relu)
-            nc.sync.dma_start(out=out[r * P : (r + 1) * P, :], in_=fin[:])
-
-        bias_cast()
-        spread_turn(1)
-        spread_turn(0)
-        spread_out(1, "s")
-        spread_turn(3)
-        spread_out(0, "s")
-        f_interleave(0, "v")
-        spread_turn(2)
-        spread_out(3, "s")
-        f_interleave(1, "s")
-        f_quant(0)
-        spread_out(2, "s")
-        spread_turn(4)
-        spread_out(4, "s")
-        f_interleave(3, "s")
-        scaled(1, 0)
-        f_interleave(2, "s")
-        scaled(0, 0)
-        scaled(0, 1)
-        turn(0, 0)
-        scaled(3, 0)
-        turned(0, 0, "s")
-        turn(0, 1)
-        turned(0, 1, "s")
-        turn(1, 0)
-        scaled(1, 1)
-        scaled(2, 0)
-        f_quant(3)
-        f_quant(1)
-        f_quant(2)
-        quant_a(0)
-        turn(1, 1)
-        scaled(2, 1)
-        turn(2, 0)
-        first_matmul(0)
-        scaled(5, 0)
-        turned(1, 0, "s")
-        turned(1, 1, "s")
-        turned(2, 0, "s")
-        agg_out(0, "s")
-        quant_a(1)
-        turn(2, 1)
-        turned(2, 1, "s")
-        turn(3, 0)
-        first_matmul(1)
-        scaled(3, 1)
-        scaled(4, 0)
-        agg_out(1, "s")
-        quant_a(2)
-        turn(3, 1)
-        scaled(4, 1)
-        turn(4, 0)
-        quant_agg(1)
-        first_matmul(2)
-        scaled(7, 0)
-        turned(3, 0, "s")
-        quant_agg(0)
-        turned(3, 1, "s")
-        turned(4, 0, "s")
-        agg_out(2, "s")
-        quant_a(3)
-        turn(4, 1)
-        turned(4, 1, "s")
-        turn(5, 0)
-        bias_column()
-        second_matmul_t(1)
-        second_matmul(0)
-        first_matmul(3)
-        scaled(5, 1)
-        scaled(6, 0)
-        relu_t(1, range(4))
-        turn_back(1)
-        agg_out(3, "s")
-        quant_a(4)
-        turn(5, 1)
-        scaled(6, 1)
-        turn(6, 0)
-        quant_agg(3)
-        first_matmul(4)
-        scaled(9, 0)
-        turned(5, 0, "s")
-        add_v(0)
-        quant_agg(2)
-        turned(5, 1, "s")
-        back_out(1, "s")
-        turned(6, 0, "s")
-        agg_out(4, "s")
-        relu(0, "s")
-        quant_a(5)
-        turn(6, 1)
-        turned(6, 1, "s")
-        turn(7, 0)
-        second_matmul_t(3)
-        second_matmul(2)
-        first_matmul(5)
-        scaled(7, 1)
-        scaled(8, 0)
-        relu_t(3, range(4))
-        turn_back(3)
-        agg_out(5, "s")
-        quant_a(6)
-        turn(7, 1)
-        scaled(8, 1)
-        turn(8, 0)
-        quant_agg(5)
-        first_matmul(6)
-        scaled(11, 0)
-        turned(7, 0, "s")
-        add_v(2)
-        quant_agg(4)
-        turned(7, 1, "s")
-        back_out(3, "s")
-        turned(8, 0, "s")
-        agg_out(6, "s")
-        relu(2, "s")
-        quant_a(7)
-        turn(8, 1)
-        turned(8, 1, "s")
-        turn(9, 0)
-        second_matmul_t(5)
-        second_matmul(4)
-        first_matmul(7)
-        scaled(9, 1)
-        scaled(10, 0)
-        relu_t(5, range(4))
-        turn_back(5)
-        agg_out(7, "s")
-        quant_a(8)
-        turn(9, 1)
-        scaled(10, 1)
-        turn(10, 0)
-        quant_agg(7)
-        first_matmul(8)
-        scaled(13, 0)
-        turned(9, 0, "s")
-        add_v(4)
-        quant_agg(6)
-        turned(9, 1, "s")
-        back_out(5, "s")
-        turned(10, 0, "s")
-        agg_out(8, "s")
-        relu(4, "s")
-        quant_a(9)
-        turn(10, 1)
-        turned(10, 1, "s")
-        turn(11, 0)
-        second_matmul_t(7)
-        second_matmul(6)
-        first_matmul(9)
-        scaled(11, 1)
-        scaled(12, 0)
-        relu_t(7, range(4))
-        turn_back(7)
-        agg_out(9, "s")
-        quant_a(10)
-        turn(11, 1)
-        scaled(12, 1)
-        turn(12, 0)
-        quant_agg(9)
-        first_matmul(10)
-        turned(11, 0, "s")
-        add_v(6)
-        quant_agg(8)
-        turned(11, 1, "s")
-        back_out(7, "s")
-        turned(12, 0, "s")
-        agg_out(10, "s")
-        relu(6, "s")
-        quant_a(11)
-        turn(12, 1)
-        turned(12, 1, "s")
-        turn(13, 0)
-        second_matmul_t(9)
-        second_matmul(8)
-        first_matmul(11)
-        scaled(13, 1)
-        scaled(14, 0)
-        relu_t(9, range(4))
-        turn_back(9)
-        agg_out(11, "s")
-        quant_a(12)
-        turn(13, 1)
-        scaled(14, 1)
-        turn(14, 0)
-        quant_agg(11)
-        first_matmul(12)
-        turned(13, 0, "s")
-        scaled(15, 0)
-        add_v(8)
-        quant_agg(10)
-        turned(13, 1, "s")
-        back_out(9, "s")
-        turned(14, 0, "s")
-        agg_out(12, "s")
-        relu(8, "s")
-        quant_a(13)
-        turn(14, 1)
-        scaled(15, 1)
-        turn(15, 0)
-        turned(14, 1, "s")
-        second_matmul_t(11)
-        second_matmul(10)
-        first_matmul(13)
-        relu_t(11, range(4))
-        turned(15, 0, "s")
-        turn_back(11)
-        agg_out(13, "s")
-        turn(15, 1)
-        quant_a(14)
-        turned(15, 1, "s")
-        quant_agg(13)
-        first_matmul(14)
-        add_v(10)
-        quant_agg(12)
-        back_out(11, "s")
-        agg_out(14, "s")
-        relu(10, "s")
-        quant_a(15)
-        second_matmul_t(13)
-        second_matmul(12)
-        first_matmul(15)
-        relu_t(13, range(4))
-        turn_back(13)
-        agg_out(15, "s")
-        add_v(12)
-        quant_agg(14)
-        back_out(13, "s")
-        relu(12, "s")
-        second_matmul(14)
-        quant_agg(15)
-        second_matmul(15)
-        add_v(14)
-        relu(14, "s")
-        add_v(15)
-        relu(15, "s")
+        add_bias(11)
+        quantize_rows(15)
+        aggregate(15)
+        add_bias(12)
+        quantize_agg(13)
+        quantize_agg(14)
+        project(13)
+        project(14)
+        relu_store(11)
+        relu_store(12)
+        add_bias(13)
+        quantize_agg(15)
+        project(15)
+        relu_store(13)
+        add_bias(14)
+        add_bias(15)
+        relu_store(14)
+        relu_store(15, "vector")

@@ -20,7 +20,7 @@ P = 128
 PASSES = NODES // 512
 TILES = NODES // P
 BANKS = 8
-TURNED = [0, 1, 2, 3, 5, 6, 8, 9]
+TURNED = [0, 1, 2, 3, 4, 5, 6, 7, 8, 9]
 FLOPS = 2 * NODES * NODES * D + 2 * NODES * D * D
 
 
@@ -103,8 +103,8 @@ def tile_net_pa_w4_kernel(tc, A_bytes, A_scale, features, Wg_words, Wg_scales, b
                     in_=bank[:].rearrange("p t n -> p (t n)"),
                 )
 
-        def group_features_on_vector(g):
-            nc.vector.tensor_copy(out=f_grouped[g][:], in_=f_raw[g][:].rearrange("p j (m t) -> p t m j", t=4))
+        def group_features_by_copy(g):
+            nc.scalar.copy(out=f_grouped[g][:], in_=f_raw[g][:].rearrange("p j (m t) -> p t m j", t=4))
 
         def quantize_features(g):
             nc.vector.quantize_mx(
@@ -139,33 +139,6 @@ def tile_net_pa_w4_kernel(tc, A_bytes, A_scale, features, Wg_words, Wg_scales, b
                     out=grouped[r][:, 2 * half : 2 * half + 2].bitcast(F32),
                     in_=bank[:].rearrange("p u g i -> p g i u"),
                 )
-
-        def widen_rows(r, half):
-            if half == 0:
-                wide[r] = keep.tile([P, NODES], BF16, name="widelate%d" % r, align_bytes=64)
-            cols = slice(half * 1024, (half + 1) * 1024)
-            nc.scalar.copy(out=wide[r][:, cols], in_=a_bytes[r][:, cols].bitcast(FP8))
-
-        def turn_unscaled(r):
-            words = wide[r][:].bitcast(F32)
-            for half in range(2):
-                bank = next_bank([P, 2, 2, P], F32)
-                unscaled[r, half] = bank
-                for gl in range(2):
-                    w0 = 256 * (2 * half + gl)
-                    for u in range(2):
-                        nc.tensor.transpose(bank[:, u, gl, :], words[:, w0 + u : w0 + 256 : 2], ident[:])
-
-        def scale_turned(r, half):
-            if half == 0:
-                grouped[r] = ring("grouped", r, 4, [P, PASSES, P, 4], BF16)
-            passes = slice(2 * half, 2 * half + 2)
-            nc.vector.tensor_tensor(
-                out=grouped[r][:, passes].rearrange("p g i (u e) -> p g i u e", u=2),
-                in0=unscaled[r, half][:].bitcast(BF16).rearrange("p u g (i e) -> p g i u e", e=2),
-                in1=scale_cols[:, passes, :].rearrange("p g (u e) -> p g u e", u=2).unsqueeze(2).to_broadcast([P, 2, P, 2, 2]),
-                op=ALU.mult,
-            )
 
         def quantize_rows(r, first=0, count=PASSES):
             if first == 0:
@@ -276,10 +249,10 @@ def tile_net_pa_w4_kernel(tc, A_bytes, A_scale, features, Wg_words, Wg_scales, b
         nc.scalar.copy(out=ident_bf[:], in_=ident[:])
 
         nc.sync.dma_start(out=scale_cols[:], in_=A_scale.rearrange("o (g p t) -> p (o g) t", p=P, t=4))
-        load_f(0)
         load_a(0)
-        load_f(1)
+        load_f(0)
         load_a(1)
+        load_f(1)
         load_f(2)
         load_f(3)
         load_a(2)
@@ -290,29 +263,30 @@ def tile_net_pa_w4_kernel(tc, A_bytes, A_scale, features, Wg_words, Wg_scales, b
         for r in range(5, TILES):
             load_a(r)
 
-        for g in range(PASSES):
+        spread_scale(0, "vector")
+        for g in range(1, PASSES):
             spread_scale(g, "scalar")
-        group_features_on_vector(0)
-        scale_rows(0, parts=2)
-        quantize_features(0)
-        group_features(1)
-        group_features(2)
+        scale_rows(0, parts=4)
+        group_features_by_copy(0)
         turn_rows(0)
-        group_features(3)
         scale_rows(1)
-        quantize_features(1)
-        quantize_features(2)
+        group_features(1)
+        group_features_by_copy(2)
+        group_features(3)
+        quantize_features(0)
         quantize_rows(0)
-        quantize_features(3)
+        quantize_features(1)
         turn_rows(1)
-        aggregate(0)
 
         for r in range(1, TILES - 1):
             scale_rows(r + 1)
             if r == 1:
                 nc.vector.tensor_copy(out=bias_cols[:], in_=bias_raw[:])
-            if plain(r - 4) and r < 13:
+            if plain(r - 4) and r <= 13:
                 add_bias(r - 4)
+            if r == 1:
+                quantize_features(2)
+                quantize_features(3)
             quantize_rows(r)
             if r <= 13 and (plain(r - 3) or (turned(r - 3) and first_of(r - 3) == r - 3)):
                 quantize_agg(r - 3)
@@ -334,8 +308,10 @@ def tile_net_pa_w4_kernel(tc, A_bytes, A_scale, features, Wg_words, Wg_scales, b
                 project(r - 3)
             if r >= 13:
                 project(r - 2)
+            if r == 1:
+                aggregate(0)
             aggregate(r)
-            if plain(r - 4) and r != 13:
+            if plain(r - 4):
                 relu_store(r - 4)
 
         add_bias(11)

@@ -18,9 +18,8 @@ NODES = 2048
 D = 512
 P = 128
 PASSES = NODES // 512
-TILES = NODES // P
-BANKS = 8
-TURNED = [0, 1, 2, 3, 4, 5, 6, 7, 8, 9]
+PAIRS = NODES // (2 * P)
+QUARTER = 1024
 FLOPS = 2 * NODES * NODES * D + 2 * NODES * D * D
 
 
@@ -31,11 +30,10 @@ def tile_net_pa_w4_kernel(tc, A_bytes, A_scale, features, Wg_words, Wg_scales, b
         psum = ctx.enter_context(tc.psum_pool(name="psum", bufs=1))
         ctx.enter_context(tc.manual_schedule())
 
-        a_bytes = [keep.tile([P, NODES], U8, name="abytes%d" % r, align_bytes=64) for r in range(TILES)]
+        a_bytes = [keep.tile([P, 2 * NODES], U8, name="abytes%d" % n, align_bytes=64) for n in range(PAIRS)]
         scale_cols = keep.tile([P, PASSES, 4], F32, name="scalecols")
         bias_raw = keep.tile([P, 4], BF16, name="biasraw")
         bias_cols = keep.tile([P, 4], F32, name="biascols")
-        scale_row = keep.tile([P, NODES], F32, name="scalerow", align_bytes=64)
         bias_row = keep.tile([P, D], F32, name="biasrow", align_bytes=64)
         bias_chunks = keep.tile([P, 4], F32, name="biaschunks")
         f_raw = [keep.tile([P, 4, D], BF16, name="fraw%d" % g, align_bytes=64) for g in range(PASSES)]
@@ -47,18 +45,26 @@ def tile_net_pa_w4_kernel(tc, A_bytes, A_scale, features, Wg_words, Wg_scales, b
         ident = keep.tile([P, P], F32, name="ident", align_bytes=64)
         ident_bf = keep.tile([P, P], BF16, name="identbf", align_bytes=64)
 
-        banks_taken = []
+        bank_names = ["other%d" % b for b in range(4)]
 
         def next_bank(shape, dtype):
-            bank = psum.tile(shape, dtype, name="bank%d" % (len(banks_taken) % BANKS))
-            banks_taken.append(bank)
-            return bank
+            name = bank_names[0]
+            bank_names.remove(name)
+            bank_names.append(name)
+            return psum.tile(shape, dtype, name=name)
 
         def ring(name, index, depth, shape, dtype):
             return keep.tile(shape, dtype, name="%s%d" % (name, index % depth), align_bytes=64)
 
-        def load_a(r):
-            nc.sync.dma_start(out=a_bytes[r][:], in_=A_bytes[r * P : (r + 1) * P, :])
+        def load_a(n, h):
+            r0 = (2 * n + h) * P
+            nc.sync.dma_start(out=a_bytes[n][:, h * NODES : (h + 1) * NODES], in_=A_bytes[r0 : r0 + P, :])
+
+        def load_pair(n):
+            nc.sync.dma_start(
+                out=a_bytes[n][:].rearrange("p (h k) -> p h k", h=2),
+                in_=A_bytes[2 * n * P : 2 * (n + 1) * P, :].rearrange("(h p) k -> p h k", p=P),
+            )
 
         def load_f(g):
             nc.sync.dma_start(out=f_raw[g][:], in_=features.rearrange("(g p j) c -> g p j c", p=P, j=4)[g])
@@ -71,20 +77,12 @@ def tile_net_pa_w4_kernel(tc, A_bytes, A_scale, features, Wg_words, Wg_scales, b
                     in_=Wg_scales.rearrange("g q n -> (g q) n")[4 * q : 4 * q + 4, :].bitcast(I32),
                 )
 
-        def copy_on(engine, dst, src):
-            if engine == "vector":
-                nc.vector.tensor_copy(out=dst, in_=src)
-            else:
-                nc.scalar.copy(out=dst, in_=src)
-
-        def spread(cols, row, engine):
+        def spread_bias():
+            nc.scalar.copy(out=bias_cols[:], in_=bias_raw[:])
             bank = next_bank([P, 4, P], F32)
             for t in range(4):
-                nc.tensor.transpose(bank[:, t, :], cols[:, t : t + 1].to_broadcast([P, P]), ident[:])
-            copy_on(engine, row.rearrange("p (n t) -> p n t", t=4), bank[:].rearrange("p t n -> p n t"))
-
-        def spread_scale(g, engine):
-            spread(scale_cols[:, g, :], scale_row[:, g * 512 : (g + 1) * 512], engine)
+                nc.tensor.transpose(bank[:, t, :], bias_cols[:, t : t + 1].to_broadcast([P, P]), ident[:])
+            nc.scalar.copy(out=bias_row[:].rearrange("p (n t) -> p n t", t=4), in_=bank[:].rearrange("p t n -> p n t"))
 
         def bias_to_partitions():
             bank = next_bank([P, 4, P], F32)
@@ -93,18 +91,30 @@ def tile_net_pa_w4_kernel(tc, A_bytes, A_scale, features, Wg_words, Wg_scales, b
             nc.scalar.copy(out=bias_chunks[:].rearrange("p (c o) -> p c o", o=1), in_=bank[:, :, 0:1])
 
         def group_features(g):
-            src = f_raw[g][:].rearrange("p j (m t) -> p t m j", t=4)
+            src = f_raw[g][:].rearrange("p j (q c) -> p q c j", q=4)
             for half in range(2):
-                bank = next_bank([P, 2, 4 * P], BF16)
-                for tl in range(2):
-                    nc.tensor.matmul(bank[:, tl, :], lhsT=ident_bf[:], rhs=src[:, 2 * half + tl], start=True, stop=True)
-                nc.scalar.copy(
-                    out=f_grouped[g][:, 2 * half : 2 * half + 2].rearrange("p t m j -> p (t m j)"),
-                    in_=bank[:].rearrange("p t n -> p (t n)"),
-                )
+                bank = next_bank([P, 4, 64, 4], BF16)
+                for ql in range(2):
+                    nc.tensor.matmul(
+                        bank[:, :, 32 * ql : 32 * (ql + 1), :].rearrange("p t m j -> p m t j"),
+                        lhsT=ident_bf[:],
+                        rhs=src[:, 2 * half + ql].rearrange("p (m t) j -> p m t j", t=4),
+                        start=True,
+                        stop=True,
+                    )
+                nc.scalar.copy(out=f_grouped[g][:, :, 64 * half : 64 * (half + 1), :], in_=bank[:])
 
         def group_features_by_copy(g):
-            nc.scalar.copy(out=f_grouped[g][:], in_=f_raw[g][:].rearrange("p j (m t) -> p t m j", t=4))
+            nc.scalar.copy(
+                out=f_grouped[g][:].rearrange("p t m j -> p m t j"),
+                in_=f_raw[g][:].rearrange("p j (m t) -> p m t j", t=4),
+            )
+
+        def group_features_on_vector(g):
+            nc.vector.tensor_copy(
+                out=f_grouped[g][:].rearrange("p t m j -> p m t j"),
+                in_=f_raw[g][:].rearrange("p j (m t) -> p m t j", t=4),
+            )
 
         def quantize_features(g):
             nc.vector.quantize_mx(
@@ -113,45 +123,57 @@ def tile_net_pa_w4_kernel(tc, A_bytes, A_scale, features, Wg_words, Wg_scales, b
                 in_=f_grouped[g][:].rearrange("p t m j -> p (t m j)"),
             )
 
-        wide, grouped, a_codes, a_scales = {}, {}, {}, {}
+        wide, grouped, a_codes, a_scales, turned_rows = {}, {}, {}, {}, {}
         agg_bf, agg_codes, agg_scales = {}, {}, {}
-        product, relu_turned, summed, unscaled = {}, {}, {}, {}
+        product, relu_turned, summed = {}, {}, {}
 
-        def scale_rows(r, parts=1):
-            wide[r] = ring("wide", r, 4, [P, NODES], BF16)
-            width = NODES // parts
-            for part in range(parts):
-                cols = slice(part * width, (part + 1) * width)
-                nc.vector.tensor_tensor(
-                    out=wide[r][:, cols], in0=a_bytes[r][:, cols].bitcast(FP8), in1=scale_row[:, cols], op=ALU.mult
-                )
+        def widen(n, first, last, engine):
+            if n not in wide:
+                wide[n] = ring("stage", n, 3, [P, 2 * NODES], BF16)
+            src = a_bytes[n][:, first:last].bitcast(FP8)
+            if engine == "scalar":
+                nc.scalar.copy(out=wide[n][:, first:last], in_=src)
+            elif engine == "vector":
+                nc.vector.tensor_copy(out=wide[n][:, first:last], in_=src)
+            else:
+                nc.gpsimd.tensor_copy(out=wide[n][:, first:last], in_=src)
 
-        def turn_rows(r):
-            words = wide[r][:].bitcast(F32)
-            grouped[r] = ring("grouped", r, 4, [P, PASSES, P, 4], BF16)
-            for half in range(2):
-                bank = next_bank([P, 2, 2, P], F32)
-                for gl in range(2):
-                    w0 = 256 * (2 * half + gl)
-                    for u in range(2):
-                        nc.tensor.transpose(bank[:, u, gl, :], words[:, w0 + u : w0 + 256 : 2], ident[:])
-                nc.scalar.copy(
-                    out=grouped[r][:, 2 * half : 2 * half + 2].bitcast(F32),
-                    in_=bank[:].rearrange("p u g i -> p g i u"),
-                )
+        def turn(n, q):
+            words = wide[n][:].bitcast(F32)
+            bank = psum.tile([P, 2, 2, P], F32, name="turn%d" % q)
+            turned_rows[n, q] = bank
+            for gl in range(2):
+                w0 = 256 * (2 * q + gl)
+                for u in range(2):
+                    nc.tensor.transpose(bank[:, u, gl, :], words[:, w0 + u : w0 + 256 : 2], ident[:])
 
-        def quantize_rows(r, first=0, count=PASSES):
-            if first == 0:
-                a_codes[r] = ring("acodes", r, 4, [P, PASSES, P], U32)
-                a_scales[r] = ring("ascales", r, 4, [P, PASSES, P], U8)
-            passes = slice(first, first + count)
-            nc.vector.quantize_mx(
-                out=a_codes[r][:, passes].rearrange("p g i -> p (g i)").bitcast(FP8X4),
-                scales=a_scales[r][:, passes].rearrange("p g i -> p (g i)"),
-                in_=grouped[r][:, passes].rearrange("p g i t -> p (g i t)"),
+        def scale_turned(n, q):
+            if q == 0:
+                grouped[n] = ring("stage", n + 2, 3, [P, 2 * PASSES, P, 4], BF16)
+            passes = slice(2 * (q % 2), 2 * (q % 2) + 2)
+            if n == PAIRS - 1:
+                dst = grouped[n][:, 2 * q : 2 * q + 2]
+            else:
+                dst = grouped[n][:].rearrange("p (g h) i t -> p h g i t", h=2)[:, q // 2, passes]
+            nc.vector.tensor_tensor(
+                out=dst.rearrange("p g i (u e) -> p g i u e", u=2),
+                in0=turned_rows[n, q][:].bitcast(BF16).rearrange("p u g (i e) -> p g i u e", e=2),
+                in1=scale_cols[:, passes, :].rearrange("p g (u e) -> p g u e", u=2).unsqueeze(2).to_broadcast([P, 2, P, 2, 2]),
+                op=ALU.mult,
             )
 
-        def aggregate(r):
+        def quantize_rows(n, first=0, count=2 * PASSES):
+            if first == 0:
+                a_codes[n] = ring("acodes", n, 3, [P, 2 * PASSES, P], U32)
+                a_scales[n] = ring("ascales", n, 3, [P, 2 * PASSES, P], U8)
+            part = slice(first, first + count)
+            nc.vector.quantize_mx(
+                out=a_codes[n][:, part].rearrange("p g i -> p (g i)").bitcast(FP8X4),
+                scales=a_scales[n][:, part].rearrange("p g i -> p (g i)"),
+                in_=grouped[n][:, part].rearrange("p g i t -> p (g i t)"),
+            )
+
+        def aggregate(n, h):
             bank = next_bank([P, 4, P], F32)
             for g in range(PASSES):
                 for t in range(4):
@@ -159,176 +181,196 @@ def tile_net_pa_w4_kernel(tc, A_bytes, A_scale, features, Wg_words, Wg_scales, b
                         out=bank[:, t, :],
                         lhsT=f_codes[g][:, t * P : (t + 1) * P].bitcast(FP8X4),
                         lhsT_scale=f_scales[g][:, t * P : (t + 1) * P],
-                        rhs=a_codes[r][:, g, :].bitcast(FP8X4),
-                        rhs_scale=a_scales[r][:, g, :],
+                        rhs=a_codes[n][:, PASSES * h + g, :].bitcast(FP8X4),
+                        rhs_scale=a_scales[n][:, PASSES * h + g, :],
                         start=(g == 0 and t == 0),
                         stop=(g == PASSES - 1 and t == 3),
                     )
-            first = first_of(r)
-            if first == r:
-                width = 2 * P if turned(r) else P
-                agg_bf[r] = ring("aggbf", r, 6, [P, width, 4], BF16)
-                agg_codes[r] = ring("aggcodes", r, 6, [P, width], U32)
-                agg_scales[r] = ring("aggscales", r, 6, [P, width], U8)
-            nc.scalar.copy(
-                out=agg_bf[first][:, (r - first) * P : (r - first + 1) * P], in_=bank[:].rearrange("p t i -> p i t")
-            )
+            if h == 0:
+                agg_bf[n] = ring("aggbf", n, 3, [P, 2, P, 4], BF16)
+                agg_codes[n] = ring("aggcodes", n, 3, [P, 2 * P], U32)
+                agg_scales[n] = ring("aggscales", n, 3, [P, 2 * P], U8)
+            nc.scalar.copy(out=agg_bf[n][:, h], in_=bank[:].rearrange("p t i -> p i t"))
 
-        def quantize_agg(r):
+        def aggregate_pair(n):
+            agg_bf[n] = ring("aggbf", n, 3, [P, 2, P, 4], BF16)
+            agg_codes[n] = ring("aggcodes", n, 3, [P, 2 * P], U32)
+            agg_scales[n] = ring("aggscales", n, 3, [P, 2 * P], U8)
+            for half in range(2):
+                bank = next_bank([P, 2, 2 * P], F32)
+                for g in range(PASSES):
+                    for tl in range(2):
+                        t = 2 * half + tl
+                        nc.tensor.matmul_mx(
+                            out=bank[:, tl, :],
+                            lhsT=f_codes[g][:, t * P : (t + 1) * P].bitcast(FP8X4),
+                            lhsT_scale=f_scales[g][:, t * P : (t + 1) * P],
+                            rhs=a_codes[n][:, 2 * g : 2 * g + 2].rearrange("p h i -> p (h i)").bitcast(FP8X4),
+                            rhs_scale=a_scales[n][:, 2 * g : 2 * g + 2].rearrange("p h i -> p (h i)"),
+                            start=(g == 0 and tl == 0),
+                            stop=(g == PASSES - 1 and tl == 1),
+                        )
+                nc.scalar.copy(
+                    out=agg_bf[n][:].rearrange("p h i t -> p (h i) t")[:, :, 2 * half : 2 * half + 2],
+                    in_=bank[:].rearrange("p t i -> p i t"),
+                )
+
+        def quantize_agg(n, first=0, count=2):
+            cols = slice(first * P, (first + count) * P)
             nc.vector.quantize_mx(
-                out=agg_codes[r][:].bitcast(FP8X4),
-                scales=agg_scales[r][:],
-                in_=agg_bf[r][:].rearrange("p i t -> p (i t)"),
+                out=agg_codes[n][:, cols].bitcast(FP8X4),
+                scales=agg_scales[n][:, cols],
+                in_=agg_bf[n][:, first : first + count].rearrange("p h i t -> p (h i t)"),
             )
 
-        def project(r):
-            product[r] = next_bank([P, D], F32)
+        def project(n, h):
+            cols = slice(h * P, (h + 1) * P)
+            product[n, h] = next_bank([P, D], F32)
             nc.tensor.matmul_mx(
-                out=product[r][:],
-                lhsT=agg_codes[r][:].bitcast(FP8X4),
-                lhsT_scale=agg_scales[r][:],
+                out=product[n, h][:],
+                lhsT=agg_codes[n][:, cols].bitcast(FP8X4),
+                lhsT_scale=agg_scales[n][:, cols],
                 rhs=w_words[:].bitcast(FP4X4),
                 rhs_scale=w_scales[:],
                 start=True,
                 stop=True,
             )
 
-        def add_bias(r):
-            summed[r] = ring("summed", r, 6, [P, D], F32)
-            nc.vector.tensor_tensor(out=summed[r][:], in0=product[r][:], in1=bias_row[:], op=ALU.add)
+        def add_bias(n, h):
+            summed[n, h] = ring("summed", 2 * n + h, 4, [P, D], F32)
+            nc.vector.tensor_tensor(out=summed[n, h][:], in0=product[n, h][:], in1=bias_row[:], op=ALU.add)
 
-        def relu_store(r, engine="scalar"):
-            rows = ring("rows", r, 8, [P, D], F32)
+        def store(n, h, rows):
+            r0 = (2 * n + h) * P
+            nc.sync.dma_start(out=out[r0 : r0 + P, :], in_=rows[:])
+
+        def relu_store(n, h, engine="scalar"):
+            rows = ring("rows", 2 * n + h, 6, [P, D], F32)
             if engine == "vector":
-                nc.vector.tensor_scalar(out=rows[:], in0=summed[r][:], scalar1=0.0, scalar2=None, op0=ALU.max)
+                nc.vector.tensor_scalar(out=rows[:], in0=summed[n, h][:], scalar1=0.0, scalar2=None, op0=ALU.max)
             else:
-                nc.scalar.activation(out=rows[:], in_=summed[r][:], func=ACT.Relu)
-            nc.sync.dma_start(out=out[r * P : (r + 1) * P, :], in_=rows[:])
+                nc.scalar.activation(out=rows[:], in_=summed[n, h][:], func=ACT.Relu)
+            store(n, h, rows)
 
-        def project_turned(first, half):
-            if half == 0:
-                relu_turned[first] = ring("reluturned", TURNED.index(first) // 2, 2, [P, 4, 2 * P], F32)
-            bank = next_bank([P, 2, 2 * P], F32)
-            for cl in range(2):
-                c = 2 * half + cl
-                nc.tensor.matmul_mx(
-                    out=bank[:, cl, :],
-                    lhsT=w_words[:, 2 * c * P : 2 * (c + 1) * P].bitcast(FP4X4),
-                    lhsT_scale=w_scales[:, c * P : (c + 1) * P],
-                    rhs=agg_codes[first][:].bitcast(FP8X4),
-                    rhs_scale=agg_scales[first][:],
-                    start=True,
-                    stop=True,
-                )
-            for cl in range(2):
-                c = 2 * half + cl
-                nc.scalar.activation(
-                    out=relu_turned[first][:, c, :], in_=bank[:, cl, :], func=ACT.Relu, bias=bias_chunks[:, c : c + 1]
-                )
+        def project_turned(n):
+            relu_turned[n] = ring("reluturned", n, 2, [P, 4, 2 * P], F32)
+            for half in range(2):
+                bank = next_bank([P, 2, 2 * P], F32)
+                for cl in range(2):
+                    c = 2 * half + cl
+                    nc.tensor.matmul_mx(
+                        out=bank[:, cl, :],
+                        lhsT=w_words[:, 2 * c * P : 2 * (c + 1) * P].bitcast(FP4X4),
+                        lhsT_scale=w_scales[:, c * P : (c + 1) * P],
+                        rhs=agg_codes[n][:].bitcast(FP8X4),
+                        rhs_scale=agg_scales[n][:],
+                        start=True,
+                        stop=True,
+                    )
+                for cl in range(2):
+                    c = 2 * half + cl
+                    nc.scalar.activation(
+                        out=relu_turned[n][:, c, :], in_=bank[:, cl, :], func=ACT.Relu, bias=bias_chunks[:, c : c + 1]
+                    )
 
-        def turn_back_store(r):
-            first = first_of(r)
+        def turn_back_store(n, h):
             bank = next_bank([P, 4, P], F32)
             for c in range(4):
-                nc.tensor.transpose(bank[:, c, :], relu_turned[first][:, c, (r - first) * P : (r - first + 1) * P], ident[:])
-            rows = ring("rows", r, 8, [P, D], F32)
+                nc.tensor.transpose(bank[:, c, :], relu_turned[n][:, c, h * P : (h + 1) * P], ident[:])
+            rows = ring("rows", 2 * n + h, 6, [P, D], F32)
             nc.scalar.copy(out=rows[:], in_=bank[:].rearrange("p c n -> p (c n)"))
-            nc.sync.dma_start(out=out[r * P : (r + 1) * P, :], in_=rows[:])
-
-        def turned(r):
-            return r in TURNED
-
-        def first_of(r):
-            return TURNED[TURNED.index(r) // 2 * 2] if turned(r) else r
-
-        def plain(r):
-            return 0 <= r < TILES and not turned(r)
+            store(n, h, rows)
 
         make_identity(nc, ident[:])
         nc.vector.memset(w_scales[:].bitcast(I32), 0)
         nc.scalar.copy(out=ident_bf[:], in_=ident[:])
 
+        load_a(0, 0)
         nc.sync.dma_start(out=scale_cols[:], in_=A_scale.rearrange("o (g p t) -> p (o g) t", p=P, t=4))
-        load_a(0)
+        load_a(0, 1)
         load_f(0)
-        load_a(1)
+        load_pair(1)
         load_f(1)
         load_f(2)
         load_f(3)
-        load_a(2)
-        load_a(3)
+        load_pair(2)
         nc.sync.dma_start(out=bias_raw[:], in_=bg.rearrange("(p t) -> p t", t=4))
-        load_a(4)
+        load_pair(3)
         load_w()
-        for r in range(5, TILES):
-            load_a(r)
+        for n in range(4, PAIRS):
+            load_pair(n)
 
-        spread_scale(0, "vector")
-        for g in range(1, PASSES):
-            spread_scale(g, "scalar")
-        scale_rows(0, parts=4)
+        for q in range(3):
+            widen(0, q * QUARTER, (q + 1) * QUARTER, "vector")
+        widen(0, 3 * QUARTER, 4 * QUARTER, "scalar")
+        for q in range(4):
+            turn(0, q)
         group_features_by_copy(0)
-        turn_rows(0)
-        scale_rows(1)
-        group_features(1)
-        group_features_by_copy(2)
-        group_features(3)
-        quantize_features(0)
-        quantize_rows(0)
-        quantize_features(1)
-        turn_rows(1)
+        widen(1, 0, QUARTER, "scalar")
+        widen(1, QUARTER, 4 * QUARTER, "gpsimd")
+        for q in range(4):
+            scale_turned(0, q)
+        group_features_by_copy(1)
+        group_features(2)
+        for q in range(4):
+            turn(1, q)
+        group_features_on_vector(3)
+        for g in (0, 3, 1, 2):
+            quantize_features(g)
+        spread_bias()
 
-        for r in range(1, TILES - 1):
-            scale_rows(r + 1)
-            if r == 1:
-                nc.vector.tensor_copy(out=bias_cols[:], in_=bias_raw[:])
-            if plain(r - 4) and r <= 13:
-                add_bias(r - 4)
-            if r == 1:
-                quantize_features(2)
-                quantize_features(3)
-            quantize_rows(r)
-            if r <= 13 and (plain(r - 3) or (turned(r - 3) and first_of(r - 3) == r - 3)):
-                quantize_agg(r - 3)
-            if r >= 13:
-                quantize_agg(r - 2)
-            if r > 13:
-                add_bias(r - 4)
-
-            turn_rows(r + 1)
-            if r == 1:
-                spread(bias_cols[:], bias_row[:], "scalar")
-            if r == 2:
+        last = PAIRS - 1
+        for n in range(1, last):
+            if n >= 2:
+                quantize_agg(n - 2)
+            quantize_rows(n - 1)
+            widen(n + 1, 0, QUARTER, "scalar")
+            widen(n + 1, QUARTER, 4 * QUARTER, "gpsimd")
+            for q in range(4):
+                scale_turned(n, q)
+            aggregate_pair(n - 1)
+            if n >= 2:
+                project_turned(n - 2)
+            turn(n + 1, 0)
+            if n == 1:
                 bias_to_partitions()
-            if turned(r - 5):
-                turn_back_store(r - 5)
-            if turned(r - 3):
-                project_turned(first_of(r - 3), r - 3 - first_of(r - 3))
-            if plain(r - 3) and r <= 13:
-                project(r - 3)
-            if r >= 13:
-                project(r - 2)
-            if r == 1:
-                aggregate(0)
-            aggregate(r)
-            if plain(r - 4):
-                relu_store(r - 4)
+            if n >= 3:
+                turn_back_store(n - 3, 0)
+                turn_back_store(n - 3, 1)
+            for q in range(1, 4):
+                turn(n + 1, q)
 
-        add_bias(11)
-        quantize_rows(15)
-        aggregate(15)
-        add_bias(12)
-        quantize_agg(13)
-        quantize_agg(14)
-        project(13)
-        project(14)
-        relu_store(11)
-        relu_store(12)
-        add_bias(13)
-        quantize_agg(15)
-        project(15)
-        relu_store(13)
-        add_bias(14)
-        add_bias(15)
-        relu_store(14)
-        relu_store(15, "vector")
+        quantize_agg(last - 2)
+        quantize_rows(last - 1)
+        scale_turned(last, 0)
+        scale_turned(last, 1)
+        scale_turned(last, 2)
+        quantize_rows(last, 0, 4)
+        aggregate_pair(last - 1)
+        project_turned(last - 2)
+        bank_names.extend(["turn0", "turn1", "turn2"])
+        turn_back_store(last - 3, 0)
+        turn_back_store(last - 3, 1)
+        quantize_agg(last - 1)
+        scale_turned(last, 3)
+        bank_names.append("turn3")
+        quantize_rows(last, 4, 2)
+        quantize_rows(last, 6, 2)
+        aggregate(last, 0)
+        project(last - 1, 0)
+        project(last - 1, 1)
+        aggregate(last, 1)
+        add_bias(last - 1, 0)
+        quantize_agg(last, 0, 1)
+        add_bias(last - 1, 1)
+        relu_store(last - 1, 0, "vector")
+        relu_store(last - 1, 1, "vector")
+        project(last, 0)
+        turn_back_store(last - 2, 0)
+        turn_back_store(last - 2, 1)
+        quantize_agg(last, 1, 1)
+        project(last, 1)
+        add_bias(last, 0)
+        add_bias(last, 1)
+        relu_store(last, 0)
+        relu_store(last, 1, "vector")

@@ -20,6 +20,7 @@ P = 128
 PASSES = NODES // 512
 PAIRS = NODES // (2 * P)
 QUARTER = 1024
+SCALAR_SHARE = 1536
 FLOPS = 2 * NODES * NODES * D + 2 * NODES * D * D
 
 
@@ -324,8 +325,8 @@ def tile_net_pa_w4_kernel(tc, A_bytes, A_scale, features, Wg_words, Wg_scales, b
             if n >= 2:
                 quantize_agg(n - 2)
             quantize_rows(n - 1)
-            widen(n + 1, 0, QUARTER, "scalar")
-            widen(n + 1, QUARTER, 4 * QUARTER, "gpsimd")
+            widen(n + 1, 0, SCALAR_SHARE, "scalar")
+            widen(n + 1, SCALAR_SHARE, 4 * QUARTER, "gpsimd")
             for q in range(4):
                 scale_turned(n, q)
             aggregate_pair(n - 1)

@@ -20,7 +20,6 @@ P = 128
 PASSES = NODES // 512
 PAIRS = NODES // (2 * P)
 QUARTER = 1024
-SCALAR_SHARE = 1536
 FLOPS = 2 * NODES * NODES * D + 2 * NODES * D * D
 
 
@@ -43,6 +42,12 @@ def tile_net_pa_w4_kernel(tc, A_bytes, A_scale, features, Wg_words, Wg_scales, b
         f_scales = [keep.tile([P, D], U8, name="fscales%d" % g, align_bytes=64) for g in range(PASSES)]
         w_words = keep.tile([P, 2 * D], U8, name="wwords", align_bytes=64)
         w_scales = keep.tile([P, D], U8, name="wscales", align_bytes=64)
+        early_wide = keep.tile([P, QUARTER], BF16, name="earlywide", align_bytes=64)
+        early_planes = keep.tile([P, 2, 2, P, 2], BF16, name="earlyplanes", align_bytes=64)
+        early_grouped = keep.tile([P, 2, P, 4], BF16, name="earlygrouped", align_bytes=64)
+        early_codes = keep.tile([P, 2, P], U32, name="earlycodes", align_bytes=64)
+        early_scales = keep.tile([P, 2, P], U8, name="earlyscales", align_bytes=64)
+        early_bytes = keep.tile([P, QUARTER], U8, name="earlybytes", align_bytes=64)
         ident = keep.tile([P, P], F32, name="ident", align_bytes=64)
         ident_bf = keep.tile([P, P], BF16, name="identbf", align_bytes=64)
 
@@ -79,7 +84,6 @@ def tile_net_pa_w4_kernel(tc, A_bytes, A_scale, features, Wg_words, Wg_scales, b
                 )
 
         def spread_bias():
-            nc.scalar.copy(out=bias_cols[:], in_=bias_raw[:])
             bank = next_bank([P, 4, P], F32)
             for t in range(4):
                 nc.tensor.transpose(bank[:, t, :], bias_cols[:, t : t + 1].to_broadcast([P, P]), ident[:])
@@ -130,7 +134,7 @@ def tile_net_pa_w4_kernel(tc, A_bytes, A_scale, features, Wg_words, Wg_scales, b
 
         def widen(n, first, last, engine):
             if n not in wide:
-                wide[n] = ring("stage", n, 3, [P, 2 * NODES], BF16)
+                wide[n] = ring("stage", n + 1, 2, [P, 2 * NODES], BF16) if n else ring("grouped", 0, 2, [P, 2 * NODES], BF16)
             src = a_bytes[n][:, first:last].bitcast(FP8)
             if engine == "scalar":
                 nc.scalar.copy(out=wide[n][:, first:last], in_=src)
@@ -150,7 +154,7 @@ def tile_net_pa_w4_kernel(tc, A_bytes, A_scale, features, Wg_words, Wg_scales, b
 
         def scale_turned(n, q):
             if q == 0:
-                grouped[n] = ring("stage", n + 2, 3, [P, 2 * PASSES, P, 4], BF16)
+                grouped[n] = ring("grouped" if n else "stage", n if n else 1, 2, [P, 2 * PASSES, P, 4], BF16)
             passes = slice(2 * (q % 2), 2 * (q % 2) + 2)
             if n == PAIRS - 1:
                 dst = grouped[n][:, 2 * q : 2 * q + 2]
@@ -161,6 +165,39 @@ def tile_net_pa_w4_kernel(tc, A_bytes, A_scale, features, Wg_words, Wg_scales, b
                 in0=turned_rows[n, q][:].bitcast(BF16).rearrange("p u g (i e) -> p g i u e", e=2),
                 in1=scale_cols[:, passes, :].rearrange("p g (u e) -> p g u e", u=2).unsqueeze(2).to_broadcast([P, 2, P, 2, 2]),
                 op=ALU.mult,
+            )
+
+        def turn_early():
+            words = early_wide[:].bitcast(F32)
+            name = bank_names[0]
+            bank_names.remove(name)
+            bank = psum.tile([P, 2, 2, P], F32, name=name)
+            for gl in range(2):
+                for u in range(2):
+                    nc.tensor.transpose(bank[:, u, gl, :], words[:, 256 * gl + u : 256 * (gl + 1) : 2], ident[:])
+            return name, bank[:].bitcast(BF16).rearrange("p u g (i e) -> p u g i e", e=2)
+
+        def scale_early(values, first, count):
+            for plane in range(first, first + count):
+                gl, t = divmod(plane, 4)
+                nc.scalar.activation(
+                    out=early_planes[:, gl, t // 2, :, t % 2],
+                    in_=values[:, t // 2, gl, :, t % 2],
+                    func=ACT.Copy,
+                    scale=scale_cols[:, 2 + gl, t : t + 1],
+                )
+
+        def group_early():
+            nc.scalar.copy(
+                out=early_grouped[:].bitcast(F32),
+                in_=early_planes[:].rearrange("p g u i e -> p g u (i e)").bitcast(F32).rearrange("p g u i -> p g i u"),
+            )
+
+        def quantize_early():
+            nc.vector.quantize_mx(
+                out=early_codes[:].rearrange("p g i -> p (g i)").bitcast(FP8X4),
+                scales=early_scales[:].rearrange("p g i -> p (g i)"),
+                in_=early_grouped[:].rearrange("p g i t -> p (g i t)"),
             )
 
         def quantize_rows(n, first=0, count=2 * PASSES):
@@ -174,46 +211,53 @@ def tile_net_pa_w4_kernel(tc, A_bytes, A_scale, features, Wg_words, Wg_scales, b
                 in_=grouped[n][:, part].rearrange("p g i t -> p (g i t)"),
             )
 
-        def aggregate(n, h):
+        def aggregate(n, h, order=range(PASSES)):
             bank = next_bank([P, 4, P], F32)
-            for g in range(PASSES):
+            for g in order:
+                early = h == 1 and g >= 2
+                codes = early_codes[:, g - 2, :] if early else a_codes[n][:, PASSES * h + g, :]
+                scales = early_scales[:, g - 2, :] if early else a_scales[n][:, PASSES * h + g, :]
                 for t in range(4):
                     nc.tensor.matmul_mx(
                         out=bank[:, t, :],
                         lhsT=f_codes[g][:, t * P : (t + 1) * P].bitcast(FP8X4),
                         lhsT_scale=f_scales[g][:, t * P : (t + 1) * P],
-                        rhs=a_codes[n][:, PASSES * h + g, :].bitcast(FP8X4),
-                        rhs_scale=a_scales[n][:, PASSES * h + g, :],
-                        start=(g == 0 and t == 0),
-                        stop=(g == PASSES - 1 and t == 3),
+                        rhs=codes.bitcast(FP8X4),
+                        rhs_scale=scales,
+                        start=(g == order[0] and t == 0),
+                        stop=(g == order[-1] and t == 3),
                     )
             if h == 0:
-                agg_bf[n] = ring("aggbf", n, 3, [P, 2, P, 4], BF16)
+                agg_bf[n] = ring("stage", n, 2, [P, 2, P, 4], BF16)
                 agg_codes[n] = ring("aggcodes", n, 3, [P, 2 * P], U32)
                 agg_scales[n] = ring("aggscales", n, 3, [P, 2 * P], U8)
             nc.scalar.copy(out=agg_bf[n][:, h], in_=bank[:].rearrange("p t i -> p i t"))
 
-        def aggregate_pair(n):
-            agg_bf[n] = ring("aggbf", n, 3, [P, 2, P, 4], BF16)
+        def aggregate_pair(n, order=range(PASSES)):
+            agg_bf[n] = ring("stage", n, 2, [P, 2, P, 4], BF16)
             agg_codes[n] = ring("aggcodes", n, 3, [P, 2 * P], U32)
             agg_scales[n] = ring("aggscales", n, 3, [P, 2 * P], U8)
+            banks = [next_bank([P, 2, 2 * P], F32) for half in range(2)]
+            if n == 0:
+                steps = [(half, g) for g in order for half in range(2)]
+            else:
+                steps = [(half, g) for half in range(2) for g in order]
+            for half, g in steps:
+                for tl in range(2):
+                    t = 2 * half + tl
+                    nc.tensor.matmul_mx(
+                        out=banks[half][:, tl, :],
+                        lhsT=f_codes[g][:, t * P : (t + 1) * P].bitcast(FP8X4),
+                        lhsT_scale=f_scales[g][:, t * P : (t + 1) * P],
+                        rhs=a_codes[n][:, 2 * g : 2 * g + 2].rearrange("p h i -> p (h i)").bitcast(FP8X4),
+                        rhs_scale=a_scales[n][:, 2 * g : 2 * g + 2].rearrange("p h i -> p (h i)"),
+                        start=(g == order[0] and tl == 0),
+                        stop=(g == order[-1] and tl == 1),
+                    )
             for half in range(2):
-                bank = next_bank([P, 2, 2 * P], F32)
-                for g in range(PASSES):
-                    for tl in range(2):
-                        t = 2 * half + tl
-                        nc.tensor.matmul_mx(
-                            out=bank[:, tl, :],
-                            lhsT=f_codes[g][:, t * P : (t + 1) * P].bitcast(FP8X4),
-                            lhsT_scale=f_scales[g][:, t * P : (t + 1) * P],
-                            rhs=a_codes[n][:, 2 * g : 2 * g + 2].rearrange("p h i -> p (h i)").bitcast(FP8X4),
-                            rhs_scale=a_scales[n][:, 2 * g : 2 * g + 2].rearrange("p h i -> p (h i)"),
-                            start=(g == 0 and tl == 0),
-                            stop=(g == PASSES - 1 and tl == 1),
-                        )
                 nc.scalar.copy(
                     out=agg_bf[n][:].rearrange("p h i t -> p (h i) t")[:, :, 2 * half : 2 * half + 2],
-                    in_=bank[:].rearrange("p t i -> p i t"),
+                    in_=banks[half][:].rearrange("p t i -> p i t"),
                 )
 
         def quantize_agg(n, first=0, count=2):
@@ -246,7 +290,7 @@ def tile_net_pa_w4_kernel(tc, A_bytes, A_scale, features, Wg_words, Wg_scales, b
             nc.sync.dma_start(out=out[r0 : r0 + P, :], in_=rows[:])
 
         def relu_store(n, h, engine="scalar"):
-            rows = ring("rows", 2 * n + h, 6, [P, D], F32)
+            rows = ring("rows", 2 * n + h, 8, [P, D], F32)
             if engine == "vector":
                 nc.vector.tensor_scalar(out=rows[:], in0=summed[n, h][:], scalar1=0.0, scalar2=None, op0=ALU.max)
             else:
@@ -254,7 +298,7 @@ def tile_net_pa_w4_kernel(tc, A_bytes, A_scale, features, Wg_words, Wg_scales, b
             store(n, h, rows)
 
         def project_turned(n):
-            relu_turned[n] = ring("reluturned", n, 2, [P, 4, 2 * P], F32)
+            relu_turned[n] = ring("reluturned", n, 3, [P, 4, 2 * P], F32)
             for half in range(2):
                 bank = next_bank([P, 2, 2 * P], F32)
                 for cl in range(2):
@@ -274,12 +318,15 @@ def tile_net_pa_w4_kernel(tc, A_bytes, A_scale, features, Wg_words, Wg_scales, b
                         out=relu_turned[n][:, c, :], in_=bank[:, cl, :], func=ACT.Relu, bias=bias_chunks[:, c : c + 1]
                     )
 
-        def turn_back_store(n, h):
+        def turn_back_store(n, h, engine="scalar"):
             bank = next_bank([P, 4, P], F32)
             for c in range(4):
                 nc.tensor.transpose(bank[:, c, :], relu_turned[n][:, c, h * P : (h + 1) * P], ident[:])
-            rows = ring("rows", 2 * n + h, 6, [P, D], F32)
-            nc.scalar.copy(out=rows[:], in_=bank[:].rearrange("p c n -> p (c n)"))
+            rows = ring("rows", 2 * n + h, 8, [P, D], F32)
+            if engine == "vector":
+                nc.vector.tensor_copy(out=rows[:], in_=bank[:].rearrange("p c n -> p (c n)"))
+            else:
+                nc.scalar.copy(out=rows[:], in_=bank[:].rearrange("p c n -> p (c n)"))
             store(n, h, rows)
 
         make_identity(nc, ident[:])
@@ -291,15 +338,18 @@ def tile_net_pa_w4_kernel(tc, A_bytes, A_scale, features, Wg_words, Wg_scales, b
         load_a(0, 1)
         load_f(0)
         load_pair(1)
-        load_f(1)
         load_f(2)
         load_f(3)
-        load_pair(2)
         nc.sync.dma_start(out=bias_raw[:], in_=bg.rearrange("(p t) -> p t", t=4))
+        load_f(1)
+        nc.sync.dma_start(out=early_bytes[:], in_=A_bytes[NODES - P :, NODES - QUARTER :])
+        load_pair(2)
         load_pair(3)
         load_w()
-        for n in range(4, PAIRS):
+        for n in range(4, PAIRS - 1):
             load_pair(n)
+        load_a(PAIRS - 1, 0)
+        nc.sync.dma_start(out=a_bytes[PAIRS - 1][:, NODES : NODES + QUARTER], in_=A_bytes[NODES - P :, 0:QUARTER])
 
         for q in range(3):
             widen(0, q * QUARTER, (q + 1) * QUARTER, "vector")
@@ -307,17 +357,19 @@ def tile_net_pa_w4_kernel(tc, A_bytes, A_scale, features, Wg_words, Wg_scales, b
         for q in range(4):
             turn(0, q)
         group_features_by_copy(0)
-        widen(1, 0, QUARTER, "scalar")
-        widen(1, QUARTER, 4 * QUARTER, "gpsimd")
+        widen(1, 0, 1792, "scalar")
+        widen(1, 1792, 4 * QUARTER, "gpsimd")
         for q in range(4):
             scale_turned(0, q)
-        group_features_by_copy(1)
         group_features(2)
+        nc.scalar.copy(out=bias_cols[:], in_=bias_raw[:])
+        group_features_by_copy(1)
         for q in range(4):
             turn(1, q)
         group_features_on_vector(3)
-        for g in (0, 3, 1, 2):
+        for g in (0, 3, 2):
             quantize_features(g)
+        nc.scalar.copy(out=early_wide[:], in_=early_bytes[:].bitcast(FP8))
         spread_bias()
 
         last = PAIRS - 1
@@ -325,52 +377,63 @@ def tile_net_pa_w4_kernel(tc, A_bytes, A_scale, features, Wg_words, Wg_scales, b
             if n >= 2:
                 quantize_agg(n - 2)
             quantize_rows(n - 1)
-            widen(n + 1, 0, SCALAR_SHARE, "scalar")
-            widen(n + 1, SCALAR_SHARE, 4 * QUARTER, "gpsimd")
+            if n == 1:
+                quantize_features(1)
+            quarters = 3 if n + 1 == last else 4
+            share = 1280 if n + 1 < last else QUARTER
+            widen(n + 1, 0, share, "scalar")
+            widen(n + 1, share, quarters * QUARTER, "gpsimd")
             for q in range(4):
                 scale_turned(n, q)
-            aggregate_pair(n - 1)
+            if n == 2:
+                scale_early(early_values, 3, 5)
+                bank_names.append(early_bank)
+            aggregate_pair(n - 1, (0, 3, 2, 1) if n == 1 else range(PASSES))
             if n >= 2:
                 project_turned(n - 2)
             turn(n + 1, 0)
             if n == 1:
                 bias_to_partitions()
+                early_bank, early_values = turn_early()
+                scale_early(early_values, 0, 3)
+            if n == 3:
+                group_early()
             if n >= 3:
                 turn_back_store(n - 3, 0)
                 turn_back_store(n - 3, 1)
-            for q in range(1, 4):
+            for q in range(1, quarters):
                 turn(n + 1, q)
 
+        b0, b1, b2, b3 = bank_names
+        bank_names.clear()
+        bank_names.extend([b0, b1, "turn3", b2, b3, b0, b1, "turn0", "turn1", "turn3", b2, b3, b0, b1])
+        turn_back_store(last - 3, 0)
+        turn_back_store(last - 3, 1)
         quantize_agg(last - 2)
         quantize_rows(last - 1)
         scale_turned(last, 0)
         scale_turned(last, 1)
-        scale_turned(last, 2)
+        quantize_early()
         quantize_rows(last, 0, 4)
-        aggregate_pair(last - 1)
+        scale_turned(last, 2)
         project_turned(last - 2)
-        bank_names.extend(["turn0", "turn1", "turn2"])
-        turn_back_store(last - 3, 0)
-        turn_back_store(last - 3, 1)
-        quantize_agg(last - 1)
-        scale_turned(last, 3)
-        bank_names.append("turn3")
-        quantize_rows(last, 4, 2)
-        quantize_rows(last, 6, 2)
-        aggregate(last, 0)
-        project(last - 1, 0)
-        project(last - 1, 1)
-        aggregate(last, 1)
-        add_bias(last - 1, 0)
-        quantize_agg(last, 0, 1)
-        add_bias(last - 1, 1)
-        relu_store(last - 1, 0, "vector")
-        relu_store(last - 1, 1, "vector")
-        project(last, 0)
+        aggregate_pair(last - 1)
         turn_back_store(last - 2, 0)
         turn_back_store(last - 2, 1)
+        quantize_agg(last - 1)
+        quantize_rows(last, 4, 2)
+        aggregate(last, 0)
+        project(last - 1, 0)
+        aggregate(last, 1, (2, 3, 0, 1))
+        project(last - 1, 1)
+        add_bias(last - 1, 0)
+        quantize_agg(last, 0, 1)
+        project(last, 0)
+        relu_store(last - 1, 0, "vector")
+        add_bias(last - 1, 1)
         quantize_agg(last, 1, 1)
         project(last, 1)
+        relu_store(last - 1, 1)
         add_bias(last, 0)
         add_bias(last, 1)
         relu_store(last, 0)

@@ -37,7 +37,9 @@ def tile_net_pa_w4_kernel(tc, A_bytes, A_scale, features, Wg_words, Wg_scales, b
         bias_row = keep.tile([P, D], F32, name="biasrow", align_bytes=64)
         bias_chunks = keep.tile([P, 4], F32, name="biaschunks")
         f_raw = [keep.tile([P, 4, D], BF16, name="fraw%d" % g, align_bytes=64) for g in range(PASSES)]
-        f_grouped = [keep.tile([P, 4, P, 4], BF16, name="fgrouped%d" % g, align_bytes=64) for g in range(PASSES)]
+        f_grouped = [
+            keep.tile([P, 4, P, 4], BF16, name="afterfeatures" if g == 1 else "fgrouped%d" % g, align_bytes=64) for g in range(PASSES)
+        ]
         f_codes = [keep.tile([P, D], U32, name="fcodes%d" % g, align_bytes=64) for g in range(PASSES)]
         f_scales = [keep.tile([P, D], U8, name="fscales%d" % g, align_bytes=64) for g in range(PASSES)]
         w_words = keep.tile([P, 2 * D], U8, name="wwords", align_bytes=64)
@@ -134,7 +136,8 @@ def tile_net_pa_w4_kernel(tc, A_bytes, A_scale, features, Wg_words, Wg_scales, b
 
         def widen(n, first, last, engine):
             if n not in wide:
-                wide[n] = ring("stage", n + 1, 2, [P, 2 * NODES], BF16) if n else ring("grouped", 0, 2, [P, 2 * NODES], BF16)
+                name = "afterfeatures" if n == 2 else "stage%d" % (n % 3)
+                wide[n] = keep.tile([P, 2 * NODES], BF16, name=name, align_bytes=64)
             src = a_bytes[n][:, first:last].bitcast(FP8)
             if engine == "scalar":
                 nc.scalar.copy(out=wide[n][:, first:last], in_=src)
@@ -154,7 +157,7 @@ def tile_net_pa_w4_kernel(tc, A_bytes, A_scale, features, Wg_words, Wg_scales, b
 
         def scale_turned(n, q):
             if q == 0:
-                grouped[n] = ring("grouped" if n else "stage", n if n else 1, 2, [P, 2 * PASSES, P, 4], BF16)
+                grouped[n] = ring("stage", n + 2, 3, [P, 2 * PASSES, P, 4], BF16)
             passes = slice(2 * (q % 2), 2 * (q % 2) + 2)
             if n == PAIRS - 1:
                 dst = grouped[n][:, 2 * q : 2 * q + 2]
@@ -228,13 +231,13 @@ def tile_net_pa_w4_kernel(tc, A_bytes, A_scale, features, Wg_words, Wg_scales, b
                         stop=(g == order[-1] and t == 3),
                     )
             if h == 0:
-                agg_bf[n] = ring("stage", n, 2, [P, 2, P, 4], BF16)
+                agg_bf[n] = ring("aggbf", n, 3, [P, 2, P, 4], BF16)
                 agg_codes[n] = ring("aggcodes", n, 3, [P, 2 * P], U32)
                 agg_scales[n] = ring("aggscales", n, 3, [P, 2 * P], U8)
             nc.scalar.copy(out=agg_bf[n][:, h], in_=bank[:].rearrange("p t i -> p i t"))
 
         def aggregate_pair(n, order=range(PASSES)):
-            agg_bf[n] = ring("stage", n, 2, [P, 2, P, 4], BF16)
+            agg_bf[n] = ring("aggbf", n, 3, [P, 2, P, 4], BF16)
             agg_codes[n] = ring("aggcodes", n, 3, [P, 2 * P], U32)
             agg_scales[n] = ring("aggscales", n, 3, [P, 2 * P], U8)
             banks = [next_bank([P, 2, 2 * P], F32) for half in range(2)]
@@ -380,7 +383,7 @@ def tile_net_pa_w4_kernel(tc, A_bytes, A_scale, features, Wg_words, Wg_scales, b
             if n == 1:
                 quantize_features(1)
             quarters = 3 if n + 1 == last else 4
-            share = 1280 if n + 1 < last else QUARTER
+            share = QUARTER if n + 1 == last else 1536
             widen(n + 1, 0, share, "scalar")
             widen(n + 1, share, quarters * QUARTER, "gpsimd")
             for q in range(4):

@@ -300,26 +300,26 @@ def tile_net_pa_w4_kernel(tc, A_bytes, A_scale, features, Wg_words, Wg_scales, b
                 nc.scalar.activation(out=rows[:], in_=summed[n, h][:], func=ACT.Relu)
             store(n, h, rows)
 
-        def project_turned(n):
-            relu_turned[n] = ring("reluturned", n, 3, [P, 4, 2 * P], F32)
-            for half in range(2):
-                bank = next_bank([P, 2, 2 * P], F32)
-                for cl in range(2):
-                    c = 2 * half + cl
-                    nc.tensor.matmul_mx(
-                        out=bank[:, cl, :],
-                        lhsT=w_words[:, 2 * c * P : 2 * (c + 1) * P].bitcast(FP4X4),
-                        lhsT_scale=w_scales[:, c * P : (c + 1) * P],
-                        rhs=agg_codes[n][:].bitcast(FP8X4),
-                        rhs_scale=agg_scales[n][:],
-                        start=True,
-                        stop=True,
-                    )
-                for cl in range(2):
-                    c = 2 * half + cl
-                    nc.scalar.activation(
-                        out=relu_turned[n][:, c, :], in_=bank[:, cl, :], func=ACT.Relu, bias=bias_chunks[:, c : c + 1]
-                    )
+        def project_turned(n, half):
+            if half == 0:
+                relu_turned[n] = ring("reluturned", n, 3, [P, 4, 2 * P], F32)
+            bank = next_bank([P, 2, 2 * P], F32)
+            for cl in range(2):
+                c = 2 * half + cl
+                nc.tensor.matmul_mx(
+                    out=bank[:, cl, :],
+                    lhsT=w_words[:, 2 * c * P : 2 * (c + 1) * P].bitcast(FP4X4),
+                    lhsT_scale=w_scales[:, c * P : (c + 1) * P],
+                    rhs=agg_codes[n][:].bitcast(FP8X4),
+                    rhs_scale=agg_scales[n][:],
+                    start=True,
+                    stop=True,
+                )
+            for cl in range(2):
+                c = 2 * half + cl
+                nc.scalar.activation(
+                    out=relu_turned[n][:, c, :], in_=bank[:, cl, :], func=ACT.Relu, bias=bias_chunks[:, c : c + 1]
+                )
 
         def turn_back_store(n, h, engine="scalar"):
             bank = next_bank([P, 4, P], F32)
@@ -388,24 +388,31 @@ def tile_net_pa_w4_kernel(tc, A_bytes, A_scale, features, Wg_words, Wg_scales, b
             widen(n + 1, share, quarters * QUARTER, "gpsimd")
             for q in range(4):
                 scale_turned(n, q)
-            if n == 2:
-                scale_early(early_values, 3, 5)
-                bank_names.append(early_bank)
             aggregate_pair(n - 1, (0, 3, 2, 1) if n == 1 else range(PASSES))
-            if n >= 2:
-                project_turned(n - 2)
+            if n == 2:
+                scale_early(early_values, 4, 4)
+                bank_names.append(early_bank)
+            if n == last - 1:
+                project_turned(n - 2, 0)
+                project_turned(n - 2, 1)
             turn(n + 1, 0)
             if n == 1:
                 bias_to_partitions()
                 early_bank, early_values = turn_early()
-                scale_early(early_values, 0, 3)
+                scale_early(early_values, 0, 4)
             if n == 3:
                 group_early()
             if n >= 3:
                 turn_back_store(n - 3, 0)
                 turn_back_store(n - 3, 1)
-            for q in range(1, quarters):
-                turn(n + 1, q)
+            if 2 <= n < last - 1:
+                project_turned(n - 2, 0)
+            turn(n + 1, 1)
+            turn(n + 1, 2)
+            if 2 <= n < last - 1:
+                project_turned(n - 2, 1)
+            if quarters == 4:
+                turn(n + 1, 3)
 
         b0, b1, b2, b3 = bank_names
         bank_names.clear()
@@ -419,7 +426,8 @@ def tile_net_pa_w4_kernel(tc, A_bytes, A_scale, features, Wg_words, Wg_scales, b
         quantize_early()
         quantize_rows(last, 0, 4)
         scale_turned(last, 2)
-        project_turned(last - 2)
+        project_turned(last - 2, 0)
+        project_turned(last - 2, 1)
         aggregate_pair(last - 1)
         turn_back_store(last - 2, 0)
         turn_back_store(last - 2, 1)

@@ -85,15 +85,16 @@ def tile_net_pa_w4_kernel(tc, A_bytes, A_scale, features, Wg_words, Wg_scales, b
                     in_=Wg_scales.rearrange("g q n -> (g q) n")[4 * q : 4 * q + 4, :].bitcast(I32),
                 )
 
-        def spread_bias():
-            bank = next_bank([P, 4, P], F32)
-            for t in range(4):
-                nc.tensor.transpose(bank[:, t, :], bias_cols[:, t : t + 1].to_broadcast([P, P]), ident[:])
-            nc.scalar.copy(out=bias_row[:].rearrange("p (n t) -> p n t", t=4), in_=bank[:].rearrange("p t n -> p n t"))
+        def spread_bias(bank, slots):
+            for t in slots:
+                column = bias_cols[:, t : t + 1].to_broadcast([P, P])
+                nc.tensor.matmul(bank[:, t, :], lhsT=column, rhs=ident[:], start=True, stop=True)
 
         def bias_to_partitions():
             bank = next_bank([P, 4, P], F32)
-            for c in range(4):
+            for c in range(2):
+                nc.tensor.matmul(bank[:, c, :], lhsT=bias_row[:, c * P : (c + 1) * P], rhs=ident[:], start=True, stop=True)
+            for c in range(2, 4):
                 nc.tensor.transpose(bank[:, c, :], bias_row[:, c * P : (c + 1) * P], ident[:])
             nc.scalar.copy(out=bias_chunks[:].rearrange("p (c o) -> p c o", o=1), in_=bank[:, :, 0:1])
 
@@ -132,7 +133,7 @@ def tile_net_pa_w4_kernel(tc, A_bytes, A_scale, features, Wg_words, Wg_scales, b
 
         wide, grouped, a_codes, a_scales, turned_rows = {}, {}, {}, {}, {}
         agg_bf, agg_codes, agg_scales = {}, {}, {}
-        product, relu_turned, summed = {}, {}, {}
+        product, relu_turned, summed, back = {}, {}, {}, {}
 
         def widen(n, first, last, engine):
             if n not in wide:
@@ -214,9 +215,11 @@ def tile_net_pa_w4_kernel(tc, A_bytes, A_scale, features, Wg_words, Wg_scales, b
                 in_=grouped[n][:, part].rearrange("p g i t -> p (g i t)"),
             )
 
-        def aggregate(n, h, order=range(PASSES)):
+        def aggregate(n, h, order=range(PASSES), midway=None):
             bank = next_bank([P, 4, P], F32)
             for g in order:
+                if midway and g == order[2]:
+                    midway()
                 early = h == 1 and g >= 2
                 codes = early_codes[:, g - 2, :] if early else a_codes[n][:, PASSES * h + g, :]
                 scales = early_scales[:, g - 2, :] if early else a_scales[n][:, PASSES * h + g, :]
@@ -241,11 +244,7 @@ def tile_net_pa_w4_kernel(tc, A_bytes, A_scale, features, Wg_words, Wg_scales, b
             agg_codes[n] = ring("aggcodes", n, 3, [P, 2 * P], U32)
             agg_scales[n] = ring("aggscales", n, 3, [P, 2 * P], U8)
             banks = [next_bank([P, 2, 2 * P], F32) for half in range(2)]
-            if n == 0:
-                steps = [(half, g) for g in order for half in range(2)]
-            else:
-                steps = [(half, g) for half in range(2) for g in order]
-            for half, g in steps:
+            for half, g in [(half, g) for half in range(2) for g in order]:
                 for tl in range(2):
                     t = 2 * half + tl
                     nc.tensor.matmul_mx(
@@ -321,16 +320,19 @@ def tile_net_pa_w4_kernel(tc, A_bytes, A_scale, features, Wg_words, Wg_scales, b
                     out=relu_turned[n][:, c, :], in_=bank[:, cl, :], func=ACT.Relu, bias=bias_chunks[:, c : c + 1]
                 )
 
-        def turn_back_store(n, h, engine="scalar"):
-            bank = next_bank([P, 4, P], F32)
+        def turn_back(n, h):
+            back[n, h] = next_bank([P, 4, P], F32)
             for c in range(4):
-                nc.tensor.transpose(bank[:, c, :], relu_turned[n][:, c, h * P : (h + 1) * P], ident[:])
+                nc.tensor.transpose(back[n, h][:, c, :], relu_turned[n][:, c, h * P : (h + 1) * P], ident[:])
+
+        def store_back(n, h):
             rows = ring("rows", 2 * n + h, 8, [P, D], F32)
-            if engine == "vector":
-                nc.vector.tensor_copy(out=rows[:], in_=bank[:].rearrange("p c n -> p (c n)"))
-            else:
-                nc.scalar.copy(out=rows[:], in_=bank[:].rearrange("p c n -> p (c n)"))
+            nc.scalar.copy(out=rows[:], in_=back[n, h][:].rearrange("p c n -> p (c n)"))
             store(n, h, rows)
+
+        def turn_back_store(n, h):
+            turn_back(n, h)
+            store_back(n, h)
 
         make_identity(nc, ident[:])
         nc.vector.memset(w_scales[:].bitcast(I32), 0)
@@ -342,10 +344,10 @@ def tile_net_pa_w4_kernel(tc, A_bytes, A_scale, features, Wg_words, Wg_scales, b
         load_f(0)
         load_pair(1)
         load_f(2)
-        load_f(3)
-        nc.sync.dma_start(out=bias_raw[:], in_=bg.rearrange("(p t) -> p t", t=4))
         load_f(1)
+        load_f(3)
         nc.sync.dma_start(out=early_bytes[:], in_=A_bytes[NODES - P :, NODES - QUARTER :])
+        nc.sync.dma_start(out=bias_raw[:], in_=bg.rearrange("(p t) -> p t", t=4))
         load_pair(2)
         load_pair(3)
         load_w()
@@ -365,15 +367,18 @@ def tile_net_pa_w4_kernel(tc, A_bytes, A_scale, features, Wg_words, Wg_scales, b
         for q in range(4):
             scale_turned(0, q)
         group_features(2)
+        nc.scalar.copy(out=early_wide[:], in_=early_bytes[:].bitcast(FP8))
         nc.scalar.copy(out=bias_cols[:], in_=bias_raw[:])
-        group_features_by_copy(1)
-        for q in range(4):
-            turn(1, q)
+        group_features(1)
+        turn(1, 0)
+        turn(1, 1)
+        bias_bank = next_bank([P, 4, P], F32)
+        spread_bias(bias_bank, (0, 1))
+        turn(1, 2)
+        turn(1, 3)
         group_features_on_vector(3)
         for g in (0, 3, 2):
             quantize_features(g)
-        nc.scalar.copy(out=early_wide[:], in_=early_bytes[:].bitcast(FP8))
-        spread_bias()
 
         last = PAIRS - 1
         for n in range(1, last):
@@ -389,22 +394,32 @@ def tile_net_pa_w4_kernel(tc, A_bytes, A_scale, features, Wg_words, Wg_scales, b
             for q in range(4):
                 scale_turned(n, q)
             aggregate_pair(n - 1, (0, 3, 2, 1) if n == 1 else range(PASSES))
+            if n == 1:
+                early_bank, early_values = turn_early()
+                scale_early(early_values, 0, 4)
             if n == 2:
                 scale_early(early_values, 4, 4)
                 bank_names.append(early_bank)
             if n == last - 1:
                 project_turned(n - 2, 0)
-                project_turned(n - 2, 1)
             turn(n + 1, 0)
             if n == 1:
+                spread_bias(bias_bank, (2, 3))
+                nc.scalar.copy(
+                    out=bias_row[:].rearrange("p (n t) -> p n t", t=4), in_=bias_bank[:].rearrange("p t n -> p n t")
+                )
+            if n == 2:
                 bias_to_partitions()
-                early_bank, early_values = turn_early()
-                scale_early(early_values, 0, 4)
             if n == 3:
                 group_early()
             if n >= 3:
-                turn_back_store(n - 3, 0)
-                turn_back_store(n - 3, 1)
+                turn_back(n - 3, 0)
+                turn_back(n - 3, 1)
+            if n == last - 1:
+                project_turned(n - 2, 1)
+            if n >= 3:
+                store_back(n - 3, 0)
+                store_back(n - 3, 1)
             if 2 <= n < last - 1:
                 project_turned(n - 2, 0)
             turn(n + 1, 1)
@@ -416,9 +431,7 @@ def tile_net_pa_w4_kernel(tc, A_bytes, A_scale, features, Wg_words, Wg_scales, b
 
         b0, b1, b2, b3 = bank_names
         bank_names.clear()
-        bank_names.extend([b0, b1, "turn3", b2, b3, b0, b1, "turn0", "turn1", "turn3", b2, b3, b0, b1])
-        turn_back_store(last - 3, 0)
-        turn_back_store(last - 3, 1)
+        bank_names.extend(["turn3", b0, b3, b1, b2, "turn0", "turn3", b1, "turn1", b0, b3, b2, "turn0", "turn2"])
         quantize_agg(last - 2)
         quantize_rows(last - 1)
         scale_turned(last, 0)
@@ -426,16 +439,19 @@ def tile_net_pa_w4_kernel(tc, A_bytes, A_scale, features, Wg_words, Wg_scales, b
         quantize_early()
         quantize_rows(last, 0, 4)
         scale_turned(last, 2)
+        quantize_rows(last, 4, 2)
         project_turned(last - 2, 0)
+        turn_back(last - 3, 0)
+        turn_back(last - 3, 1)
         project_turned(last - 2, 1)
+        store_back(last - 3, 0)
+        store_back(last - 3, 1)
         aggregate_pair(last - 1)
         turn_back_store(last - 2, 0)
         turn_back_store(last - 2, 1)
         quantize_agg(last - 1)
-        quantize_rows(last, 4, 2)
         aggregate(last, 0)
-        project(last - 1, 0)
-        aggregate(last, 1, (2, 3, 0, 1))
+        aggregate(last, 1, (2, 3, 0, 1), lambda: project(last - 1, 0))
         project(last - 1, 1)
         add_bias(last - 1, 0)
         quantize_agg(last, 0, 1)

@@ -20,6 +20,7 @@ P = 128
 PASSES = NODES // 512
 PAIRS = NODES // (2 * P)
 QUARTER = 1024
+SCALAR_COLUMNS = 1536
 FLOPS = 2 * NODES * NODES * D + 2 * NODES * D * D
 
 
@@ -37,9 +38,8 @@ def tile_net_pa_w4_kernel(tc, A_bytes, A_scale, features, Wg_words, Wg_scales, b
         bias_row = keep.tile([P, D], F32, name="biasrow", align_bytes=64)
         bias_chunks = keep.tile([P, 4], F32, name="biaschunks")
         f_raw = [keep.tile([P, 4, D], BF16, name="fraw%d" % g, align_bytes=64) for g in range(PASSES)]
-        f_grouped = [
-            keep.tile([P, 4, P, 4], BF16, name="afterfeatures" if g == 1 else "fgrouped%d" % g, align_bytes=64) for g in range(PASSES)
-        ]
+        f_names = ["fgrouped0", "fgrouped1", "fgrouped2", "afterfeatures"]
+        f_grouped = [keep.tile([P, 4, P, 4], BF16, name=name, align_bytes=64) for name in f_names]
         f_codes = [keep.tile([P, D], U32, name="fcodes%d" % g, align_bytes=64) for g in range(PASSES)]
         f_scales = [keep.tile([P, D], U8, name="fscales%d" % g, align_bytes=64) for g in range(PASSES)]
         w_words = keep.tile([P, 2 * D], U8, name="wwords", align_bytes=64)
@@ -92,9 +92,7 @@ def tile_net_pa_w4_kernel(tc, A_bytes, A_scale, features, Wg_words, Wg_scales, b
 
         def bias_to_partitions():
             bank = next_bank([P, 4, P], F32)
-            for c in range(2):
-                nc.tensor.matmul(bank[:, c, :], lhsT=bias_row[:, c * P : (c + 1) * P], rhs=ident[:], start=True, stop=True)
-            for c in range(2, 4):
+            for c in range(4):
                 nc.tensor.transpose(bank[:, c, :], bias_row[:, c * P : (c + 1) * P], ident[:])
             nc.scalar.copy(out=bias_chunks[:].rearrange("p (c o) -> p c o", o=1), in_=bank[:, :, 0:1])
 
@@ -160,6 +158,7 @@ def tile_net_pa_w4_kernel(tc, A_bytes, A_scale, features, Wg_words, Wg_scales, b
             if q == 0:
                 grouped[n] = ring("stage", n + 2, 3, [P, 2 * PASSES, P, 4], BF16)
             passes = slice(2 * (q % 2), 2 * (q % 2) + 2)
+            scales = scale_cols[:, passes, :].rearrange("p g (u e) -> p g u e", u=2)
             if n == PAIRS - 1:
                 dst = grouped[n][:, 2 * q : 2 * q + 2]
             else:
@@ -167,7 +166,7 @@ def tile_net_pa_w4_kernel(tc, A_bytes, A_scale, features, Wg_words, Wg_scales, b
             nc.vector.tensor_tensor(
                 out=dst.rearrange("p g i (u e) -> p g i u e", u=2),
                 in0=turned_rows[n, q][:].bitcast(BF16).rearrange("p u g (i e) -> p g i u e", e=2),
-                in1=scale_cols[:, passes, :].rearrange("p g (u e) -> p g u e", u=2).unsqueeze(2).to_broadcast([P, 2, P, 2, 2]),
+                in1=scales.unsqueeze(2).to_broadcast([P, 2, P, 2, 2]),
                 op=ALU.mult,
             )
 
@@ -341,13 +340,13 @@ def tile_net_pa_w4_kernel(tc, A_bytes, A_scale, features, Wg_words, Wg_scales, b
         load_a(0, 0)
         nc.sync.dma_start(out=scale_cols[:], in_=A_scale.rearrange("o (g p t) -> p (o g) t", p=P, t=4))
         load_a(0, 1)
-        load_f(0)
         load_pair(1)
+        load_f(0)
         load_f(2)
         load_f(1)
         load_f(3)
-        nc.sync.dma_start(out=early_bytes[:], in_=A_bytes[NODES - P :, NODES - QUARTER :])
         nc.sync.dma_start(out=bias_raw[:], in_=bg.rearrange("(p t) -> p t", t=4))
+        nc.sync.dma_start(out=early_bytes[:], in_=A_bytes[NODES - P :, NODES - QUARTER :])
         load_pair(2)
         load_pair(3)
         load_w()
@@ -361,39 +360,40 @@ def tile_net_pa_w4_kernel(tc, A_bytes, A_scale, features, Wg_words, Wg_scales, b
         widen(0, 3 * QUARTER, 4 * QUARTER, "scalar")
         for q in range(4):
             turn(0, q)
+        widen(1, 0, SCALAR_COLUMNS, "scalar")
+        widen(1, SCALAR_COLUMNS, 4 * QUARTER, "gpsimd")
         group_features_by_copy(0)
-        widen(1, 0, 1792, "scalar")
-        widen(1, 1792, 4 * QUARTER, "gpsimd")
         for q in range(4):
             scale_turned(0, q)
         group_features(2)
-        nc.scalar.copy(out=early_wide[:], in_=early_bytes[:].bitcast(FP8))
-        nc.scalar.copy(out=bias_cols[:], in_=bias_raw[:])
         group_features(1)
+        nc.scalar.copy(out=bias_cols[:], in_=bias_raw[:])
+        nc.scalar.copy(out=early_wide[:], in_=early_bytes[:].bitcast(FP8))
         turn(1, 0)
         turn(1, 1)
         bias_bank = next_bank([P, 4, P], F32)
         spread_bias(bias_bank, (0, 1))
         turn(1, 2)
         turn(1, 3)
+        quantize_features(0)
+        quantize_rows(0)
+        quantize_features(2)
         group_features_on_vector(3)
-        for g in (0, 3, 2):
-            quantize_features(g)
+        quantize_features(1)
+        quantize_features(3)
 
         last = PAIRS - 1
         for n in range(1, last):
             if n >= 2:
                 quantize_agg(n - 2)
-            quantize_rows(n - 1)
-            if n == 1:
-                quantize_features(1)
+                quantize_rows(n - 1)
             quarters = 3 if n + 1 == last else 4
-            share = QUARTER if n + 1 == last else 1536
+            share = QUARTER if n + 1 == last else SCALAR_COLUMNS
             widen(n + 1, 0, share, "scalar")
             widen(n + 1, share, quarters * QUARTER, "gpsimd")
             for q in range(4):
                 scale_turned(n, q)
-            aggregate_pair(n - 1, (0, 3, 2, 1) if n == 1 else range(PASSES))
+            aggregate_pair(n - 1, (0, 2, 1, 3) if n == 1 else range(PASSES))
             if n == 1:
                 early_bank, early_values = turn_early()
                 scale_early(early_values, 0, 4)

@@ -21,6 +21,7 @@ PASSES = NODES // 512
 PAIRS = NODES // (2 * P)
 QUARTER = 1024
 SCALAR_COLUMNS = 1536
+FIRST_SCALAR_COLUMNS = 1792
 FLOPS = 2 * NODES * NODES * D + 2 * NODES * D * D
 
 
@@ -38,7 +39,7 @@ def tile_net_pa_w4_kernel(tc, A_bytes, A_scale, features, Wg_words, Wg_scales, b
         bias_row = keep.tile([P, D], F32, name="biasrow", align_bytes=64)
         bias_chunks = keep.tile([P, 4], F32, name="biaschunks")
         f_raw = [keep.tile([P, 4, D], BF16, name="fraw%d" % g, align_bytes=64) for g in range(PASSES)]
-        f_names = ["fgrouped0", "fgrouped1", "fgrouped2", "afterfeatures"]
+        f_names = ["fgrouped0", "fgrouped1", "afterfeatures", "fgrouped3"]
         f_grouped = [keep.tile([P, 4, P, 4], BF16, name=name, align_bytes=64) for name in f_names]
         f_codes = [keep.tile([P, D], U32, name="fcodes%d" % g, align_bytes=64) for g in range(PASSES)]
         f_scales = [keep.tile([P, D], U8, name="fscales%d" % g, align_bytes=64) for g in range(PASSES)]
@@ -85,14 +86,18 @@ def tile_net_pa_w4_kernel(tc, A_bytes, A_scale, features, Wg_words, Wg_scales, b
                     in_=Wg_scales.rearrange("g q n -> (g q) n")[4 * q : 4 * q + 4, :].bitcast(I32),
                 )
 
-        def spread_bias(bank, slots):
-            for t in slots:
+        def spread_bias():
+            bank = next_bank([P, 4, P], F32)
+            for t in range(4):
                 column = bias_cols[:, t : t + 1].to_broadcast([P, P])
                 nc.tensor.matmul(bank[:, t, :], lhsT=column, rhs=ident[:], start=True, stop=True)
+            nc.scalar.copy(out=bias_row[:].rearrange("p (n t) -> p n t", t=4), in_=bank[:].rearrange("p t n -> p n t"))
 
         def bias_to_partitions():
             bank = next_bank([P, 4, P], F32)
-            for c in range(4):
+            for c in range(2):
+                nc.tensor.matmul(bank[:, c, :], lhsT=bias_row[:, c * P : (c + 1) * P], rhs=ident[:], start=True, stop=True)
+            for c in range(2, 4):
                 nc.tensor.transpose(bank[:, c, :], bias_row[:, c * P : (c + 1) * P], ident[:])
             nc.scalar.copy(out=bias_chunks[:].rearrange("p (c o) -> p c o", o=1), in_=bank[:, :, 0:1])
 
@@ -131,7 +136,7 @@ def tile_net_pa_w4_kernel(tc, A_bytes, A_scale, features, Wg_words, Wg_scales, b
 
         wide, grouped, a_codes, a_scales, turned_rows = {}, {}, {}, {}, {}
         agg_bf, agg_codes, agg_scales = {}, {}, {}
-        product, relu_turned, summed, back = {}, {}, {}, {}
+        product, relu_turned, summed = {}, {}, {}
 
         def widen(n, first, last, engine):
             if n not in wide:
@@ -214,11 +219,9 @@ def tile_net_pa_w4_kernel(tc, A_bytes, A_scale, features, Wg_words, Wg_scales, b
                 in_=grouped[n][:, part].rearrange("p g i t -> p (g i t)"),
             )
 
-        def aggregate(n, h, order=range(PASSES), midway=None):
+        def aggregate(n, h, order=range(PASSES)):
             bank = next_bank([P, 4, P], F32)
             for g in order:
-                if midway and g == order[2]:
-                    midway()
                 early = h == 1 and g >= 2
                 codes = early_codes[:, g - 2, :] if early else a_codes[n][:, PASSES * h + g, :]
                 scales = early_scales[:, g - 2, :] if early else a_scales[n][:, PASSES * h + g, :]
@@ -243,7 +246,10 @@ def tile_net_pa_w4_kernel(tc, A_bytes, A_scale, features, Wg_words, Wg_scales, b
             agg_codes[n] = ring("aggcodes", n, 3, [P, 2 * P], U32)
             agg_scales[n] = ring("aggscales", n, 3, [P, 2 * P], U8)
             banks = [next_bank([P, 2, 2 * P], F32) for half in range(2)]
-            for half, g in [(half, g) for half in range(2) for g in order]:
+            steps = [(half, g) for half in range(2) for g in order]
+            if n == 0:
+                steps = [(half, g) for g in order for half in range(2)]
+            for half, g in steps:
                 for tl in range(2):
                     t = 2 * half + tl
                     nc.tensor.matmul_mx(
@@ -319,19 +325,13 @@ def tile_net_pa_w4_kernel(tc, A_bytes, A_scale, features, Wg_words, Wg_scales, b
                     out=relu_turned[n][:, c, :], in_=bank[:, cl, :], func=ACT.Relu, bias=bias_chunks[:, c : c + 1]
                 )
 
-        def turn_back(n, h):
-            back[n, h] = next_bank([P, 4, P], F32)
-            for c in range(4):
-                nc.tensor.transpose(back[n, h][:, c, :], relu_turned[n][:, c, h * P : (h + 1) * P], ident[:])
-
-        def store_back(n, h):
-            rows = ring("rows", 2 * n + h, 8, [P, D], F32)
-            nc.scalar.copy(out=rows[:], in_=back[n, h][:].rearrange("p c n -> p (c n)"))
-            store(n, h, rows)
-
         def turn_back_store(n, h):
-            turn_back(n, h)
-            store_back(n, h)
+            bank = next_bank([P, 4, P], F32)
+            for c in range(4):
+                nc.tensor.transpose(bank[:, c, :], relu_turned[n][:, c, h * P : (h + 1) * P], ident[:])
+            rows = ring("rows", 2 * n + h, 8, [P, D], F32)
+            nc.scalar.copy(out=rows[:], in_=bank[:].rearrange("p c n -> p (c n)"))
+            store(n, h, rows)
 
         make_identity(nc, ident[:])
         nc.vector.memset(w_scales[:].bitcast(I32), 0)
@@ -340,8 +340,8 @@ def tile_net_pa_w4_kernel(tc, A_bytes, A_scale, features, Wg_words, Wg_scales, b
         load_a(0, 0)
         nc.sync.dma_start(out=scale_cols[:], in_=A_scale.rearrange("o (g p t) -> p (o g) t", p=P, t=4))
         load_a(0, 1)
-        load_pair(1)
         load_f(0)
+        load_pair(1)
         load_f(2)
         load_f(1)
         load_f(3)
@@ -360,27 +360,22 @@ def tile_net_pa_w4_kernel(tc, A_bytes, A_scale, features, Wg_words, Wg_scales, b
         widen(0, 3 * QUARTER, 4 * QUARTER, "scalar")
         for q in range(4):
             turn(0, q)
-        widen(1, 0, SCALAR_COLUMNS, "scalar")
-        widen(1, SCALAR_COLUMNS, 4 * QUARTER, "gpsimd")
         group_features_by_copy(0)
+        widen(1, 0, FIRST_SCALAR_COLUMNS, "scalar")
+        widen(1, FIRST_SCALAR_COLUMNS, 4 * QUARTER, "gpsimd")
         for q in range(4):
             scale_turned(0, q)
-        group_features(2)
-        group_features(1)
+        group_features_by_copy(1)
         nc.scalar.copy(out=bias_cols[:], in_=bias_raw[:])
-        nc.scalar.copy(out=early_wide[:], in_=early_bytes[:].bitcast(FP8))
-        turn(1, 0)
-        turn(1, 1)
-        bias_bank = next_bank([P, 4, P], F32)
-        spread_bias(bias_bank, (0, 1))
-        turn(1, 2)
-        turn(1, 3)
+        group_features(2)
+        for q in range(4):
+            turn(1, q)
         quantize_features(0)
-        quantize_rows(0)
-        quantize_features(2)
         group_features_on_vector(3)
-        quantize_features(1)
-        quantize_features(3)
+        quantize_rows(0)
+        for g in (3, 1, 2):
+            quantize_features(g)
+        nc.scalar.copy(out=early_wide[:], in_=early_bytes[:].bitcast(FP8))
 
         last = PAIRS - 1
         for n in range(1, last):
@@ -393,7 +388,7 @@ def tile_net_pa_w4_kernel(tc, A_bytes, A_scale, features, Wg_words, Wg_scales, b
             widen(n + 1, share, quarters * QUARTER, "gpsimd")
             for q in range(4):
                 scale_turned(n, q)
-            aggregate_pair(n - 1, (0, 2, 1, 3) if n == 1 else range(PASSES))
+            aggregate_pair(n - 1, (0, 3, 1, 2) if n == 1 else range(PASSES))
             if n == 1:
                 early_bank, early_values = turn_early()
                 scale_early(early_values, 0, 4)
@@ -404,22 +399,16 @@ def tile_net_pa_w4_kernel(tc, A_bytes, A_scale, features, Wg_words, Wg_scales, b
                 project_turned(n - 2, 0)
             turn(n + 1, 0)
             if n == 1:
-                spread_bias(bias_bank, (2, 3))
-                nc.scalar.copy(
-                    out=bias_row[:].rearrange("p (n t) -> p n t", t=4), in_=bias_bank[:].rearrange("p t n -> p n t")
-                )
+                spread_bias()
             if n == 2:
                 bias_to_partitions()
-            if n == 3:
+            if n == 5:
                 group_early()
-            if n >= 3:
-                turn_back(n - 3, 0)
-                turn_back(n - 3, 1)
             if n == last - 1:
                 project_turned(n - 2, 1)
             if n >= 3:
-                store_back(n - 3, 0)
-                store_back(n - 3, 1)
+                turn_back_store(n - 3, 0)
+                turn_back_store(n - 3, 1)
             if 2 <= n < last - 1:
                 project_turned(n - 2, 0)
             turn(n + 1, 1)
@@ -431,7 +420,7 @@ def tile_net_pa_w4_kernel(tc, A_bytes, A_scale, features, Wg_words, Wg_scales, b
 
         b0, b1, b2, b3 = bank_names
         bank_names.clear()
-        bank_names.extend(["turn3", b0, b3, b1, b2, "turn0", "turn3", b1, "turn1", b0, b3, b2, "turn0", "turn2"])
+        bank_names.extend(["turn3", b0, b1, b2, b3, "turn0", "turn3", b2, "turn1", b0, b1, b3, "turn0", "turn2"])
         quantize_agg(last - 2)
         quantize_rows(last - 1)
         scale_turned(last, 0)
@@ -439,19 +428,18 @@ def tile_net_pa_w4_kernel(tc, A_bytes, A_scale, features, Wg_words, Wg_scales, b
         quantize_early()
         quantize_rows(last, 0, 4)
         scale_turned(last, 2)
-        quantize_rows(last, 4, 2)
         project_turned(last - 2, 0)
-        turn_back(last - 3, 0)
-        turn_back(last - 3, 1)
+        turn_back_store(last - 3, 0)
+        turn_back_store(last - 3, 1)
         project_turned(last - 2, 1)
-        store_back(last - 3, 0)
-        store_back(last - 3, 1)
         aggregate_pair(last - 1)
         turn_back_store(last - 2, 0)
         turn_back_store(last - 2, 1)
         quantize_agg(last - 1)
+        quantize_rows(last, 4, 2)
         aggregate(last, 0)
-        aggregate(last, 1, (2, 3, 0, 1), lambda: project(last - 1, 0))
+        project(last - 1, 0)
+        aggregate(last, 1, (2, 3, 0, 1))
         project(last - 1, 1)
         add_bias(last - 1, 0)
         quantize_agg(last, 0, 1)

@@ -22,6 +22,7 @@ PAIRS = NODES // (2 * P)
 QUARTER = 1024
 SCALAR_COLUMNS = 1536
 FIRST_SCALAR_COLUMNS = 1792
+GROUPING_PERIOD = 5
 FLOPS = 2 * NODES * NODES * D + 2 * NODES * D * D
 
 
@@ -45,12 +46,12 @@ def tile_net_pa_w4_kernel(tc, A_bytes, A_scale, features, Wg_words, Wg_scales, b
         f_scales = [keep.tile([P, D], U8, name="fscales%d" % g, align_bytes=64) for g in range(PASSES)]
         w_words = keep.tile([P, 2 * D], U8, name="wwords", align_bytes=64)
         w_scales = keep.tile([P, D], U8, name="wscales", align_bytes=64)
-        early_wide = keep.tile([P, QUARTER], BF16, name="earlywide", align_bytes=64)
-        early_planes = keep.tile([P, 2, 2, P, 2], BF16, name="earlyplanes", align_bytes=64)
-        early_grouped = keep.tile([P, 2, P, 4], BF16, name="earlygrouped", align_bytes=64)
-        early_codes = keep.tile([P, 2, P], U32, name="earlycodes", align_bytes=64)
-        early_scales = keep.tile([P, 2, P], U8, name="earlyscales", align_bytes=64)
-        early_bytes = keep.tile([P, QUARTER], U8, name="earlybytes", align_bytes=64)
+        early_wide = keep.tile([P, NODES], BF16, name="earlywide", align_bytes=64)
+        early_planes = keep.tile([P, PASSES, 2, P, 2], BF16, name="earlyplanes", align_bytes=64)
+        early_grouped = keep.tile([P, PASSES, P, 4], BF16, name="earlygrouped", align_bytes=64)
+        early_codes = keep.tile([P, PASSES, P], U32, name="earlycodes", align_bytes=64)
+        early_scales = keep.tile([P, PASSES, P], U8, name="earlyscales", align_bytes=64)
+        early_bytes = keep.tile([P, NODES], U8, name="earlybytes", align_bytes=64)
         ident = keep.tile([P, P], F32, name="ident", align_bytes=64)
         ident_bf = keep.tile([P, P], BF16, name="identbf", align_bytes=64)
 
@@ -96,7 +97,8 @@ def tile_net_pa_w4_kernel(tc, A_bytes, A_scale, features, Wg_words, Wg_scales, b
         def bias_to_partitions():
             bank = next_bank([P, 4, P], F32)
             for c in range(2):
-                nc.tensor.matmul(bank[:, c, :], lhsT=bias_row[:, c * P : (c + 1) * P], rhs=ident[:], start=True, stop=True)
+                chunk = bias_row[:, c * P : (c + 1) * P]
+                nc.tensor.matmul(bank[:, c, :], lhsT=chunk, rhs=ident[:], start=True, stop=True)
             for c in range(2, 4):
                 nc.tensor.transpose(bank[:, c, :], bias_row[:, c * P : (c + 1) * P], ident[:])
             nc.scalar.copy(out=bias_chunks[:].rearrange("p (c o) -> p c o", o=1), in_=bank[:, :, 0:1])
@@ -136,7 +138,7 @@ def tile_net_pa_w4_kernel(tc, A_bytes, A_scale, features, Wg_words, Wg_scales, b
 
         wide, grouped, a_codes, a_scales, turned_rows = {}, {}, {}, {}, {}
         agg_bf, agg_codes, agg_scales = {}, {}, {}
-        product, relu_turned, summed = {}, {}, {}
+        product, relu_turned, summed, back = {}, {}, {}, {}
 
         def widen(n, first, last, engine):
             if n not in wide:
@@ -175,30 +177,29 @@ def tile_net_pa_w4_kernel(tc, A_bytes, A_scale, features, Wg_words, Wg_scales, b
                 op=ALU.mult,
             )
 
-        def turn_early():
+        def turn_early(passes):
             words = early_wide[:].bitcast(F32)
             name = bank_names[0]
             bank_names.remove(name)
             bank = psum.tile([P, 2, 2, P], F32, name=name)
-            for gl in range(2):
+            for g in passes:
                 for u in range(2):
-                    nc.tensor.transpose(bank[:, u, gl, :], words[:, 256 * gl + u : 256 * (gl + 1) : 2], ident[:])
+                    nc.tensor.transpose(bank[:, u, g % 2, :], words[:, 256 * g + u : 256 * (g + 1) : 2], ident[:])
             return name, bank[:].bitcast(BF16).rearrange("p u g (i e) -> p u g i e", e=2)
 
-        def scale_early(values, first, count):
-            for plane in range(first, first + count):
-                gl, t = divmod(plane, 4)
+        def scale_early(values, g):
+            for t in range(4):
                 nc.scalar.activation(
-                    out=early_planes[:, gl, t // 2, :, t % 2],
-                    in_=values[:, t // 2, gl, :, t % 2],
+                    out=early_planes[:, g, t // 2, :, t % 2],
+                    in_=values[:, t // 2, g % 2, :, t % 2],
                     func=ACT.Copy,
-                    scale=scale_cols[:, 2 + gl, t : t + 1],
+                    scale=scale_cols[:, g, t : t + 1],
                 )
 
-        def group_early():
+        def group_early(first, count):
             nc.scalar.copy(
-                out=early_grouped[:].bitcast(F32),
-                in_=early_planes[:].rearrange("p g u i e -> p g u (i e)").bitcast(F32).rearrange("p g u i -> p g i u"),
+                out=early_grouped[:, first : first + count].bitcast(F32),
+                in_=early_planes[:, first : first + count].rearrange("p g u i e -> p g u (i e)").bitcast(F32).rearrange("p g u i -> p g i u"),
             )
 
         def quantize_early():
@@ -219,12 +220,11 @@ def tile_net_pa_w4_kernel(tc, A_bytes, A_scale, features, Wg_words, Wg_scales, b
                 in_=grouped[n][:, part].rearrange("p g i t -> p (g i t)"),
             )
 
-        def aggregate(n, h, order=range(PASSES)):
+        def aggregate(n, h):
             bank = next_bank([P, 4, P], F32)
-            for g in order:
-                early = h == 1 and g >= 2
-                codes = early_codes[:, g - 2, :] if early else a_codes[n][:, PASSES * h + g, :]
-                scales = early_scales[:, g - 2, :] if early else a_scales[n][:, PASSES * h + g, :]
+            for g in range(PASSES):
+                codes = early_codes[:, g, :] if h == 1 else a_codes[n][:, g, :]
+                scales = early_scales[:, g, :] if h == 1 else a_scales[n][:, g, :]
                 for t in range(4):
                     nc.tensor.matmul_mx(
                         out=bank[:, t, :],
@@ -232,10 +232,10 @@ def tile_net_pa_w4_kernel(tc, A_bytes, A_scale, features, Wg_words, Wg_scales, b
                         lhsT_scale=f_scales[g][:, t * P : (t + 1) * P],
                         rhs=codes.bitcast(FP8X4),
                         rhs_scale=scales,
-                        start=(g == order[0] and t == 0),
-                        stop=(g == order[-1] and t == 3),
+                        start=(g == 0 and t == 0),
+                        stop=(g == PASSES - 1 and t == 3),
                     )
-            if h == 0:
+            if h == 1:
                 agg_bf[n] = ring("aggbf", n, 3, [P, 2, P, 4], BF16)
                 agg_codes[n] = ring("aggcodes", n, 3, [P, 2 * P], U32)
                 agg_scales[n] = ring("aggscales", n, 3, [P, 2 * P], U8)
@@ -289,7 +289,7 @@ def tile_net_pa_w4_kernel(tc, A_bytes, A_scale, features, Wg_words, Wg_scales, b
             )
 
         def add_bias(n, h):
-            summed[n, h] = ring("summed", 2 * n + h, 4, [P, D], F32)
+            summed[n, h] = ring("summed", 2 * n + h, 6, [P, D], F32)
             nc.vector.tensor_tensor(out=summed[n, h][:], in0=product[n, h][:], in1=bias_row[:], op=ALU.add)
 
         def store(n, h, rows):
@@ -325,13 +325,19 @@ def tile_net_pa_w4_kernel(tc, A_bytes, A_scale, features, Wg_words, Wg_scales, b
                     out=relu_turned[n][:, c, :], in_=bank[:, cl, :], func=ACT.Relu, bias=bias_chunks[:, c : c + 1]
                 )
 
-        def turn_back_store(n, h):
-            bank = next_bank([P, 4, P], F32)
+        def turn_back(n, h):
+            back[n, h] = next_bank([P, 4, P], F32)
             for c in range(4):
-                nc.tensor.transpose(bank[:, c, :], relu_turned[n][:, c, h * P : (h + 1) * P], ident[:])
+                nc.tensor.transpose(back[n, h][:, c, :], relu_turned[n][:, c, h * P : (h + 1) * P], ident[:])
+
+        def store_back(n, h):
             rows = ring("rows", 2 * n + h, 8, [P, D], F32)
-            nc.scalar.copy(out=rows[:], in_=bank[:].rearrange("p c n -> p (c n)"))
+            nc.scalar.copy(out=rows[:], in_=back[n, h][:].rearrange("p c n -> p (c n)"))
             store(n, h, rows)
+
+        def turn_back_store(n, h):
+            turn_back(n, h)
+            store_back(n, h)
 
         make_identity(nc, ident[:])
         nc.vector.memset(w_scales[:].bitcast(I32), 0)
@@ -346,14 +352,13 @@ def tile_net_pa_w4_kernel(tc, A_bytes, A_scale, features, Wg_words, Wg_scales, b
         load_f(1)
         load_f(3)
         nc.sync.dma_start(out=bias_raw[:], in_=bg.rearrange("(p t) -> p t", t=4))
-        nc.sync.dma_start(out=early_bytes[:], in_=A_bytes[NODES - P :, NODES - QUARTER :])
+        nc.sync.dma_start(out=early_bytes[:], in_=A_bytes[NODES - P :, :])
         load_pair(2)
         load_pair(3)
         load_w()
         for n in range(4, PAIRS - 1):
             load_pair(n)
         load_a(PAIRS - 1, 0)
-        nc.sync.dma_start(out=a_bytes[PAIRS - 1][:, NODES : NODES + QUARTER], in_=A_bytes[NODES - P :, 0:QUARTER])
 
         for q in range(3):
             widen(0, q * QUARTER, (q + 1) * QUARTER, "vector")
@@ -378,78 +383,108 @@ def tile_net_pa_w4_kernel(tc, A_bytes, A_scale, features, Wg_words, Wg_scales, b
         nc.scalar.copy(out=early_wide[:], in_=early_bytes[:].bitcast(FP8))
 
         last = PAIRS - 1
-        for n in range(1, last):
+        for n in range(1, last - 1):
             if n >= 2:
                 quantize_agg(n - 2)
                 quantize_rows(n - 1)
-            quarters = 3 if n + 1 == last else 4
-            share = QUARTER if n + 1 == last else SCALAR_COLUMNS
-            widen(n + 1, 0, share, "scalar")
-            widen(n + 1, share, quarters * QUARTER, "gpsimd")
+            widen(n + 1, 0, SCALAR_COLUMNS, "scalar")
+            widen(n + 1, SCALAR_COLUMNS, 4 * QUARTER, "gpsimd")
             for q in range(4):
                 scale_turned(n, q)
             aggregate_pair(n - 1, (0, 3, 1, 2) if n == 1 else range(PASSES))
             if n == 1:
-                early_bank, early_values = turn_early()
-                scale_early(early_values, 0, 4)
+                first_bank, first_values = turn_early((0, 1))
+                scale_early(first_values, 0)
             if n == 2:
-                scale_early(early_values, 4, 4)
-                bank_names.append(early_bank)
-            if n == last - 1:
-                project_turned(n - 2, 0)
+                scale_early(first_values, 1)
+                bank_names.append(first_bank)
             turn(n + 1, 0)
             if n == 1:
                 spread_bias()
+                second_bank, second_values = turn_early((2,))
+                scale_early(second_values, 2)
+                bank_names.append(second_bank)
             if n == 2:
                 bias_to_partitions()
-            if n == 5:
-                group_early()
-            if n == last - 1:
-                project_turned(n - 2, 1)
             if n >= 3:
                 turn_back_store(n - 3, 0)
                 turn_back_store(n - 3, 1)
-            if 2 <= n < last - 1:
+            if n >= 2:
                 project_turned(n - 2, 0)
+            if n == GROUPING_PERIOD:
+                group_early(0, 3)
             turn(n + 1, 1)
             turn(n + 1, 2)
-            if 2 <= n < last - 1:
+            if n >= 2:
                 project_turned(n - 2, 1)
-            if quarters == 4:
-                turn(n + 1, 3)
+            turn(n + 1, 3)
 
-        b0, b1, b2, b3 = bank_names
+        third_bank, third_values = turn_early((3,))
+        quantize_agg(last - 3)
+        quantize_rows(last - 2)
+        widen(last, 0, NODES, "gpsimd")
+        scale_early(third_values, 3)
+        bank_names.append(third_bank)
+        for q in range(4):
+            scale_turned(last - 1, q)
+        aggregate_pair(last - 2)
+        group_early(3, 1)
+        project_turned(last - 3, 0)
+        turn_back_store(last - 4, 0)
+        turn_back(last - 4, 1)
+        turn(last, 0)
+        project_turned(last - 3, 1)
+        store_back(last - 4, 1)
+        turn(last, 1)
+
+        mid0, back0, back1, mid1 = bank_names
         bank_names.clear()
-        bank_names.extend(["turn3", b0, b1, b2, b3, "turn0", "turn3", b2, "turn1", b0, b1, b3, "turn0", "turn2"])
+        bank_names.extend(
+            [
+                "turn2",
+                "turn3",
+                mid0,
+                mid1,
+                back0,
+                back1,
+                "turn0",
+                "turn1",
+                mid0,
+                mid1,
+                back0,
+                "turn2",
+            ]
+        )
         quantize_agg(last - 2)
         quantize_rows(last - 1)
+        quantize_early()
         scale_turned(last, 0)
         scale_turned(last, 1)
-        quantize_early()
-        quantize_rows(last, 0, 4)
-        scale_turned(last, 2)
-        project_turned(last - 2, 0)
+        quantize_rows(last, 0, 2)
+        project(last - 2, 0)
+        project(last - 2, 1)
         turn_back_store(last - 3, 0)
         turn_back_store(last - 3, 1)
-        project_turned(last - 2, 1)
+        add_bias(last - 2, 0)
+        quantize_rows(last, 2, 2)
+        add_bias(last - 2, 1)
         aggregate_pair(last - 1)
-        turn_back_store(last - 2, 0)
-        turn_back_store(last - 2, 1)
+        relu_store(last - 2, 0)
+        aggregate(last, 1)
         quantize_agg(last - 1)
-        quantize_rows(last, 4, 2)
+        relu_store(last - 2, 1, "vector")
+        quantize_agg(last, 1, 1)
         aggregate(last, 0)
         project(last - 1, 0)
-        aggregate(last, 1, (2, 3, 0, 1))
         project(last - 1, 1)
+        project(last, 1)
         add_bias(last - 1, 0)
         quantize_agg(last, 0, 1)
         project(last, 0)
-        relu_store(last - 1, 0, "vector")
         add_bias(last - 1, 1)
-        quantize_agg(last, 1, 1)
-        project(last, 1)
+        relu_store(last - 1, 0)
+        add_bias(last, 1)
         relu_store(last - 1, 1)
         add_bias(last, 0)
-        add_bias(last, 1)
-        relu_store(last, 0)
-        relu_store(last, 1, "vector")
+        relu_store(last, 1)
+        relu_store(last, 0, "vector")

@@ -17,12 +17,16 @@ ACT = mybir.ActivationFunctionType
 NODES = 2048
 D = 512
 P = 128
-PASSES = NODES // 512
+PASS = 512
+PASSES = NODES // PASS
 PAIRS = NODES // (2 * P)
-QUARTER = 1024
-SCALAR_COLUMNS = 1536
-FIRST_SCALAR_COLUMNS = 1792
-GROUPING_PERIOD = 5
+LAST = PAIRS - 1
+TURN_BANKS = 4
+PARTED_TILES = 1
+FIRST_SHARE = 1280
+SHARE = 256
+SIDE_PERIOD = 6
+HALVED = 2
 FLOPS = 2 * NODES * NODES * D + 2 * NODES * D * D
 
 
@@ -35,40 +39,40 @@ def tile_net_pa_w4_kernel(tc, A_bytes, A_scale, features, Wg_words, Wg_scales, b
 
         a_bytes = [keep.tile([P, 2 * NODES], U8, name="abytes%d" % n, align_bytes=64) for n in range(PAIRS)]
         scale_cols = keep.tile([P, PASSES, 4], F32, name="scalecols")
-        bias_raw = keep.tile([P, 4], BF16, name="biasraw")
-        bias_cols = keep.tile([P, 4], F32, name="biascols")
-        bias_row = keep.tile([P, D], F32, name="biasrow", align_bytes=64)
+        ones = keep.tile([P, 1], F32, name="ones")
+        bias_row = keep.tile([P, D], BF16, name="biasrow", align_bytes=64)
         bias_chunks = keep.tile([P, 4], F32, name="biaschunks")
         f_raw = [keep.tile([P, 4, D], BF16, name="fraw%d" % g, align_bytes=64) for g in range(PASSES)]
-        f_names = ["fgrouped0", "fgrouped1", "afterfeatures", "fgrouped3"]
-        f_grouped = [keep.tile([P, 4, P, 4], BF16, name=name, align_bytes=64) for name in f_names]
         f_codes = [keep.tile([P, D], U32, name="fcodes%d" % g, align_bytes=64) for g in range(PASSES)]
         f_scales = [keep.tile([P, D], U8, name="fscales%d" % g, align_bytes=64) for g in range(PASSES)]
         w_words = keep.tile([P, 2 * D], U8, name="wwords", align_bytes=64)
         w_scales = keep.tile([P, D], U8, name="wscales", align_bytes=64)
-        early_wide = keep.tile([P, NODES], BF16, name="earlywide", align_bytes=64)
-        early_planes = keep.tile([P, PASSES, 2, P, 2], BF16, name="earlyplanes", align_bytes=64)
-        early_grouped = keep.tile([P, PASSES, P, 4], BF16, name="earlygrouped", align_bytes=64)
-        early_codes = keep.tile([P, PASSES, P], U32, name="earlycodes", align_bytes=64)
-        early_scales = keep.tile([P, PASSES, P], U8, name="earlyscales", align_bytes=64)
-        early_bytes = keep.tile([P, NODES], U8, name="earlybytes", align_bytes=64)
+        side_bytes = keep.tile([P, NODES], U8, name="sidebytes", align_bytes=64)
+        side_wide = keep.tile([P, NODES], BF16, name="sidewide", align_bytes=64)
+        side_planes = keep.tile([P, PASSES, 2, P, 2], BF16, name="sideplanes", align_bytes=64)
+        side_grouped = keep.tile([P, PASSES, P, 4], BF16, name="sidegrouped", align_bytes=64)
+        side_codes = keep.tile([P, PASSES, P], U32, name="sidecodes", align_bytes=64)
+        side_scales = keep.tile([P, PASSES, P], U8, name="sidescales", align_bytes=64)
         ident = keep.tile([P, P], F32, name="ident", align_bytes=64)
         ident_bf = keep.tile([P, P], BF16, name="identbf", align_bytes=64)
 
-        bank_names = ["other%d" % b for b in range(4)]
+        bank_names = ["other%d" % b for b in range(8 - TURN_BANKS)]
+        turn_names = ["turn%d" % b for b in range(TURN_BANKS)]
 
-        def next_bank(shape, dtype):
-            name = bank_names[0]
-            bank_names.remove(name)
-            bank_names.append(name)
+        def next_bank(shape, dtype, names=bank_names):
+            name = names[0]
+            names.remove(name)
+            names.append(name)
             return psum.tile(shape, dtype, name=name)
 
         def ring(name, index, depth, shape, dtype):
             return keep.tile(shape, dtype, name="%s%d" % (name, index % depth), align_bytes=64)
 
-        def load_a(n, h):
+        def load_a(n, h, first=0, last=NODES):
             r0 = (2 * n + h) * P
-            nc.sync.dma_start(out=a_bytes[n][:, h * NODES : (h + 1) * NODES], in_=A_bytes[r0 : r0 + P, :])
+            nc.sync.dma_start(
+                out=a_bytes[n][:, h * NODES + first : h * NODES + last], in_=A_bytes[r0 : r0 + P, first:last]
+            )
 
         def load_pair(n):
             nc.sync.dma_start(
@@ -87,35 +91,32 @@ def tile_net_pa_w4_kernel(tc, A_bytes, A_scale, features, Wg_words, Wg_scales, b
                     in_=Wg_scales.rearrange("g q n -> (g q) n")[4 * q : 4 * q + 4, :].bitcast(I32),
                 )
 
-        def spread_bias():
-            bank = next_bank([P, 4, P], F32)
-            for t in range(4):
-                column = bias_cols[:, t : t + 1].to_broadcast([P, P])
-                nc.tensor.matmul(bank[:, t, :], lhsT=column, rhs=ident[:], start=True, stop=True)
-            nc.scalar.copy(out=bias_row[:].rearrange("p (n t) -> p n t", t=4), in_=bank[:].rearrange("p t n -> p n t"))
-
         def bias_to_partitions():
-            bank = next_bank([P, 4, P], F32)
-            for c in range(2):
-                chunk = bias_row[:, c * P : (c + 1) * P]
-                nc.tensor.matmul(bank[:, c, :], lhsT=chunk, rhs=ident[:], start=True, stop=True)
-            for c in range(2, 4):
-                nc.tensor.transpose(bank[:, c, :], bias_row[:, c * P : (c + 1) * P], ident[:])
+            bank = next_bank([P, 4, P], BF16)
+            for c in range(4):
+                nc.tensor.transpose(bank[:, c, :], bias_row[:, c * P : (c + 1) * P], ident_bf[:])
             nc.scalar.copy(out=bias_chunks[:].rearrange("p (c o) -> p c o", o=1), in_=bank[:, :, 0:1])
 
-        def group_features(g):
+        f_grouped, f_banks = {}, {}
+
+        def features_tile(g, name):
+            f_grouped[g] = keep.tile([P, 4, P, 4], BF16, name=name, align_bytes=64)
+
+        def group_features_by_matmul(g, q):
+            half, ql = divmod(q, 2)
             src = f_raw[g][:].rearrange("p j (q c) -> p q c j", q=4)
-            for half in range(2):
-                bank = next_bank([P, 4, 64, 4], BF16)
-                for ql in range(2):
-                    nc.tensor.matmul(
-                        bank[:, :, 32 * ql : 32 * (ql + 1), :].rearrange("p t m j -> p m t j"),
-                        lhsT=ident_bf[:],
-                        rhs=src[:, 2 * half + ql].rearrange("p (m t) j -> p m t j", t=4),
-                        start=True,
-                        stop=True,
-                    )
-                nc.scalar.copy(out=f_grouped[g][:, :, 64 * half : 64 * (half + 1), :], in_=bank[:])
+            if ql == 0:
+                f_banks[g, half] = next_bank([P, 4, 64, 4], BF16)
+            nc.tensor.matmul(
+                f_banks[g, half][:, :, 32 * ql : 32 * (ql + 1), :].rearrange("p t m j -> p m t j"),
+                lhsT=ident_bf[:],
+                rhs=src[:, q].rearrange("p (m t) j -> p m t j", t=4),
+                start=True,
+                stop=True,
+            )
+
+        def copy_features(g, half):
+            nc.scalar.copy(out=f_grouped[g][:, :, 64 * half : 64 * (half + 1), :], in_=f_banks[g, half][:])
 
         def group_features_by_copy(g):
             nc.scalar.copy(
@@ -136,124 +137,156 @@ def tile_net_pa_w4_kernel(tc, A_bytes, A_scale, features, Wg_words, Wg_scales, b
                 in_=f_grouped[g][:].rearrange("p t m j -> p (t m j)"),
             )
 
-        wide, grouped, a_codes, a_scales, turned_rows = {}, {}, {}, {}, {}
-        agg_bf, agg_codes, agg_scales = {}, {}, {}
-        product, relu_turned, summed, back = {}, {}, {}, {}
+        wide, grouped, a_codes, a_scales, turned = {}, {}, {}, {}, {}
+        agg_banks, agg_bf, agg_codes, agg_scales = {}, {}, {}, {}
+        product, relu_turned, summed, back, side_banks = {}, {}, {}, {}, {}
+
+        def wide_tile(n):
+            if n not in wide:
+                name = "stage%d" % (n % 3)
+                wide[n] = keep.tile([P, 2 * NODES], BF16, name=name, align_bytes=64)
+            return wide[n]
 
         def widen(n, first, last, engine):
-            if n not in wide:
-                name = "afterfeatures" if n == 2 else "stage%d" % (n % 3)
-                wide[n] = keep.tile([P, 2 * NODES], BF16, name=name, align_bytes=64)
             src = a_bytes[n][:, first:last].bitcast(FP8)
             if engine == "scalar":
-                nc.scalar.copy(out=wide[n][:, first:last], in_=src)
+                nc.scalar.copy(out=wide_tile(n)[:, first:last], in_=src)
             elif engine == "vector":
-                nc.vector.tensor_copy(out=wide[n][:, first:last], in_=src)
+                nc.vector.tensor_copy(out=wide_tile(n)[:, first:last], in_=src)
             else:
-                nc.gpsimd.tensor_copy(out=wide[n][:, first:last], in_=src)
+                nc.gpsimd.tensor_copy(out=wide_tile(n)[:, first:last], in_=src)
 
-        def turn(n, q):
+        def widen_parted(g):
+            cols = slice(g * PASS, (g + 1) * PASS)
+            nc.vector.tensor_scalar(
+                out=wide_tile(0)[:, cols].rearrange("p (u q e) -> p q u e", u=2, e=2),
+                in0=a_bytes[0][:, cols].bitcast(FP8).rearrange("p (q u e) -> p q u e", u=2, e=2),
+                scalar1=ones[:],
+                scalar2=None,
+                op0=ALU.mult,
+            )
+
+        def word_columns(n, h, g, u):
             words = wide[n][:].bitcast(F32)
-            bank = psum.tile([P, 2, 2, P], F32, name="turn%d" % q)
-            turned_rows[n, q] = bank
-            for gl in range(2):
-                w0 = 256 * (2 * q + gl)
-                for u in range(2):
-                    nc.tensor.transpose(bank[:, u, gl, :], words[:, w0 + u : w0 + 256 : 2], ident[:])
+            w0 = 256 * (PASSES * h + g)
+            if n == 0 and h < PARTED_TILES:
+                return words[:, w0 + P * u : w0 + P * (u + 1)]
+            return words[:, w0 + u : w0 + 256 : 2]
 
-        def scale_turned(n, q):
-            if q == 0:
-                grouped[n] = ring("stage", n + 2, 3, [P, 2 * PASSES, P, 4], BF16)
-            passes = slice(2 * (q % 2), 2 * (q % 2) + 2)
+        def turn(n, h, first, count=2):
+            bank = next_bank([P, 2, count, P], F32, turn_names)
+            turned[n, h, first] = bank
+            for gl in range(count):
+                for u in range(2):
+                    nc.tensor.transpose(bank[:, u, gl, :], word_columns(n, h, first + gl, u), ident[:])
+
+        def grouped_tile(n, half):
+            key = (n, half if n < HALVED else 0)
+            if key not in grouped:
+                if n < HALVED:
+                    name = "stage%d" % ((n + 2) % 3) if half == 0 else "upper%d" % n
+                    grouped[key] = keep.tile([P, PASSES, P, 4], BF16, name=name, align_bytes=64)
+                else:
+                    grouped[key] = ring("grouped", n, 2, [P, 2 * PASSES, P, 4], BF16)
+            return grouped[key]
+
+        def scale_turned(n, h, first, count=2):
+            passes = slice(first, first + count)
             scales = scale_cols[:, passes, :].rearrange("p g (u e) -> p g u e", u=2)
-            if n == PAIRS - 1:
-                dst = grouped[n][:, 2 * q : 2 * q + 2]
+            tile = grouped_tile(n, first // 2)
+            g0 = first % 2 if n < HALVED else first
+            if n == LAST:
+                dst = tile[:, passes]
             else:
-                dst = grouped[n][:].rearrange("p (g h) i t -> p h g i t", h=2)[:, q // 2, passes]
+                dst = tile[:].rearrange("p (g h) i t -> p h g i t", h=2)[:, h, g0 : g0 + count]
             nc.vector.tensor_tensor(
                 out=dst.rearrange("p g i (u e) -> p g i u e", u=2),
-                in0=turned_rows[n, q][:].bitcast(BF16).rearrange("p u g (i e) -> p g i u e", e=2),
-                in1=scales.unsqueeze(2).to_broadcast([P, 2, P, 2, 2]),
+                in0=turned[n, h, first][:].bitcast(BF16).rearrange("p u g (i e) -> p g i u e", e=2),
+                in1=scales.unsqueeze(2).to_broadcast([P, count, P, 2, 2]),
                 op=ALU.mult,
             )
 
-        def turn_early(passes):
-            words = early_wide[:].bitcast(F32)
+        def turn_side(first):
+            words = side_wide[:].bitcast(F32)
             name = bank_names[0]
             bank_names.remove(name)
             bank = psum.tile([P, 2, 2, P], F32, name=name)
-            for g in passes:
+            side_banks[first] = (name, bank)
+            for g in range(first, first + 2):
                 for u in range(2):
                     nc.tensor.transpose(bank[:, u, g % 2, :], words[:, 256 * g + u : 256 * (g + 1) : 2], ident[:])
-            return name, bank[:].bitcast(BF16).rearrange("p u g (i e) -> p u g i e", e=2)
 
-        def scale_early(values, g):
+        def scale_side(g):
+            name, bank = side_banks[g - g % 2]
+            values = bank[:].bitcast(BF16).rearrange("p u g (i e) -> p u g i e", e=2)
             for t in range(4):
                 nc.scalar.activation(
-                    out=early_planes[:, g, t // 2, :, t % 2],
+                    out=side_planes[:, g, t // 2, :, t % 2],
                     in_=values[:, t // 2, g % 2, :, t % 2],
                     func=ACT.Copy,
                     scale=scale_cols[:, g, t : t + 1],
                 )
+            if g % 2 == 1:
+                bank_names.append(name)
 
-        def group_early(first, count):
+        def group_side(first, count):
+            part = slice(first, first + count)
             nc.scalar.copy(
-                out=early_grouped[:, first : first + count].bitcast(F32),
-                in_=early_planes[:, first : first + count].rearrange("p g u i e -> p g u (i e)").bitcast(F32).rearrange("p g u i -> p g i u"),
+                out=side_grouped[:, part].bitcast(F32),
+                in_=side_planes[:, part].rearrange("p g u i e -> p g u (i e)").bitcast(F32).rearrange("p g u i -> p g i u"),
             )
 
-        def quantize_early():
+        def quantize_side():
             nc.vector.quantize_mx(
-                out=early_codes[:].rearrange("p g i -> p (g i)").bitcast(FP8X4),
-                scales=early_scales[:].rearrange("p g i -> p (g i)"),
-                in_=early_grouped[:].rearrange("p g i t -> p (g i t)"),
+                out=side_codes[:].rearrange("p g i -> p (g i)").bitcast(FP8X4),
+                scales=side_scales[:].rearrange("p g i -> p (g i)"),
+                in_=side_grouped[:].rearrange("p g i t -> p (g i t)"),
             )
 
         def quantize_rows(n, first=0, count=2 * PASSES):
-            if first == 0:
+            if n not in a_codes:
                 a_codes[n] = ring("acodes", n, 3, [P, 2 * PASSES, P], U32)
                 a_scales[n] = ring("ascales", n, 3, [P, 2 * PASSES, P], U8)
             part = slice(first, first + count)
+            rows = grouped_tile(n, first // PASSES)[:] if n < HALVED else grouped_tile(n, 0)[:, part]
             nc.vector.quantize_mx(
                 out=a_codes[n][:, part].rearrange("p g i -> p (g i)").bitcast(FP8X4),
                 scales=a_scales[n][:, part].rearrange("p g i -> p (g i)"),
-                in_=grouped[n][:, part].rearrange("p g i t -> p (g i t)"),
+                in_=rows.rearrange("p g i t -> p (g i t)"),
             )
 
-        def aggregate(n, h):
-            bank = next_bank([P, 4, P], F32)
-            for g in range(PASSES):
-                codes = early_codes[:, g, :] if h == 1 else a_codes[n][:, g, :]
-                scales = early_scales[:, g, :] if h == 1 else a_scales[n][:, g, :]
+        def agg_tile(n):
+            if n not in agg_bf:
+                name = "stage%d" % (n % 3) if 1 <= n <= LAST - 3 else "aggbf%d" % n
+                agg_bf[n] = keep.tile([P, 2, P, 4], BF16, name=name, align_bytes=64)
+            return agg_bf[n]
+
+        def aggregate_tile(n, h, passes=range(PASSES)):
+            if (n, h) not in agg_banks:
+                agg_banks[n, h] = next_bank([P, 4, P], F32)
+            for g in passes:
                 for t in range(4):
                     nc.tensor.matmul_mx(
-                        out=bank[:, t, :],
+                        out=agg_banks[n, h][:, t, :],
                         lhsT=f_codes[g][:, t * P : (t + 1) * P].bitcast(FP8X4),
                         lhsT_scale=f_scales[g][:, t * P : (t + 1) * P],
-                        rhs=codes.bitcast(FP8X4),
-                        rhs_scale=scales,
+                        rhs=(side_codes[:, g, :] if h == 1 else a_codes[n][:, g, :]).bitcast(FP8X4),
+                        rhs_scale=side_scales[:, g, :] if h == 1 else a_scales[n][:, g, :],
                         start=(g == 0 and t == 0),
                         stop=(g == PASSES - 1 and t == 3),
                     )
-            if h == 1:
-                agg_bf[n] = ring("aggbf", n, 3, [P, 2, P, 4], BF16)
-                agg_codes[n] = ring("aggcodes", n, 3, [P, 2 * P], U32)
-                agg_scales[n] = ring("aggscales", n, 3, [P, 2 * P], U8)
-            nc.scalar.copy(out=agg_bf[n][:, h], in_=bank[:].rearrange("p t i -> p i t"))
 
-        def aggregate_pair(n, order=range(PASSES)):
-            agg_bf[n] = ring("aggbf", n, 3, [P, 2, P, 4], BF16)
-            agg_codes[n] = ring("aggcodes", n, 3, [P, 2 * P], U32)
-            agg_scales[n] = ring("aggscales", n, 3, [P, 2 * P], U8)
-            banks = [next_bank([P, 2, 2 * P], F32) for half in range(2)]
-            steps = [(half, g) for half in range(2) for g in order]
-            if n == 0:
-                steps = [(half, g) for g in order for half in range(2)]
-            for half, g in steps:
+        def copy_agg_tile(n, h):
+            nc.scalar.copy(out=agg_tile(n)[:, h], in_=agg_banks[n, h][:].rearrange("p t i -> p i t"))
+
+        def aggregate(n, half, passes=range(PASSES), order=range(PASSES)):
+            if (n, half) not in agg_banks:
+                agg_banks[n, half] = next_bank([P, 2, 2 * P], F32)
+            for g in passes:
                 for tl in range(2):
                     t = 2 * half + tl
                     nc.tensor.matmul_mx(
-                        out=banks[half][:, tl, :],
+                        out=agg_banks[n, half][:, tl, :],
                         lhsT=f_codes[g][:, t * P : (t + 1) * P].bitcast(FP8X4),
                         lhsT_scale=f_scales[g][:, t * P : (t + 1) * P],
                         rhs=a_codes[n][:, 2 * g : 2 * g + 2].rearrange("p h i -> p (h i)").bitcast(FP8X4),
@@ -261,13 +294,17 @@ def tile_net_pa_w4_kernel(tc, A_bytes, A_scale, features, Wg_words, Wg_scales, b
                         start=(g == order[0] and tl == 0),
                         stop=(g == order[-1] and tl == 1),
                     )
-            for half in range(2):
-                nc.scalar.copy(
-                    out=agg_bf[n][:].rearrange("p h i t -> p (h i) t")[:, :, 2 * half : 2 * half + 2],
-                    in_=banks[half][:].rearrange("p t i -> p i t"),
-                )
+
+        def copy_agg(n, half):
+            nc.scalar.copy(
+                out=agg_tile(n)[:].rearrange("p h i t -> p (h i) t")[:, :, 2 * half : 2 * half + 2],
+                in_=agg_banks[n, half][:].rearrange("p t i -> p i t"),
+            )
 
         def quantize_agg(n, first=0, count=2):
+            if n not in agg_codes:
+                agg_codes[n] = ring("aggcodes", n, 4, [P, 2 * P], U32)
+                agg_scales[n] = ring("aggscales", n, 4, [P, 2 * P], U8)
             cols = slice(first * P, (first + count) * P)
             nc.vector.quantize_mx(
                 out=agg_codes[n][:, cols].bitcast(FP8X4),
@@ -288,6 +325,36 @@ def tile_net_pa_w4_kernel(tc, A_bytes, A_scale, features, Wg_words, Wg_scales, b
                 stop=True,
             )
 
+        def finish_in_halves(n, h):
+            halves = [slice(c * D // 2, (c + 1) * D // 2) for c in range(2)]
+            banks = [next_bank([P, D // 2], F32) for c in range(2)]
+            sums = [keep.tile([P, D // 2], F32, name="lastsum%d" % c, align_bytes=64) for c in range(2)]
+            rows = [keep.tile([P, D // 2], F32, name="lastrows%d" % c, align_bytes=64) for c in range(2)]
+            for c in range(2):
+                nc.tensor.matmul_mx(
+                    out=banks[c][:],
+                    lhsT=agg_codes[n][:, h * P : (h + 1) * P].bitcast(FP8X4),
+                    lhsT_scale=agg_scales[n][:, h * P : (h + 1) * P],
+                    rhs=w_words[:, c * D : (c + 1) * D].bitcast(FP4X4),
+                    rhs_scale=w_scales[:, halves[c]],
+                    start=True,
+                    stop=True,
+                )
+            return halves, banks, sums, rows
+
+        def add_half(parts, c):
+            halves, banks, sums, rows = parts
+            nc.vector.tensor_tensor(out=sums[c][:], in0=banks[c][:], in1=bias_row[:, halves[c]], op=ALU.add)
+
+        def relu_store_half(n, h, parts, c, engine):
+            halves, banks, sums, rows = parts
+            if engine == "vector":
+                nc.vector.tensor_scalar(out=rows[c][:], in0=sums[c][:], scalar1=0.0, scalar2=None, op0=ALU.max)
+            else:
+                nc.scalar.activation(out=rows[c][:], in_=sums[c][:], func=ACT.Relu)
+            r0 = (2 * n + h) * P
+            nc.sync.dma_start(out=out[r0 : r0 + P, halves[c]], in_=rows[c][:])
+
         def add_bias(n, h):
             summed[n, h] = ring("summed", 2 * n + h, 6, [P, D], F32)
             nc.vector.tensor_tensor(out=summed[n, h][:], in0=product[n, h][:], in1=bias_row[:], op=ALU.add)
@@ -305,13 +372,11 @@ def tile_net_pa_w4_kernel(tc, A_bytes, A_scale, features, Wg_words, Wg_scales, b
             store(n, h, rows)
 
         def project_turned(n, half):
-            if half == 0:
-                relu_turned[n] = ring("reluturned", n, 3, [P, 4, 2 * P], F32)
-            bank = next_bank([P, 2, 2 * P], F32)
+            product[n, half] = next_bank([P, 2, 2 * P], F32)
             for cl in range(2):
                 c = 2 * half + cl
                 nc.tensor.matmul_mx(
-                    out=bank[:, cl, :],
+                    out=product[n, half][:, cl, :],
                     lhsT=w_words[:, 2 * c * P : 2 * (c + 1) * P].bitcast(FP4X4),
                     lhsT_scale=w_scales[:, c * P : (c + 1) * P],
                     rhs=agg_codes[n][:].bitcast(FP8X4),
@@ -319,10 +384,17 @@ def tile_net_pa_w4_kernel(tc, A_bytes, A_scale, features, Wg_words, Wg_scales, b
                     start=True,
                     stop=True,
                 )
+
+        def relu_of_turned(n, half):
+            if n not in relu_turned:
+                relu_turned[n] = ring("reluturned", n, 3, [P, 4, 2 * P], F32)
             for cl in range(2):
                 c = 2 * half + cl
                 nc.scalar.activation(
-                    out=relu_turned[n][:, c, :], in_=bank[:, cl, :], func=ACT.Relu, bias=bias_chunks[:, c : c + 1]
+                    out=relu_turned[n][:, c, :],
+                    in_=product[n, half][:, cl, :],
+                    func=ACT.Relu,
+                    bias=bias_chunks[:, c : c + 1],
                 )
 
         def turn_back(n, h):
@@ -335,156 +407,199 @@ def tile_net_pa_w4_kernel(tc, A_bytes, A_scale, features, Wg_words, Wg_scales, b
             nc.scalar.copy(out=rows[:], in_=back[n, h][:].rearrange("p c n -> p (c n)"))
             store(n, h, rows)
 
-        def turn_back_store(n, h):
-            turn_back(n, h)
-            store_back(n, h)
-
         make_identity(nc, ident[:])
+        nc.vector.memset(ones[:], 1.0)
         nc.vector.memset(w_scales[:].bitcast(I32), 0)
         nc.scalar.copy(out=ident_bf[:], in_=ident[:])
 
-        load_a(0, 0)
+        load_a(0, 0, 0, NODES // 2)
+        load_a(0, 0, NODES // 2, NODES)
+        load_a(0, 1, 0, NODES // 2)
         nc.sync.dma_start(out=scale_cols[:], in_=A_scale.rearrange("o (g p t) -> p (o g) t", p=P, t=4))
-        load_a(0, 1)
-        load_f(0)
-        load_pair(1)
-        load_f(2)
-        load_f(1)
-        load_f(3)
-        nc.sync.dma_start(out=bias_raw[:], in_=bg.rearrange("(p t) -> p t", t=4))
-        nc.sync.dma_start(out=early_bytes[:], in_=A_bytes[NODES - P :, :])
+        load_a(0, 1, NODES // 2, NODES)
+        load_a(1, 0)
+        load_a(1, 1)
+        for g in range(2):
+            load_f(g)
         load_pair(2)
+        nc.sync.dma_start(out=bias_row[:], in_=bg.partition_broadcast(P))
+        load_f(2)
+        load_f(3)
+        nc.sync.dma_start(out=side_bytes[:], in_=A_bytes[NODES - P :, :])
         load_pair(3)
         load_w()
-        for n in range(4, PAIRS - 1):
+        for n in range(4, LAST):
             load_pair(n)
-        load_a(PAIRS - 1, 0)
+        load_a(LAST, 0)
 
-        for q in range(3):
-            widen(0, q * QUARTER, (q + 1) * QUARTER, "vector")
-        widen(0, 3 * QUARTER, 4 * QUARTER, "scalar")
-        for q in range(4):
-            turn(0, q)
+        def widen_pair(n, share=SHARE):
+            widen(n, 0, NODES, "gpsimd")
+            widen(n, NODES, 2 * NODES - share, "gpsimd")
+
+        def widen_share(n, share=SHARE):
+            widen(n, 2 * NODES - share, 2 * NODES, "scalar")
+
+        for g in range(PASSES):
+            widen_parted(g)
+        widen(0, NODES, NODES + 1024, "scalar")
+        widen(0, NODES + 1024, 2 * NODES, "scalar")
+        turn(0, 0, 0, 1)
+        turn(0, 0, 1, 1)
+        turn(0, 0, 2)
+        turn(0, 1, 0)
+        scale_turned(0, 0, 0, 1)
+        turn(0, 1, 2)
+        scale_turned(0, 0, 1, 1)
+        scale_turned(0, 0, 2)
+        widen_pair(1, FIRST_SHARE)
+        widen_share(1, FIRST_SHARE)
+        scale_turned(0, 1, 0)
+        scale_turned(0, 1, 2)
+        turn(1, 0, 0)
+        turn(1, 0, 2)
+        for g in range(PASSES):
+            features_tile(g, "fgrouped%d" % g)
         group_features_by_copy(0)
-        widen(1, 0, FIRST_SCALAR_COLUMNS, "scalar")
-        widen(1, FIRST_SCALAR_COLUMNS, 4 * QUARTER, "gpsimd")
-        for q in range(4):
-            scale_turned(0, q)
         group_features_by_copy(1)
-        nc.scalar.copy(out=bias_cols[:], in_=bias_raw[:])
-        group_features(2)
-        for q in range(4):
-            turn(1, q)
+
+        quantize_rows(0, 0, 4)
+        quantize_rows(0, 4, 4)
         quantize_features(0)
-        group_features_on_vector(3)
-        quantize_rows(0)
-        for g in (3, 1, 2):
-            quantize_features(g)
-        nc.scalar.copy(out=early_wide[:], in_=early_bytes[:].bitcast(FP8))
+        widen_pair(2)
+        widen_share(2)
+        group_features_by_copy(2)
+        group_features_by_copy(3)
+        nc.scalar.copy(out=side_wide[:], in_=side_bytes[:].bitcast(FP8))
+        turn(1, 1, 0)
+        turn(1, 1, 2)
+        scale_turned(1, 0, 0)
+        scale_turned(1, 0, 2)
+        bias_to_partitions()
+        turn(2, 0, 0)
+        turn(2, 0, 2)
+        scale_turned(1, 1, 0)
+        scale_turned(1, 1, 2)
 
-        last = PAIRS - 1
-        for n in range(1, last - 1):
-            if n >= 2:
-                quantize_agg(n - 2)
-                quantize_rows(n - 1)
-            widen(n + 1, 0, SCALAR_COLUMNS, "scalar")
-            widen(n + 1, SCALAR_COLUMNS, 4 * QUARTER, "gpsimd")
-            for q in range(4):
-                scale_turned(n, q)
-            aggregate_pair(n - 1, (0, 3, 1, 2) if n == 1 else range(PASSES))
-            if n == 1:
-                first_bank, first_values = turn_early((0, 1))
-                scale_early(first_values, 0)
-            if n == 2:
-                scale_early(first_values, 1)
-                bank_names.append(first_bank)
-            turn(n + 1, 0)
-            if n == 1:
-                spread_bias()
-                second_bank, second_values = turn_early((2,))
-                scale_early(second_values, 2)
-                bank_names.append(second_bank)
-            if n == 2:
-                bias_to_partitions()
-            if n >= 3:
-                turn_back_store(n - 3, 0)
-                turn_back_store(n - 3, 1)
-            if n >= 2:
-                project_turned(n - 2, 0)
-            if n == GROUPING_PERIOD:
-                group_early(0, 3)
-            turn(n + 1, 1)
-            turn(n + 1, 2)
-            if n >= 2:
-                project_turned(n - 2, 1)
-            turn(n + 1, 3)
+        quantize_features(1)
+        quantize_features(2)
+        quantize_rows(1, 0, 4)
+        quantize_rows(1, 4, 4)
+        quantize_features(3)
+        widen_pair(3)
+        widen_share(3)
+        for g in range(PASSES):
+            if g == 3:
+                turn(2, 1, 0)
+                turn(2, 1, 2)
+            for half in range(2):
+                aggregate(0, half, (g,))
+        copy_agg(0, 0)
+        copy_agg(0, 1)
+        aggregate(1, 0)
+        aggregate(1, 1)
+        copy_agg(1, 0)
+        copy_agg(1, 1)
+        scale_turned(2, 0, 0)
+        scale_turned(2, 0, 2)
+        turn_side(0)
+        turn(3, 0, 0)
+        turn(3, 0, 2)
+        scale_side(0)
+        scale_side(1)
+        scale_turned(2, 1, 0)
+        scale_turned(2, 1, 2)
 
-        third_bank, third_values = turn_early((3,))
-        quantize_agg(last - 3)
-        quantize_rows(last - 2)
-        widen(last, 0, NODES, "gpsimd")
-        scale_early(third_values, 3)
-        bank_names.append(third_bank)
-        for q in range(4):
-            scale_turned(last - 1, q)
-        aggregate_pair(last - 2)
-        group_early(3, 1)
-        project_turned(last - 3, 0)
-        turn_back_store(last - 4, 0)
-        turn_back(last - 4, 1)
-        turn(last, 0)
-        project_turned(last - 3, 1)
-        store_back(last - 4, 1)
-        turn(last, 1)
+        for n in range(3, LAST):
+            if n == 3:
+                quantize_agg(0)
+            if n == SIDE_PERIOD:
+                quantize_side()
+            quantize_agg(n - 2)
+            quantize_rows(n - 1)
+            if n + 1 < LAST:
+                widen_pair(n + 1)
+                widen_share(n + 1)
+            else:
+                widen(LAST, 0, NODES, "gpsimd")
+            if n == 3:
+                project_turned(0, 0)
+                project_turned(0, 1)
+            turn(n, 1, 0)
+            turn(n, 1, 2)
+            if n == 3:
+                relu_of_turned(0, 0)
+                relu_of_turned(0, 1)
+            if n == 4:
+                group_side(0, 2)
+            if n == 5:
+                scale_side(3)
+            project_turned(n - 2, 0)
+            relu_of_turned(n - 2, 0)
+            if n == 5:
+                group_side(2, 2)
+            aggregate(n - 1, 0)
+            copy_agg(n - 1, 0)
+            aggregate(n - 1, 1)
+            copy_agg(n - 1, 1)
+            scale_turned(n, 0, 0)
+            scale_turned(n, 0, 2)
+            for h in range(2):
+                turn_back(n - 3, h)
+                store_back(n - 3, h)
+            turn(n + 1, 0, 0)
+            if n == 4:
+                turn_side(2)
+            project_turned(n - 2, 1)
+            relu_of_turned(n - 2, 1)
+            if n == 4:
+                scale_side(2)
+            if n == SIDE_PERIOD:
+                aggregate_tile(LAST, 1)
+                copy_agg_tile(LAST, 1)
+            turn(n + 1, 0, 2)
+            scale_turned(n, 1, 0)
+            scale_turned(n, 1, 2)
 
-        mid0, back0, back1, mid1 = bank_names
+        free0, free1, held0, held1 = turn_names
+        ring0, ring1, ring2, ring3 = bank_names
         bank_names.clear()
-        bank_names.extend(
-            [
-                "turn2",
-                "turn3",
-                mid0,
-                mid1,
-                back0,
-                back1,
-                "turn0",
-                "turn1",
-                mid0,
-                mid1,
-                back0,
-                "turn2",
-            ]
-        )
-        quantize_agg(last - 2)
-        quantize_rows(last - 1)
-        quantize_early()
-        scale_turned(last, 0)
-        scale_turned(last, 1)
-        quantize_rows(last, 0, 2)
-        project(last - 2, 0)
-        project(last - 2, 1)
-        turn_back_store(last - 3, 0)
-        turn_back_store(last - 3, 1)
-        add_bias(last - 2, 0)
-        quantize_rows(last, 2, 2)
-        add_bias(last - 2, 1)
-        aggregate_pair(last - 1)
-        relu_store(last - 2, 0)
-        aggregate(last, 1)
-        quantize_agg(last - 1)
-        relu_store(last - 2, 1, "vector")
-        quantize_agg(last, 1, 1)
-        aggregate(last, 0)
-        project(last - 1, 0)
-        project(last - 1, 1)
-        project(last, 1)
-        add_bias(last - 1, 0)
-        quantize_agg(last, 0, 1)
-        project(last, 0)
-        add_bias(last - 1, 1)
-        relu_store(last - 1, 0)
-        add_bias(last, 1)
-        relu_store(last - 1, 1)
-        add_bias(last, 0)
-        relu_store(last, 1)
-        relu_store(last, 0, "vector")
+        bank_names.extend([free0, free1, ring0, ring1, ring2, ring3, held0, ring0, ring1, free0, held1, ring2])
+        quantize_agg(LAST - 2)
+        quantize_rows(LAST - 1)
+        project(LAST - 2, 0)
+        project(LAST - 2, 1)
+        turn_back(LAST - 3, 0)
+        turn_back(LAST - 3, 1)
+        store_back(LAST - 3, 0)
+        store_back(LAST - 3, 1)
+        scale_turned(LAST, 0, 0)
+        quantize_agg(LAST, 1, 1)
+        aggregate(LAST - 1, 0)
+        copy_agg(LAST - 1, 0)
+        quantize_rows(LAST, 0, 2)
+        scale_turned(LAST, 0, 2)
+        add_bias(LAST - 2, 0)
+        aggregate(LAST - 1, 1)
+        copy_agg(LAST - 1, 1)
+        quantize_rows(LAST, 2, 2)
+        project(LAST, 1)
+        aggregate_tile(LAST, 0)
+        add_bias(LAST - 2, 1)
+        relu_store(LAST - 2, 0)
+        quantize_agg(LAST - 1)
+        add_bias(LAST, 1)
+        relu_store(LAST - 2, 1)
+        copy_agg_tile(LAST, 0)
+        project(LAST - 1, 0)
+        project(LAST - 1, 1)
+        relu_store(LAST, 1)
+        add_bias(LAST - 1, 0)
+        quantize_agg(LAST, 0, 1)
+        parts = finish_in_halves(LAST, 0)
+        add_bias(LAST - 1, 1)
+        relu_store(LAST - 1, 0)
+        add_half(parts, 0)
+        add_half(parts, 1)
+        relu_store(LAST - 1, 1)
+        relu_store_half(LAST, 0, parts, 0, "vector")
+        relu_store_half(LAST, 0, parts, 1, "vector")

@@ -18,14 +18,15 @@ NODES = 2048
 D = 512
 P = 128
 PASS = 512
+QUARTER = 1024
+PAIR = 4 * QUARTER
 PASSES = NODES // PASS
 PAIRS = NODES // (2 * P)
 LAST = PAIRS - 1
 TURN_BANKS = 4
-PARTED_TILES = 1
-FIRST_SHARE = 1280
-SHARE = 256
-SIDE_PERIOD = 6
+FIRST = 2048
+SECOND_SHARE = 768
+SHARE = 512
 HALVED = 2
 FLOPS = 2 * NODES * NODES * D + 2 * NODES * D * D
 
@@ -37,10 +38,12 @@ def tile_net_pa_w4_kernel(tc, A_bytes, A_scale, features, Wg_words, Wg_scales, b
         psum = ctx.enter_context(tc.psum_pool(name="psum", bufs=1))
         ctx.enter_context(tc.manual_schedule())
 
-        a_bytes = [keep.tile([P, 2 * NODES], U8, name="abytes%d" % n, align_bytes=64) for n in range(PAIRS)]
+        a_bytes = keep.tile([P, (2 * PAIRS - 1) * NODES], U8, name="abytes", align_bytes=64)
         scale_cols = keep.tile([P, PASSES, 4], F32, name="scalecols")
         ones = keep.tile([P, 1], F32, name="ones")
-        bias_row = keep.tile([P, D], BF16, name="biasrow", align_bytes=64)
+        bias_raw = keep.tile([P, 4], BF16, name="biasraw")
+        bias_cols = keep.tile([P, 4], F32, name="biascols")
+        bias_row = keep.tile([P, D], F32, name="biasrow", align_bytes=64)
         bias_chunks = keep.tile([P, 4], F32, name="biaschunks")
         f_raw = [keep.tile([P, 4, D], BF16, name="fraw%d" % g, align_bytes=64) for g in range(PASSES)]
         f_codes = [keep.tile([P, D], U32, name="fcodes%d" % g, align_bytes=64) for g in range(PASSES)]
@@ -54,7 +57,6 @@ def tile_net_pa_w4_kernel(tc, A_bytes, A_scale, features, Wg_words, Wg_scales, b
         side_codes = keep.tile([P, PASSES, P], U32, name="sidecodes", align_bytes=64)
         side_scales = keep.tile([P, PASSES, P], U8, name="sidescales", align_bytes=64)
         ident = keep.tile([P, P], F32, name="ident", align_bytes=64)
-        ident_bf = keep.tile([P, P], BF16, name="identbf", align_bytes=64)
 
         bank_names = ["other%d" % b for b in range(8 - TURN_BANKS)]
         turn_names = ["turn%d" % b for b in range(TURN_BANKS)]
@@ -71,12 +73,12 @@ def tile_net_pa_w4_kernel(tc, A_bytes, A_scale, features, Wg_words, Wg_scales, b
         def load_a(n, h, first=0, last=NODES):
             r0 = (2 * n + h) * P
             nc.sync.dma_start(
-                out=a_bytes[n][:, h * NODES + first : h * NODES + last], in_=A_bytes[r0 : r0 + P, first:last]
+                out=a_bytes[:, (2 * n + h) * NODES + first : (2 * n + h) * NODES + last], in_=A_bytes[r0 : r0 + P, first:last]
             )
 
         def load_pair(n):
             nc.sync.dma_start(
-                out=a_bytes[n][:].rearrange("p (h k) -> p h k", h=2),
+                out=a_bytes[:, 2 * n * NODES : 2 * (n + 1) * NODES].rearrange("p (h k) -> p h k", h=2),
                 in_=A_bytes[2 * n * P : 2 * (n + 1) * P, :].rearrange("(h p) k -> p h k", p=P),
             )
 
@@ -91,32 +93,24 @@ def tile_net_pa_w4_kernel(tc, A_bytes, A_scale, features, Wg_words, Wg_scales, b
                     in_=Wg_scales.rearrange("g q n -> (g q) n")[4 * q : 4 * q + 4, :].bitcast(I32),
                 )
 
+        def spread_bias():
+            bank = next_bank([P, 4, P], F32)
+            for t in range(4):
+                column = bias_cols[:, t : t + 1].to_broadcast([P, P])
+                nc.tensor.matmul(bank[:, t, :], lhsT=column, rhs=ident[:], start=True, stop=True)
+            nc.scalar.copy(out=bias_row[:].rearrange("p (n t) -> p n t", t=4), in_=bank[:].rearrange("p t n -> p n t"))
+
         def bias_to_partitions():
-            bank = next_bank([P, 4, P], BF16)
+            bank = next_bank([P, 4, P], F32)
             for c in range(4):
-                nc.tensor.transpose(bank[:, c, :], bias_row[:, c * P : (c + 1) * P], ident_bf[:])
+                chunk = bias_row[:, c * P : (c + 1) * P]
+                nc.tensor.matmul(bank[:, c, :], lhsT=chunk, rhs=ident[:], start=True, stop=True)
             nc.scalar.copy(out=bias_chunks[:].rearrange("p (c o) -> p c o", o=1), in_=bank[:, :, 0:1])
 
-        f_grouped, f_banks = {}, {}
+        f_grouped = {}
 
         def features_tile(g, name):
             f_grouped[g] = keep.tile([P, 4, P, 4], BF16, name=name, align_bytes=64)
-
-        def group_features_by_matmul(g, q):
-            half, ql = divmod(q, 2)
-            src = f_raw[g][:].rearrange("p j (q c) -> p q c j", q=4)
-            if ql == 0:
-                f_banks[g, half] = next_bank([P, 4, 64, 4], BF16)
-            nc.tensor.matmul(
-                f_banks[g, half][:, :, 32 * ql : 32 * (ql + 1), :].rearrange("p t m j -> p m t j"),
-                lhsT=ident_bf[:],
-                rhs=src[:, q].rearrange("p (m t) j -> p m t j", t=4),
-                start=True,
-                stop=True,
-            )
-
-        def copy_features(g, half):
-            nc.scalar.copy(out=f_grouped[g][:, :, 64 * half : 64 * (half + 1), :], in_=f_banks[g, half][:])
 
         def group_features_by_copy(g):
             nc.scalar.copy(
@@ -141,37 +135,37 @@ def tile_net_pa_w4_kernel(tc, A_bytes, A_scale, features, Wg_words, Wg_scales, b
         agg_banks, agg_bf, agg_codes, agg_scales = {}, {}, {}, {}
         product, relu_turned, summed, back, side_banks = {}, {}, {}, {}, {}
 
-        def wide_tile(n):
-            if n not in wide:
-                name = "stage%d" % (n % 3)
-                wide[n] = keep.tile([P, 2 * NODES], BF16, name=name, align_bytes=64)
-            return wide[n]
+        starts = [0, PAIR] + [n * PAIR + QUARTER for n in range(2, LAST)] + [LAST * PAIR, LAST * PAIR + NODES]
 
-        def widen(n, first, last, engine):
-            src = a_bytes[n][:, first:last].bitcast(FP8)
+        def wide_columns(first, last):
+            n = max(m for m in range(PAIRS) if starts[m] <= first)
+            if n not in wide:
+                shape = [P, starts[n + 1] - starts[n]]
+                wide[n] = keep.tile(shape, BF16, name="stage%d" % (n % 3), align_bytes=64)
+            return wide[n][:, first - starts[n] : last - starts[n]]
+
+        def widen(first, last, engine):
+            src = a_bytes[:, first:last].bitcast(FP8)
             if engine == "scalar":
-                nc.scalar.copy(out=wide_tile(n)[:, first:last], in_=src)
-            elif engine == "vector":
-                nc.vector.tensor_copy(out=wide_tile(n)[:, first:last], in_=src)
+                nc.scalar.copy(out=wide_columns(first, last), in_=src)
             else:
-                nc.gpsimd.tensor_copy(out=wide_tile(n)[:, first:last], in_=src)
+                nc.gpsimd.tensor_copy(out=wide_columns(first, last), in_=src)
 
         def widen_parted(g):
-            cols = slice(g * PASS, (g + 1) * PASS)
             nc.vector.tensor_scalar(
-                out=wide_tile(0)[:, cols].rearrange("p (u q e) -> p q u e", u=2, e=2),
-                in0=a_bytes[0][:, cols].bitcast(FP8).rearrange("p (q u e) -> p q u e", u=2, e=2),
+                out=wide_columns(g * PASS, (g + 1) * PASS).rearrange("p (u q e) -> p q u e", u=2, e=2),
+                in0=a_bytes[:, g * PASS : (g + 1) * PASS].bitcast(FP8).rearrange("p (q u e) -> p q u e", u=2, e=2),
                 scalar1=ones[:],
                 scalar2=None,
                 op0=ALU.mult,
             )
 
         def word_columns(n, h, g, u):
-            words = wide[n][:].bitcast(F32)
-            w0 = 256 * (PASSES * h + g)
-            if n == 0 and h < PARTED_TILES:
-                return words[:, w0 + P * u : w0 + P * (u + 1)]
-            return words[:, w0 + u : w0 + 256 : 2]
+            first = (2 * n + h) * NODES + g * PASS
+            words = wide_columns(first, first + PASS).bitcast(F32)
+            if n == 0 and h == 0:
+                return words[:, P * u : P * (u + 1)]
+            return words[:, u : 2 * P : 2]
 
         def turn(n, h, first, count=2):
             bank = next_bank([P, 2, count, P], F32, turn_names)
@@ -206,28 +200,21 @@ def tile_net_pa_w4_kernel(tc, A_bytes, A_scale, features, Wg_words, Wg_scales, b
                 op=ALU.mult,
             )
 
-        def turn_side(first):
-            words = side_wide[:].bitcast(F32)
-            name = bank_names[0]
-            bank_names.remove(name)
-            bank = psum.tile([P, 2, 2, P], F32, name=name)
-            side_banks[first] = (name, bank)
-            for g in range(first, first + 2):
-                for u in range(2):
-                    nc.tensor.transpose(bank[:, u, g % 2, :], words[:, 256 * g + u : 256 * (g + 1) : 2], ident[:])
+        def turn_side(g):
+            words = side_wide[:, g * PASS : (g + 1) * PASS].bitcast(F32)
+            side_banks[g] = next_bank([P, 2, P], F32)
+            for u in range(2):
+                nc.tensor.transpose(side_banks[g][:, u, :], words[:, u : 2 * P : 2], ident[:])
 
         def scale_side(g):
-            name, bank = side_banks[g - g % 2]
-            values = bank[:].bitcast(BF16).rearrange("p u g (i e) -> p u g i e", e=2)
+            values = side_banks[g][:].bitcast(BF16).rearrange("p u (i e) -> p u i e", e=2)
             for t in range(4):
                 nc.scalar.activation(
                     out=side_planes[:, g, t // 2, :, t % 2],
-                    in_=values[:, t // 2, g % 2, :, t % 2],
+                    in_=values[:, t // 2, :, t % 2],
                     func=ACT.Copy,
                     scale=scale_cols[:, g, t : t + 1],
                 )
-            if g % 2 == 1:
-                bank_names.append(name)
 
         def group_side(first, count):
             part = slice(first, first + count)
@@ -410,7 +397,6 @@ def tile_net_pa_w4_kernel(tc, A_bytes, A_scale, features, Wg_words, Wg_scales, b
         make_identity(nc, ident[:])
         nc.vector.memset(ones[:], 1.0)
         nc.vector.memset(w_scales[:].bitcast(I32), 0)
-        nc.scalar.copy(out=ident_bf[:], in_=ident[:])
 
         load_a(0, 0, 0, NODES // 2)
         load_a(0, 0, NODES // 2, NODES)
@@ -418,11 +404,11 @@ def tile_net_pa_w4_kernel(tc, A_bytes, A_scale, features, Wg_words, Wg_scales, b
         nc.sync.dma_start(out=scale_cols[:], in_=A_scale.rearrange("o (g p t) -> p (o g) t", p=P, t=4))
         load_a(0, 1, NODES // 2, NODES)
         load_a(1, 0)
+        load_f(0)
         load_a(1, 1)
-        for g in range(2):
-            load_f(g)
+        nc.sync.dma_start(out=bias_raw[:], in_=bg.rearrange("(p t) -> p t", t=4))
+        load_f(1)
         load_pair(2)
-        nc.sync.dma_start(out=bias_row[:], in_=bg.partition_broadcast(P))
         load_f(2)
         load_f(3)
         nc.sync.dma_start(out=side_bytes[:], in_=A_bytes[NODES - P :, :])
@@ -432,17 +418,10 @@ def tile_net_pa_w4_kernel(tc, A_bytes, A_scale, features, Wg_words, Wg_scales, b
             load_pair(n)
         load_a(LAST, 0)
 
-        def widen_pair(n, share=SHARE):
-            widen(n, 0, NODES, "gpsimd")
-            widen(n, NODES, 2 * NODES - share, "gpsimd")
-
-        def widen_share(n, share=SHARE):
-            widen(n, 2 * NODES - share, 2 * NODES, "scalar")
-
         for g in range(PASSES):
             widen_parted(g)
-        widen(0, NODES, NODES + 1024, "scalar")
-        widen(0, NODES + 1024, 2 * NODES, "scalar")
+        widen(2 * QUARTER, 3 * QUARTER, "scalar")
+        widen(3 * QUARTER, 4 * QUARTER, "scalar")
         turn(0, 0, 0, 1)
         turn(0, 0, 1, 1)
         turn(0, 0, 2)
@@ -451,48 +430,50 @@ def tile_net_pa_w4_kernel(tc, A_bytes, A_scale, features, Wg_words, Wg_scales, b
         turn(0, 1, 2)
         scale_turned(0, 0, 1, 1)
         scale_turned(0, 0, 2)
-        widen_pair(1, FIRST_SHARE)
-        widen_share(1, FIRST_SHARE)
+        widen(PAIR, PAIR + NODES, "gpsimd")
+        for g in range(PASSES):
+            features_tile(g, "fgrouped%d" % g)
+        group_features_by_copy(0)
+        for q in range(2, 5):
+            widen(PAIR + q * QUARTER, PAIR + (q + 1) * QUARTER, "scalar")
         scale_turned(0, 1, 0)
         scale_turned(0, 1, 2)
         turn(1, 0, 0)
         turn(1, 0, 2)
-        for g in range(PASSES):
-            features_tile(g, "fgrouped%d" % g)
-        group_features_by_copy(0)
+        nc.scalar.copy(out=bias_cols[:], in_=bias_raw[:])
         group_features_by_copy(1)
 
         quantize_rows(0, 0, 4)
         quantize_rows(0, 4, 4)
         quantize_features(0)
-        widen_pair(2)
-        widen_share(2)
+        widen(2 * PAIR + QUARTER, 3 * PAIR, "gpsimd")
         group_features_by_copy(2)
-        group_features_by_copy(3)
-        nc.scalar.copy(out=side_wide[:], in_=side_bytes[:].bitcast(FP8))
         turn(1, 1, 0)
         turn(1, 1, 2)
         scale_turned(1, 0, 0)
-        scale_turned(1, 0, 2)
-        bias_to_partitions()
         turn(2, 0, 0)
-        turn(2, 0, 2)
+        spread_bias()
+        widen(3 * PAIR, 3 * PAIR + QUARTER, "scalar")
+        nc.scalar.copy(out=side_wide[:], in_=side_bytes[:].bitcast(FP8))
+        aggregate(0, 0, (0,))
+        aggregate(0, 1, (0,))
+        scale_turned(1, 0, 2)
         scale_turned(1, 1, 0)
         scale_turned(1, 1, 2)
+        turn(2, 0, 2)
 
         quantize_features(1)
+        group_features_on_vector(3)
         quantize_features(2)
+        quantize_features(3)
         quantize_rows(1, 0, 4)
         quantize_rows(1, 4, 4)
-        quantize_features(3)
-        widen_pair(3)
-        widen_share(3)
-        for g in range(PASSES):
-            if g == 3:
-                turn(2, 1, 0)
-                turn(2, 1, 2)
+        widen(3 * PAIR + QUARTER, 4 * PAIR + QUARTER - SECOND_SHARE, "gpsimd")
+        for g in range(1, PASSES):
             for half in range(2):
                 aggregate(0, half, (g,))
+            if g < 3:
+                turn(2, 1, 2 * g - 2)
         copy_agg(0, 0)
         copy_agg(0, 1)
         aggregate(1, 0)
@@ -501,97 +482,93 @@ def tile_net_pa_w4_kernel(tc, A_bytes, A_scale, features, Wg_words, Wg_scales, b
         copy_agg(1, 1)
         scale_turned(2, 0, 0)
         scale_turned(2, 0, 2)
-        turn_side(0)
         turn(3, 0, 0)
-        turn(3, 0, 2)
+        turn_side(0)
+        widen(4 * PAIR + QUARTER - SECOND_SHARE, 4 * PAIR + QUARTER, "scalar")
+        bias_to_partitions()
         scale_side(0)
-        scale_side(1)
         scale_turned(2, 1, 0)
         scale_turned(2, 1, 2)
 
         for n in range(3, LAST):
             if n == 3:
                 quantize_agg(0)
-            if n == SIDE_PERIOD:
-                quantize_side()
             quantize_agg(n - 2)
             quantize_rows(n - 1)
-            if n + 1 < LAST:
-                widen_pair(n + 1)
-                widen_share(n + 1)
-            else:
-                widen(LAST, 0, NODES, "gpsimd")
+            start = min((n + 1) * PAIR + QUARTER, LAST * PAIR)
+            stop = min(start + PAIR, LAST * PAIR) if n < LAST - 1 else start + NODES
+            share = SHARE if stop - start == PAIR else 0
+            widen(start, stop - share, "gpsimd")
+            turn(n, 0, 2)
             if n == 3:
-                project_turned(0, 0)
-                project_turned(0, 1)
+                for half in range(2):
+                    project_turned(0, half)
+                    relu_of_turned(0, half)
             turn(n, 1, 0)
             turn(n, 1, 2)
-            if n == 3:
-                relu_of_turned(0, 0)
-                relu_of_turned(0, 1)
-            if n == 4:
-                group_side(0, 2)
-            if n == 5:
-                scale_side(3)
+            if n == LAST - 1:
+                group_side(0, 4)
             project_turned(n - 2, 0)
             relu_of_turned(n - 2, 0)
-            if n == 5:
-                group_side(2, 2)
+            scale_turned(n, 0, 0)
             aggregate(n - 1, 0)
             copy_agg(n - 1, 0)
             aggregate(n - 1, 1)
             copy_agg(n - 1, 1)
-            scale_turned(n, 0, 0)
             scale_turned(n, 0, 2)
             for h in range(2):
                 turn_back(n - 3, h)
                 store_back(n - 3, h)
             turn(n + 1, 0, 0)
-            if n == 4:
-                turn_side(2)
+            if n < LAST - 1:
+                turn_side(n - 2)
             project_turned(n - 2, 1)
             relu_of_turned(n - 2, 1)
-            if n == 4:
-                scale_side(2)
-            if n == SIDE_PERIOD:
-                aggregate_tile(LAST, 1)
-                copy_agg_tile(LAST, 1)
-            turn(n + 1, 0, 2)
+            if n < LAST - 1:
+                scale_side(n - 2)
+            if share:
+                widen(stop - share, stop, "scalar")
+            if n == LAST - 1:
+                turn(LAST, 0, 2)
             scale_turned(n, 1, 0)
+            if n == LAST - 1:
+                quantize_side()
             scale_turned(n, 1, 2)
 
+        aggregate_tile(LAST, 1)
+        copy_agg_tile(LAST, 1)
         free0, free1, held0, held1 = turn_names
         ring0, ring1, ring2, ring3 = bank_names
         bank_names.clear()
-        bank_names.extend([free0, free1, ring0, ring1, ring2, ring3, held0, ring0, ring1, free0, held1, ring2])
+        bank_names.extend([free0, free1, ring0, ring1, ring2, ring3, held0, held1, free0, ring1, ring0, ring2, ring3])
         quantize_agg(LAST - 2)
         quantize_rows(LAST - 1)
         project(LAST - 2, 0)
         project(LAST - 2, 1)
         turn_back(LAST - 3, 0)
-        turn_back(LAST - 3, 1)
         store_back(LAST - 3, 0)
-        store_back(LAST - 3, 1)
         scale_turned(LAST, 0, 0)
+        add_bias(LAST - 2, 0)
         quantize_agg(LAST, 1, 1)
-        aggregate(LAST - 1, 0)
-        copy_agg(LAST - 1, 0)
         quantize_rows(LAST, 0, 2)
         scale_turned(LAST, 0, 2)
-        add_bias(LAST - 2, 0)
+        add_bias(LAST - 2, 1)
+        quantize_rows(LAST, 2, 2)
+        relu_store(LAST - 2, 0)
+        aggregate(LAST - 1, 0)
+        copy_agg(LAST - 1, 0)
         aggregate(LAST - 1, 1)
         copy_agg(LAST - 1, 1)
-        quantize_rows(LAST, 2, 2)
+        turn_back(LAST - 3, 1)
         project(LAST, 1)
-        aggregate_tile(LAST, 0)
-        add_bias(LAST - 2, 1)
-        relu_store(LAST - 2, 0)
-        quantize_agg(LAST - 1)
-        add_bias(LAST, 1)
         relu_store(LAST - 2, 1)
-        copy_agg_tile(LAST, 0)
+        add_bias(LAST, 1)
+        quantize_agg(LAST - 1)
+        store_back(LAST - 3, 1)
+        aggregate_tile(LAST, 0)
         project(LAST - 1, 0)
         project(LAST - 1, 1)
+        copy_agg_tile(LAST, 0)
         relu_store(LAST, 1)
         add_bias(LAST - 1, 0)
         quantize_agg(LAST, 0, 1)

@@ -28,6 +28,7 @@ FIRST = 2048
 SECOND_SHARE = 768
 SHARE = 512
 HALVED = 2
+BIAS_MATMULS = 2
 FLOPS = 2 * NODES * NODES * D + 2 * NODES * D * D
 
 
@@ -93,18 +94,26 @@ def tile_net_pa_w4_kernel(tc, A_bytes, A_scale, features, Wg_words, Wg_scales, b
                     in_=Wg_scales.rearrange("g q n -> (g q) n")[4 * q : 4 * q + 4, :].bitcast(I32),
                 )
 
-        def spread_bias():
-            bank = next_bank([P, 4, P], F32)
-            for t in range(4):
+        bias_bank = next_bank([P, 4, P], F32)
+
+        def spread_bias(slots):
+            for t in slots:
                 column = bias_cols[:, t : t + 1].to_broadcast([P, P])
-                nc.tensor.matmul(bank[:, t, :], lhsT=column, rhs=ident[:], start=True, stop=True)
-            nc.scalar.copy(out=bias_row[:].rearrange("p (n t) -> p n t", t=4), in_=bank[:].rearrange("p t n -> p n t"))
+                nc.tensor.matmul(bias_bank[:, t, :], lhsT=column, rhs=ident[:], start=True, stop=True)
+
+        def copy_bias():
+            nc.scalar.copy(
+                out=bias_row[:].rearrange("p (n t) -> p n t", t=4), in_=bias_bank[:].rearrange("p t n -> p n t")
+            )
 
         def bias_to_partitions():
             bank = next_bank([P, 4, P], F32)
             for c in range(4):
                 chunk = bias_row[:, c * P : (c + 1) * P]
-                nc.tensor.matmul(bank[:, c, :], lhsT=chunk, rhs=ident[:], start=True, stop=True)
+                if c < BIAS_MATMULS:
+                    nc.tensor.matmul(bank[:, c, :], lhsT=chunk, rhs=ident[:], start=True, stop=True)
+                else:
+                    nc.tensor.transpose(bank[:, c, :], chunk, ident[:])
             nc.scalar.copy(out=bias_chunks[:].rearrange("p (c o) -> p c o", o=1), in_=bank[:, :, 0:1])
 
         f_grouped = {}
@@ -178,7 +187,7 @@ def tile_net_pa_w4_kernel(tc, A_bytes, A_scale, features, Wg_words, Wg_scales, b
             key = (n, half if n < HALVED else 0)
             if key not in grouped:
                 if n < HALVED:
-                    name = "stage%d" % ((n + 2) % 3) if half == 0 else "upper%d" % n
+                    name = "stage2" if (n, half) == (0, 0) else "half%d%d" % (n, half)
                     grouped[key] = keep.tile([P, PASSES, P, 4], BF16, name=name, align_bytes=64)
                 else:
                     grouped[key] = ring("grouped", n, 2, [P, 2 * PASSES, P, 4], BF16)
@@ -189,8 +198,8 @@ def tile_net_pa_w4_kernel(tc, A_bytes, A_scale, features, Wg_words, Wg_scales, b
             scales = scale_cols[:, passes, :].rearrange("p g (u e) -> p g u e", u=2)
             tile = grouped_tile(n, first // 2)
             g0 = first % 2 if n < HALVED else first
-            if n == LAST:
-                dst = tile[:, passes]
+            if n >= LAST - 1:
+                dst = tile[:, PASSES * h + first : PASSES * h + first + count]
             else:
                 dst = tile[:].rearrange("p (g h) i t -> p h g i t", h=2)[:, h, g0 : g0 + count]
             nc.vector.tensor_tensor(
@@ -249,6 +258,7 @@ def tile_net_pa_w4_kernel(tc, A_bytes, A_scale, features, Wg_words, Wg_scales, b
             return agg_bf[n]
 
         def aggregate_tile(n, h, passes=range(PASSES)):
+            side = (n, h) == (LAST, 1)
             if (n, h) not in agg_banks:
                 agg_banks[n, h] = next_bank([P, 4, P], F32)
             for g in passes:
@@ -257,8 +267,8 @@ def tile_net_pa_w4_kernel(tc, A_bytes, A_scale, features, Wg_words, Wg_scales, b
                         out=agg_banks[n, h][:, t, :],
                         lhsT=f_codes[g][:, t * P : (t + 1) * P].bitcast(FP8X4),
                         lhsT_scale=f_scales[g][:, t * P : (t + 1) * P],
-                        rhs=(side_codes[:, g, :] if h == 1 else a_codes[n][:, g, :]).bitcast(FP8X4),
-                        rhs_scale=side_scales[:, g, :] if h == 1 else a_scales[n][:, g, :],
+                        rhs=(side_codes[:, g] if side else a_codes[n][:, PASSES * h + g]).bitcast(FP8X4),
+                        rhs_scale=side_scales[:, g] if side else a_scales[n][:, PASSES * h + g],
                         start=(g == 0 and t == 0),
                         stop=(g == PASSES - 1 and t == 3),
                     )
@@ -404,9 +414,9 @@ def tile_net_pa_w4_kernel(tc, A_bytes, A_scale, features, Wg_words, Wg_scales, b
         nc.sync.dma_start(out=scale_cols[:], in_=A_scale.rearrange("o (g p t) -> p (o g) t", p=P, t=4))
         load_a(0, 1, NODES // 2, NODES)
         load_a(1, 0)
+        nc.sync.dma_start(out=bias_raw[:], in_=bg.rearrange("(p t) -> p t", t=4))
         load_f(0)
         load_a(1, 1)
-        nc.sync.dma_start(out=bias_raw[:], in_=bg.rearrange("(p t) -> p t", t=4))
         load_f(1)
         load_pair(2)
         load_f(2)
@@ -431,8 +441,10 @@ def tile_net_pa_w4_kernel(tc, A_bytes, A_scale, features, Wg_words, Wg_scales, b
         scale_turned(0, 0, 1, 1)
         scale_turned(0, 0, 2)
         widen(PAIR, PAIR + NODES, "gpsimd")
-        for g in range(PASSES):
+        for g in range(PASSES - 1):
             features_tile(g, "fgrouped%d" % g)
+        nc.scalar.copy(out=bias_cols[:], in_=bias_raw[:])
+        spread_bias((0, 1))
         group_features_by_copy(0)
         for q in range(2, 5):
             widen(PAIR + q * QUARTER, PAIR + (q + 1) * QUARTER, "scalar")
@@ -440,7 +452,6 @@ def tile_net_pa_w4_kernel(tc, A_bytes, A_scale, features, Wg_words, Wg_scales, b
         scale_turned(0, 1, 2)
         turn(1, 0, 0)
         turn(1, 0, 2)
-        nc.scalar.copy(out=bias_cols[:], in_=bias_raw[:])
         group_features_by_copy(1)
 
         quantize_rows(0, 0, 4)
@@ -452,7 +463,8 @@ def tile_net_pa_w4_kernel(tc, A_bytes, A_scale, features, Wg_words, Wg_scales, b
         turn(1, 1, 2)
         scale_turned(1, 0, 0)
         turn(2, 0, 0)
-        spread_bias()
+        spread_bias((2, 3))
+        copy_bias()
         widen(3 * PAIR, 3 * PAIR + QUARTER, "scalar")
         nc.scalar.copy(out=side_wide[:], in_=side_bytes[:].bitcast(FP8))
         aggregate(0, 0, (0,))
@@ -463,6 +475,7 @@ def tile_net_pa_w4_kernel(tc, A_bytes, A_scale, features, Wg_words, Wg_scales, b
         turn(2, 0, 2)
 
         quantize_features(1)
+        features_tile(3, "stage0")
         group_features_on_vector(3)
         quantize_features(2)
         quantize_features(3)
@@ -533,50 +546,52 @@ def tile_net_pa_w4_kernel(tc, A_bytes, A_scale, features, Wg_words, Wg_scales, b
             scale_turned(n, 1, 0)
             if n == LAST - 1:
                 quantize_side()
+                quantize_rows(n, 0, PASSES)
             scale_turned(n, 1, 2)
 
-        aggregate_tile(LAST, 1)
-        copy_agg_tile(LAST, 1)
         free0, free1, held0, held1 = turn_names
         ring0, ring1, ring2, ring3 = bank_names
         bank_names.clear()
-        bank_names.extend([free0, free1, ring0, ring1, ring2, ring3, held0, held1, free0, ring1, ring0, ring2, ring3])
+        bank_names.extend([free0, ring0, ring1, free1, ring2, ring3, free0, held0, ring0, ring2, held1, ring3, free0])
+        aggregate_tile(LAST, 1)
+        copy_agg_tile(LAST, 1)
         quantize_agg(LAST - 2)
-        quantize_rows(LAST - 1)
+        scale_turned(LAST, 0, 0)
+        quantize_rows(LAST - 1, PASSES, PASSES)
+        aggregate_tile(LAST - 1, 0)
         project(LAST - 2, 0)
         project(LAST - 2, 1)
         turn_back(LAST - 3, 0)
+        copy_agg_tile(LAST - 1, 0)
         store_back(LAST - 3, 0)
-        scale_turned(LAST, 0, 0)
-        add_bias(LAST - 2, 0)
         quantize_agg(LAST, 1, 1)
         quantize_rows(LAST, 0, 2)
         scale_turned(LAST, 0, 2)
-        add_bias(LAST - 2, 1)
+        quantize_agg(LAST - 1, 0, 1)
+        add_bias(LAST - 2, 0)
         quantize_rows(LAST, 2, 2)
-        relu_store(LAST - 2, 0)
-        aggregate(LAST - 1, 0)
-        copy_agg(LAST - 1, 0)
-        aggregate(LAST - 1, 1)
-        copy_agg(LAST - 1, 1)
+        add_bias(LAST - 2, 1)
         turn_back(LAST - 3, 1)
+        store_back(LAST - 3, 1)
+        aggregate_tile(LAST - 1, 1)
+        relu_store(LAST - 2, 0)
+        copy_agg_tile(LAST - 1, 1)
         project(LAST, 1)
+        project(LAST - 1, 0)
         relu_store(LAST - 2, 1)
         add_bias(LAST, 1)
-        quantize_agg(LAST - 1)
-        store_back(LAST - 3, 1)
-        aggregate_tile(LAST, 0)
-        project(LAST - 1, 0)
-        project(LAST - 1, 1)
-        copy_agg_tile(LAST, 0)
-        relu_store(LAST, 1)
+        quantize_agg(LAST - 1, 1, 1)
         add_bias(LAST - 1, 0)
+        aggregate_tile(LAST, 0)
+        project(LAST - 1, 1)
+        relu_store(LAST, 1)
+        copy_agg_tile(LAST, 0)
+        relu_store(LAST - 1, 0)
+        add_bias(LAST - 1, 1)
         quantize_agg(LAST, 0, 1)
         parts = finish_in_halves(LAST, 0)
-        add_bias(LAST - 1, 1)
-        relu_store(LAST - 1, 0)
+        relu_store(LAST - 1, 1)
         add_half(parts, 0)
         add_half(parts, 1)
-        relu_store(LAST - 1, 1)
         relu_store_half(LAST, 0, parts, 0, "vector")
         relu_store_half(LAST, 0, parts, 1, "vector")

@@ -24,11 +24,10 @@ PASSES = NODES // PASS
 PAIRS = NODES // (2 * P)
 LAST = PAIRS - 1
 TURN_BANKS = 4
-FIRST = 2048
-SECOND_SHARE = 768
-SHARE = 512
+SECOND_SHARE = 1024
+SHARE = 768
 HALVED = 2
-BIAS_MATMULS = 2
+BIAS_MATMULS = 4
 FLOPS = 2 * NODES * NODES * D + 2 * NODES * D * D
 
 
@@ -57,6 +56,7 @@ def tile_net_pa_w4_kernel(tc, A_bytes, A_scale, features, Wg_words, Wg_scales, b
         side_grouped = keep.tile([P, PASSES, P, 4], BF16, name="sidegrouped", align_bytes=64)
         side_codes = keep.tile([P, PASSES, P], U32, name="sidecodes", align_bytes=64)
         side_scales = keep.tile([P, PASSES, P], U8, name="sidescales", align_bytes=64)
+        last_planes = keep.tile([P, 2, 2, P, 2], BF16, name="lastplanes", align_bytes=64)
         ident = keep.tile([P, P], F32, name="ident", align_bytes=64)
 
         bank_names = ["other%d" % b for b in range(8 - TURN_BANKS)]
@@ -230,6 +230,22 @@ def tile_net_pa_w4_kernel(tc, A_bytes, A_scale, features, Wg_words, Wg_scales, b
             nc.scalar.copy(
                 out=side_grouped[:, part].bitcast(F32),
                 in_=side_planes[:, part].rearrange("p g u i e -> p g u (i e)").bitcast(F32).rearrange("p g u i -> p g i u"),
+            )
+
+        def scale_on_scalar(g):
+            values = turned[LAST, 0, g][:].bitcast(BF16).rearrange("p u o (i e) -> p u (o i) e", e=2)
+            for t in range(4):
+                nc.scalar.activation(
+                    out=last_planes[:, g % 2, t // 2, :, t % 2],
+                    in_=values[:, t // 2, :, t % 2],
+                    func=ACT.Copy,
+                    scale=scale_cols[:, g, t : t + 1],
+                )
+
+        def group_on_scalar(g):
+            nc.scalar.copy(
+                out=grouped_tile(LAST, 0)[:, g].bitcast(F32),
+                in_=last_planes[:, g % 2].rearrange("p u i e -> p u (i e)").bitcast(F32).rearrange("p u i -> p i u"),
             )
 
         def quantize_side():
@@ -542,43 +558,46 @@ def tile_net_pa_w4_kernel(tc, A_bytes, A_scale, features, Wg_words, Wg_scales, b
             if share:
                 widen(stop - share, stop, "scalar")
             if n == LAST - 1:
-                turn(LAST, 0, 2)
+                turn(LAST, 0, 3, 1)
             scale_turned(n, 1, 0)
             if n == LAST - 1:
                 quantize_side()
                 quantize_rows(n, 0, PASSES)
             scale_turned(n, 1, 2)
 
-        free0, free1, held0, held1 = turn_names
+        turn(LAST, 0, 2, 1)
+        free0, held0, held3, held2 = turn_names
         ring0, ring1, ring2, ring3 = bank_names
         bank_names.clear()
-        bank_names.extend([free0, ring0, ring1, free1, ring2, ring3, free0, held0, ring0, ring2, held1, ring3, free0])
+        bank_names.extend([ring0, ring1, free0, ring2, ring3, ring0, held3, held0, ring1, ring2, free0, held2, ring3])
         aggregate_tile(LAST, 1)
         copy_agg_tile(LAST, 1)
+        scale_on_scalar(3)
         quantize_agg(LAST - 2)
-        scale_turned(LAST, 0, 0)
-        quantize_rows(LAST - 1, PASSES, PASSES)
-        aggregate_tile(LAST - 1, 0)
         project(LAST - 2, 0)
         project(LAST - 2, 1)
+        scale_turned(LAST, 0, 0)
+        add_bias(LAST - 2, 0)
+        quantize_rows(LAST - 1, PASSES, PASSES)
+        aggregate_tile(LAST - 1, 0)
         turn_back(LAST - 3, 0)
+        relu_store(LAST - 2, 0)
         copy_agg_tile(LAST - 1, 0)
+        group_on_scalar(3)
         store_back(LAST - 3, 0)
         quantize_agg(LAST, 1, 1)
+        scale_turned(LAST, 0, 2, 1)
         quantize_rows(LAST, 0, 2)
-        scale_turned(LAST, 0, 2)
-        quantize_agg(LAST - 1, 0, 1)
-        add_bias(LAST - 2, 0)
-        quantize_rows(LAST, 2, 2)
         add_bias(LAST - 2, 1)
+        quantize_agg(LAST - 1, 0, 1)
+        quantize_rows(LAST, 2, 2)
         turn_back(LAST - 3, 1)
         store_back(LAST - 3, 1)
         aggregate_tile(LAST - 1, 1)
-        relu_store(LAST - 2, 0)
         copy_agg_tile(LAST - 1, 1)
+        relu_store(LAST - 2, 1)
         project(LAST, 1)
         project(LAST - 1, 0)
-        relu_store(LAST - 2, 1)
         add_bias(LAST, 1)
         quantize_agg(LAST - 1, 1, 1)
         add_bias(LAST - 1, 0)

@@ -40,7 +40,6 @@ def tile_net_pa_w4_kernel(tc, A_bytes, A_scale, features, Wg_words, Wg_scales, b
 
         a_bytes = keep.tile([P, (2 * PAIRS - 1) * NODES], U8, name="abytes", align_bytes=64)
         scale_cols = keep.tile([P, PASSES, 4], F32, name="scalecols")
-        ones = keep.tile([P, 1], F32, name="ones")
         bias_raw = keep.tile([P, 4], BF16, name="biasraw")
         bias_cols = keep.tile([P, 4], F32, name="biascols")
         bias_row = keep.tile([P, D], F32, name="biasrow", align_bytes=64)
@@ -157,24 +156,14 @@ def tile_net_pa_w4_kernel(tc, A_bytes, A_scale, features, Wg_words, Wg_scales, b
             src = a_bytes[:, first:last].bitcast(FP8)
             if engine == "scalar":
                 nc.scalar.copy(out=wide_columns(first, last), in_=src)
+            elif engine == "vector":
+                nc.vector.tensor_copy(out=wide_columns(first, last), in_=src)
             else:
                 nc.gpsimd.tensor_copy(out=wide_columns(first, last), in_=src)
 
-        def widen_parted(g):
-            nc.vector.tensor_scalar(
-                out=wide_columns(g * PASS, (g + 1) * PASS).rearrange("p (u q e) -> p q u e", u=2, e=2),
-                in0=a_bytes[:, g * PASS : (g + 1) * PASS].bitcast(FP8).rearrange("p (q u e) -> p q u e", u=2, e=2),
-                scalar1=ones[:],
-                scalar2=None,
-                op0=ALU.mult,
-            )
-
         def word_columns(n, h, g, u):
             first = (2 * n + h) * NODES + g * PASS
-            words = wide_columns(first, first + PASS).bitcast(F32)
-            if n == 0 and h == 0:
-                return words[:, P * u : P * (u + 1)]
-            return words[:, u : 2 * P : 2]
+            return wide_columns(first, first + PASS).bitcast(F32)[:, u : 2 * P : 2]
 
         def turn(n, h, first, count=2):
             bank = next_bank([P, 2, count, P], F32, turn_names)
@@ -421,11 +410,10 @@ def tile_net_pa_w4_kernel(tc, A_bytes, A_scale, features, Wg_words, Wg_scales, b
             store(n, h, rows)
 
         make_identity(nc, ident[:])
-        nc.vector.memset(ones[:], 1.0)
         nc.vector.memset(w_scales[:].bitcast(I32), 0)
 
-        load_a(0, 0, 0, NODES // 2)
-        load_a(0, 0, NODES // 2, NODES)
+        load_a(0, 0, 0, PASS)
+        load_a(0, 0, PASS, NODES)
         load_a(0, 1, 0, NODES // 2)
         nc.sync.dma_start(out=scale_cols[:], in_=A_scale.rearrange("o (g p t) -> p (o g) t", p=P, t=4))
         load_a(0, 1, NODES // 2, NODES)
@@ -444,18 +432,16 @@ def tile_net_pa_w4_kernel(tc, A_bytes, A_scale, features, Wg_words, Wg_scales, b
             load_pair(n)
         load_a(LAST, 0)
 
-        for g in range(PASSES):
-            widen_parted(g)
+        widen(0, PASS, "vector")
+        widen(PASS, 2 * PASS, "vector")
+        widen(2 * PASS, NODES, "vector")
         widen(2 * QUARTER, 3 * QUARTER, "scalar")
         widen(3 * QUARTER, 4 * QUARTER, "scalar")
-        turn(0, 0, 0, 1)
-        turn(0, 0, 1, 1)
-        turn(0, 0, 2)
-        turn(0, 1, 0)
-        scale_turned(0, 0, 0, 1)
-        turn(0, 1, 2)
-        scale_turned(0, 0, 1, 1)
-        scale_turned(0, 0, 2)
+        for g in range(PASSES):
+            turn(0, 0, g, 1)
+        for g in range(PASSES):
+            scale_turned(0, 0, g, 1)
+            turn(0, 1, g, 1)
         widen(PAIR, PAIR + NODES, "gpsimd")
         for g in range(PASSES - 1):
             features_tile(g, "fgrouped%d" % g)
@@ -464,8 +450,8 @@ def tile_net_pa_w4_kernel(tc, A_bytes, A_scale, features, Wg_words, Wg_scales, b
         group_features_by_copy(0)
         for q in range(2, 5):
             widen(PAIR + q * QUARTER, PAIR + (q + 1) * QUARTER, "scalar")
-        scale_turned(0, 1, 0)
-        scale_turned(0, 1, 2)
+        for g in range(PASSES):
+            scale_turned(0, 1, g, 1)
         turn(1, 0, 0)
         turn(1, 0, 2)
         group_features_by_copy(1)

@@ -24,8 +24,8 @@ PASSES = NODES // PASS
 PAIRS = NODES // (2 * P)
 LAST = PAIRS - 1
 TURN_BANKS = 4
-SECOND_SHARE = 1024
-SHARE = 768
+SECOND_SHARE = 768
+SHARE = 512
 HALVED = 2
 BIAS_MATMULS = 4
 FLOPS = 2 * NODES * NODES * D + 2 * NODES * D * D

@@ -27,7 +27,9 @@ TURN_BANKS = 4
 SECOND_SHARE = 768
 SHARE = 512
 HALVED = 2
-BIAS_MATMULS = 4
+BIAS_MATMULS = 3
+BY_TILE = ()
+SPLIT = 64
 FLOPS = 2 * NODES * NODES * D + 2 * NODES * D * D
 
 
@@ -120,17 +122,17 @@ def tile_net_pa_w4_kernel(tc, A_bytes, A_scale, features, Wg_words, Wg_scales, b
         def features_tile(g, name):
             f_grouped[g] = keep.tile([P, 4, P, 4], BF16, name=name, align_bytes=64)
 
-        def group_features_by_copy(g):
-            nc.scalar.copy(
-                out=f_grouped[g][:].rearrange("p t m j -> p m t j"),
-                in_=f_raw[g][:].rearrange("p j (m t) -> p m t j", t=4),
-            )
+        def group_features(g, engine, first=0, last=P):
+            dst = f_grouped[g][:].rearrange("p t m j -> p m t j")[:, first:last]
+            src = f_raw[g][:].rearrange("p j (m t) -> p m t j", t=4)[:, first:last]
+            if engine == "scalar":
+                nc.scalar.copy(out=dst, in_=src)
+            else:
+                nc.vector.tensor_copy(out=dst, in_=src)
 
-        def group_features_on_vector(g):
-            nc.vector.tensor_copy(
-                out=f_grouped[g][:].rearrange("p t m j -> p m t j"),
-                in_=f_raw[g][:].rearrange("p j (m t) -> p m t j", t=4),
-            )
+        def widen_side(g):
+            cols = slice(g * PASS, (g + 1) * PASS)
+            nc.scalar.copy(out=side_wide[:, cols], in_=side_bytes[:, cols].bitcast(FP8))
 
         def quantize_features(g):
             nc.vector.quantize_mx(
@@ -143,7 +145,7 @@ def tile_net_pa_w4_kernel(tc, A_bytes, A_scale, features, Wg_words, Wg_scales, b
         agg_banks, agg_bf, agg_codes, agg_scales = {}, {}, {}, {}
         product, relu_turned, summed, back, side_banks = {}, {}, {}, {}, {}
 
-        starts = [0, PAIR] + [n * PAIR + QUARTER for n in range(2, LAST)] + [LAST * PAIR, LAST * PAIR + NODES]
+        starts = [0, PAIR, 2 * PAIR] + [n * PAIR + QUARTER for n in range(3, LAST)] + [LAST * PAIR, LAST * PAIR + NODES]
 
         def wide_columns(first, last):
             n = max(m for m in range(PAIRS) if starts[m] <= first)
@@ -262,26 +264,29 @@ def tile_net_pa_w4_kernel(tc, A_bytes, A_scale, features, Wg_words, Wg_scales, b
                 agg_bf[n] = keep.tile([P, 2, P, 4], BF16, name=name, align_bytes=64)
             return agg_bf[n]
 
-        def aggregate_tile(n, h, passes=range(PASSES)):
+        def aggregate_tile(n, h, passes=range(PASSES), order=range(PASSES)):
             side = (n, h) == (LAST, 1)
             if (n, h) not in agg_banks:
                 agg_banks[n, h] = next_bank([P, 4, P], F32)
             for g in passes:
+                slot = PASSES * h + g if n >= LAST - 1 else 2 * g + h
                 for t in range(4):
                     nc.tensor.matmul_mx(
                         out=agg_banks[n, h][:, t, :],
                         lhsT=f_codes[g][:, t * P : (t + 1) * P].bitcast(FP8X4),
                         lhsT_scale=f_scales[g][:, t * P : (t + 1) * P],
-                        rhs=(side_codes[:, g] if side else a_codes[n][:, PASSES * h + g]).bitcast(FP8X4),
-                        rhs_scale=side_scales[:, g] if side else a_scales[n][:, PASSES * h + g],
-                        start=(g == 0 and t == 0),
-                        stop=(g == PASSES - 1 and t == 3),
+                        rhs=(side_codes[:, g] if side else a_codes[n][:, slot]).bitcast(FP8X4),
+                        rhs_scale=side_scales[:, g] if side else a_scales[n][:, slot],
+                        start=(g == order[0] and t == 0),
+                        stop=(g == order[-1] and t == 3),
                     )
 
         def copy_agg_tile(n, h):
             nc.scalar.copy(out=agg_tile(n)[:, h], in_=agg_banks[n, h][:].rearrange("p t i -> p i t"))
 
         def aggregate(n, half, passes=range(PASSES), order=range(PASSES)):
+            if n in BY_TILE:
+                return aggregate_tile(n, half, passes, order)
             if (n, half) not in agg_banks:
                 agg_banks[n, half] = next_bank([P, 2, 2 * P], F32)
             for g in passes:
@@ -298,6 +303,8 @@ def tile_net_pa_w4_kernel(tc, A_bytes, A_scale, features, Wg_words, Wg_scales, b
                     )
 
         def copy_agg(n, half):
+            if n in BY_TILE:
+                return copy_agg_tile(n, half)
             nc.scalar.copy(
                 out=agg_tile(n)[:].rearrange("p h i t -> p (h i) t")[:, :, 2 * half : 2 * half + 2],
                 in_=agg_banks[n, half][:].rearrange("p t i -> p i t"),
@@ -443,55 +450,60 @@ def tile_net_pa_w4_kernel(tc, A_bytes, A_scale, features, Wg_words, Wg_scales, b
             scale_turned(0, 0, g, 1)
             turn(0, 1, g, 1)
         widen(PAIR, PAIR + NODES, "gpsimd")
-        for g in range(PASSES - 1):
+        for g in (0, 1, 3):
             features_tile(g, "fgrouped%d" % g)
-        nc.scalar.copy(out=bias_cols[:], in_=bias_raw[:])
+        nc.scalar.copy(out=bias_cols[:, :2], in_=bias_raw[:, :2])
         spread_bias((0, 1))
-        group_features_by_copy(0)
-        for q in range(2, 5):
+        group_features(0, "scalar")
+        for q in range(2, 4):
             widen(PAIR + q * QUARTER, PAIR + (q + 1) * QUARTER, "scalar")
         for g in range(PASSES):
             scale_turned(0, 1, g, 1)
         turn(1, 0, 0)
         turn(1, 0, 2)
-        group_features_by_copy(1)
+        group_features(1, "scalar")
+        nc.scalar.copy(out=bias_cols[:, 2:], in_=bias_raw[:, 2:])
 
         quantize_rows(0, 0, 4)
         quantize_rows(0, 4, 4)
         quantize_features(0)
-        widen(2 * PAIR + QUARTER, 3 * PAIR, "gpsimd")
-        group_features_by_copy(2)
+        widen(2 * PAIR, 3 * PAIR - SHARE, "gpsimd")
+        group_features(3, "scalar", 0, SPLIT)
+        features_tile(2, "stage0")
+        group_features(2, "scalar")
         turn(1, 1, 0)
         turn(1, 1, 2)
-        scale_turned(1, 0, 0)
-        turn(2, 0, 0)
         spread_bias((2, 3))
+        widen(3 * PAIR - SHARE, 3 * PAIR, "scalar")
         copy_bias()
         widen(3 * PAIR, 3 * PAIR + QUARTER, "scalar")
-        nc.scalar.copy(out=side_wide[:], in_=side_bytes[:].bitcast(FP8))
-        aggregate(0, 0, (0,))
-        aggregate(0, 1, (0,))
+        widen_side(0)
+        order = (0, 1, 3, 2)
+        aggregate(0, 0, (0,), order)
+        aggregate(0, 1, (0,), order)
+        scale_turned(1, 0, 0)
         scale_turned(1, 0, 2)
         scale_turned(1, 1, 0)
         scale_turned(1, 1, 2)
-        turn(2, 0, 2)
+        turn(2, 0, 0)
 
         quantize_features(1)
-        features_tile(3, "stage0")
-        group_features_on_vector(3)
-        quantize_features(2)
-        quantize_features(3)
+        group_features(3, "vector", SPLIT, P)
         quantize_rows(1, 0, 4)
+        quantize_features(3)
+        quantize_features(2)
         quantize_rows(1, 4, 4)
         widen(3 * PAIR + QUARTER, 4 * PAIR + QUARTER - SECOND_SHARE, "gpsimd")
-        for g in range(1, PASSES):
+        for g in order[1:]:
             for half in range(2):
-                aggregate(0, half, (g,))
-            if g < 3:
-                turn(2, 1, 2 * g - 2)
+                aggregate(0, half, (g,), order)
+            if g == 1:
+                turn(2, 0, 2)
+                turn(2, 1, 0)
         copy_agg(0, 0)
         copy_agg(0, 1)
         aggregate(1, 0)
+        turn(2, 1, 2)
         aggregate(1, 1)
         copy_agg(1, 0)
         copy_agg(1, 1)
@@ -526,6 +538,8 @@ def tile_net_pa_w4_kernel(tc, A_bytes, A_scale, features, Wg_words, Wg_scales, b
             project_turned(n - 2, 0)
             relu_of_turned(n - 2, 0)
             scale_turned(n, 0, 0)
+            if n < LAST - 1:
+                widen_side(n - 2)
             aggregate(n - 1, 0)
             copy_agg(n - 1, 0)
             aggregate(n - 1, 1)

@@ -21,15 +21,15 @@ PASS = 512
 QUARTER = 1024
 PAIR = 4 * QUARTER
 PASSES = NODES // PASS
-PAIRS = NODES // (2 * P)
-LAST = PAIRS - 1
+SIDE = 7
+LAST = SIDE - 1
 TURN_BANKS = 4
-SECOND_SHARE = 768
 SHARE = 512
-HALVED = 2
-BIAS_MATMULS = 3
-BY_TILE = ()
-SPLIT = 64
+UNITS = 128
+POOL_UNITS = 88
+HALVED = (0,)
+BY_TILE = (0, 1, LAST)
+RELEASES = {0: "stage1", 1: "stage2", (SIDE, 0): "sidegrouped", SIDE: "stage0"}
 FLOPS = 2 * NODES * NODES * D + 2 * NODES * D * D
 
 
@@ -40,34 +40,38 @@ def tile_net_pa_w4_kernel(tc, A_bytes, A_scale, features, Wg_words, Wg_scales, b
         psum = ctx.enter_context(tc.psum_pool(name="psum", bufs=1))
         ctx.enter_context(tc.manual_schedule())
 
-        a_bytes = keep.tile([P, (2 * PAIRS - 1) * NODES], U8, name="abytes", align_bytes=64)
+        a_bytes = keep.tile([P, SIDE * PAIR], U8, name="abytes", align_bytes=64)
+        side_bytes = keep.tile([P, PAIR], U8, name="sidebytes", align_bytes=64)
         scale_cols = keep.tile([P, PASSES, 4], F32, name="scalecols")
-        bias_raw = keep.tile([P, 4], BF16, name="biasraw")
-        bias_cols = keep.tile([P, 4], F32, name="biascols")
-        bias_row = keep.tile([P, D], F32, name="biasrow", align_bytes=64)
+        bias_raw = keep.tile([P, 4, 2], BF16, name="biasraw")
         bias_chunks = keep.tile([P, 4], F32, name="biaschunks")
-        f_raw = [keep.tile([P, 4, D], BF16, name="fraw%d" % g, align_bytes=64) for g in range(PASSES)]
-        f_codes = [keep.tile([P, D], U32, name="fcodes%d" % g, align_bytes=64) for g in range(PASSES)]
-        f_scales = [keep.tile([P, D], U8, name="fscales%d" % g, align_bytes=64) for g in range(PASSES)]
+        bias_row = keep.tile([P, D], F32, name="biasrow", align_bytes=64)
+        f_raw = [keep.tile([P, 4, D], BF16, name="fraw%d" % g, align_bytes=64) for g in range(2)]
+        f_raw_late = keep.tile([P, 4, 2 * D], BF16, name="frawlate", align_bytes=64)
+        f_codes = [keep.tile([P, 4, P], U32, name="fcodes%d" % g, align_bytes=64) for g in range(2)]
+        f_scales = [keep.tile([P, 4, P], U8, name="fscales%d" % g, align_bytes=64) for g in range(2)]
+        f_codes_late = keep.tile([P, 4, 2 * P], U32, name="fcodeslate", align_bytes=64)
+        f_scales_late = keep.tile([P, 4, 2 * P], U8, name="fscaleslate", align_bytes=64)
         w_words = keep.tile([P, 2 * D], U8, name="wwords", align_bytes=64)
         w_scales = keep.tile([P, D], U8, name="wscales", align_bytes=64)
-        side_bytes = keep.tile([P, NODES], U8, name="sidebytes", align_bytes=64)
-        side_wide = keep.tile([P, NODES], BF16, name="sidewide", align_bytes=64)
-        side_planes = keep.tile([P, PASSES, 2, P, 2], BF16, name="sideplanes", align_bytes=64)
-        side_grouped = keep.tile([P, PASSES, P, 4], BF16, name="sidegrouped", align_bytes=64)
-        side_codes = keep.tile([P, PASSES, P], U32, name="sidecodes", align_bytes=64)
-        side_scales = keep.tile([P, PASSES, P], U8, name="sidescales", align_bytes=64)
-        last_planes = keep.tile([P, 2, 2, P, 2], BF16, name="lastplanes", align_bytes=64)
+        side_wide = keep.tile([P, PAIR], BF16, name="sidewide", align_bytes=64)
         ident = keep.tile([P, P], F32, name="ident", align_bytes=64)
+        ident_bf = keep.tile([P, P], BF16, name="identbf", align_bytes=64)
 
         bank_names = ["other%d" % b for b in range(8 - TURN_BANKS)]
         turn_names = ["turn%d" % b for b in range(TURN_BANKS)]
 
-        def next_bank(shape, dtype, names=bank_names):
+        held = {}
+
+        def take_bank(key, shape, names=bank_names, dtype=F32):
             name = names[0]
             names.remove(name)
-            names.append(name)
+            held[key] = (name, names)
             return psum.tile(shape, dtype, name=name)
+
+        def give_bank(key, names=None):
+            name, home = held[key]
+            (home if names is None else names).append(name)
 
         def ring(name, index, depth, shape, dtype):
             return keep.tile(shape, dtype, name="%s%d" % (name, index % depth), align_bytes=64)
@@ -79,13 +83,15 @@ def tile_net_pa_w4_kernel(tc, A_bytes, A_scale, features, Wg_words, Wg_scales, b
             )
 
         def load_pair(n):
+            dst = side_bytes[:] if n == SIDE else a_bytes[:, n * PAIR : (n + 1) * PAIR]
             nc.sync.dma_start(
-                out=a_bytes[:, 2 * n * NODES : 2 * (n + 1) * NODES].rearrange("p (h k) -> p h k", h=2),
+                out=dst.rearrange("p (h k) -> p h k", h=2),
                 in_=A_bytes[2 * n * P : 2 * (n + 1) * P, :].rearrange("(h p) k -> p h k", p=P),
             )
 
         def load_f(g):
-            nc.sync.dma_start(out=f_raw[g][:], in_=features.rearrange("(g p j) c -> g p j c", p=P, j=4)[g])
+            dst = f_raw[g][:] if g < 2 else f_raw_late[:, :, (g - 2) * D : (g - 1) * D]
+            nc.sync.dma_start(out=dst, in_=features.rearrange("(g p j) c -> g p j c", p=P, j=4)[g])
 
         def load_w():
             nc.sync.dma_start(out=w_words[:], in_=Wg_words.rearrange("g p w -> p (g w)"))
@@ -95,155 +101,179 @@ def tile_net_pa_w4_kernel(tc, A_bytes, A_scale, features, Wg_words, Wg_scales, b
                     in_=Wg_scales.rearrange("g q n -> (g q) n")[4 * q : 4 * q + 4, :].bitcast(I32),
                 )
 
-        bias_bank = next_bank([P, 4, P], F32)
+        bias_banks = []
 
-        def spread_bias(slots):
-            for t in slots:
-                column = bias_cols[:, t : t + 1].to_broadcast([P, P])
-                nc.tensor.matmul(bias_bank[:, t, :], lhsT=column, rhs=ident[:], start=True, stop=True)
+        def spread_bias(chunks):
+            if not bias_banks:
+                bias_banks.append(take_bank("bias", [P, 4, P]))
+            for c in chunks:
+                column = bias_chunks[:, c : c + 1].to_broadcast([P, P])
+                nc.tensor.matmul(bias_banks[0][:, c, :], lhsT=column, rhs=ident[:], start=True, stop=True)
 
         def copy_bias():
-            nc.scalar.copy(
-                out=bias_row[:].rearrange("p (n t) -> p n t", t=4), in_=bias_bank[:].rearrange("p t n -> p n t")
-            )
+            nc.scalar.copy(out=bias_row[:], in_=bias_banks[0][:].rearrange("p c n -> p (c n)"))
+            give_bank("bias")
 
-        def bias_to_partitions():
-            bank = next_bank([P, 4, P], F32)
-            for c in range(4):
-                chunk = bias_row[:, c * P : (c + 1) * P]
-                if c < BIAS_MATMULS:
-                    nc.tensor.matmul(bank[:, c, :], lhsT=chunk, rhs=ident[:], start=True, stop=True)
-                else:
-                    nc.tensor.transpose(bank[:, c, :], chunk, ident[:])
-            nc.scalar.copy(out=bias_chunks[:].rearrange("p (c o) -> p c o", o=1), in_=bank[:, :, 0:1])
+        def copy_on(engine, dst, src):
+            if engine == "scalar":
+                nc.scalar.copy(out=dst, in_=src)
+            elif engine == "vector":
+                nc.vector.tensor_copy(out=dst, in_=src)
+            else:
+                nc.gpsimd.tensor_copy(out=dst, in_=src)
 
         f_grouped = {}
 
-        def features_tile(g, name):
-            f_grouped[g] = keep.tile([P, 4, P, 4], BF16, name=name, align_bytes=64)
-
-        def group_features(g, engine, first=0, last=P):
-            dst = f_grouped[g][:].rearrange("p t m j -> p m t j")[:, first:last]
-            src = f_raw[g][:].rearrange("p j (m t) -> p m t j", t=4)[:, first:last]
-            if engine == "scalar":
-                nc.scalar.copy(out=dst, in_=src)
-            else:
-                nc.vector.tensor_copy(out=dst, in_=src)
-
-        def widen_side(g):
-            cols = slice(g * PASS, (g + 1) * PASS)
-            nc.scalar.copy(out=side_wide[:, cols], in_=side_bytes[:, cols].bitcast(FP8))
+        def group_features(g, engine, first, last):
+            raw = f_raw[g] if g < 2 else f_raw_late
+            dst = f_grouped[g][:].rearrange("p t (m i) j -> p m t i j", i=2)[:, first:last]
+            src = raw[:].rearrange("p j (m i t) -> p m t i j", i=2, t=4)[:, first:last]
+            copy_on(engine, dst, src)
 
         def quantize_features(g):
+            codes, scales = (f_codes[g], f_scales[g]) if g < 2 else (f_codes_late, f_scales_late)
             nc.vector.quantize_mx(
-                out=f_codes[g][:].bitcast(FP8X4),
-                scales=f_scales[g][:],
+                out=codes[:].rearrange("p t m -> p (t m)").bitcast(FP8X4),
+                scales=scales[:].rearrange("p t m -> p (t m)"),
                 in_=f_grouped[g][:].rearrange("p t m j -> p (t m j)"),
             )
 
+        def features_operand(g, t):
+            if g < 2:
+                return f_codes[g][:, t], f_scales[g][:, t]
+            cols = slice((g - 2) * P, (g - 1) * P)
+            return f_codes_late[:, t, cols], f_scales_late[:, t, cols]
+
         wide, grouped, a_codes, a_scales, turned = {}, {}, {}, {}, {}
         agg_banks, agg_bf, agg_codes, agg_scales = {}, {}, {}, {}
-        product, relu_turned, summed, back, side_banks = {}, {}, {}, {}, {}
+        product, relu_turned, summed, back, side_banks, side_planes = {}, {}, {}, {}, {}, {}
 
-        starts = [0, PAIR, 2 * PAIR] + [n * PAIR + QUARTER for n in range(3, LAST)] + [LAST * PAIR, LAST * PAIR + NODES]
+        starts = [0, PAIR, 2 * PAIR] + [n * PAIR + QUARTER for n in range(3, SIDE)] + [SIDE * PAIR]
 
         def wide_columns(first, last):
-            n = max(m for m in range(PAIRS) if starts[m] <= first)
+            n = max(m for m in range(SIDE) if starts[m] <= first)
             if n not in wide:
-                shape = [P, starts[n + 1] - starts[n]]
-                wide[n] = keep.tile(shape, BF16, name="stage%d" % (n % 3), align_bytes=64)
+                name = "stage%d" % (n % 3) if n else "wide0"
+                wide[n] = keep.tile([P, starts[n + 1] - starts[n]], BF16, name=name, align_bytes=64)
             return wide[n][:, first - starts[n] : last - starts[n]]
 
         def widen(first, last, engine):
-            src = a_bytes[:, first:last].bitcast(FP8)
-            if engine == "scalar":
-                nc.scalar.copy(out=wide_columns(first, last), in_=src)
-            elif engine == "vector":
-                nc.vector.tensor_copy(out=wide_columns(first, last), in_=src)
-            else:
-                nc.gpsimd.tensor_copy(out=wide_columns(first, last), in_=src)
+            copy_on(engine, wide_columns(first, last), a_bytes[:, first:last].bitcast(FP8))
 
-        def word_columns(n, h, g, u):
-            first = (2 * n + h) * NODES + g * PASS
-            return wide_columns(first, first + PASS).bitcast(F32)[:, u : 2 * P : 2]
+        def widen_side(g):
+            for h in range(2):
+                cols = slice(h * NODES + g * PASS, h * NODES + (g + 1) * PASS)
+                nc.scalar.copy(out=side_wide[:, cols], in_=side_bytes[:, cols].bitcast(FP8))
 
         def turn(n, h, first, count=2):
-            bank = next_bank([P, 2, count, P], F32, turn_names)
+            bank = take_bank(("turn", n, h, first), [P, 2, count, P], turn_names)
             turned[n, h, first] = bank
             for gl in range(count):
+                col = (2 * n + h) * NODES + (first + gl) * PASS
+                words = wide_columns(col, col + PASS).bitcast(F32)
                 for u in range(2):
-                    nc.tensor.transpose(bank[:, u, gl, :], word_columns(n, h, first + gl, u), ident[:])
+                    nc.tensor.transpose(bank[:, u, gl, :], words[:, u : 2 * P : 2], ident[:])
 
-        def grouped_tile(n, half):
-            key = (n, half if n < HALVED else 0)
+        by_matmul = []
+
+        def turn_by_matmul(n, h, first):
+            bank = take_bank(("turn", n, h, first), [P, 2, 4, P], turn_names, BF16)
+            turned[n, h, first] = bank
+            by_matmul.append((n, h, first))
+            for gl in range(2):
+                col = (2 * n + h) * NODES + (first + gl) * PASS
+                values = wide_columns(col, col + PASS)
+                for t in range(4):
+                    nc.tensor.matmul(bank[:, gl, t, :], lhsT=values[:, t:PASS:4], rhs=ident_bf[:], start=True, stop=True)
+
+        def by_tile(n):
+            return n in BY_TILE
+
+        def slot_of(n, h, g):
+            return PASSES * h + g if n == LAST else 2 * g + h
+
+        def grouped_slots(n, first, count, step=1):
+            width = PASSES if n in HALVED else 2 * PASSES
+            key = (n, first // width)
             if key not in grouped:
-                if n < HALVED:
-                    name = "stage2" if (n, half) == (0, 0) else "half%d%d" % (n, half)
-                    grouped[key] = keep.tile([P, PASSES, P, 4], BF16, name=name, align_bytes=64)
+                if n in HALVED:
+                    grouped[key] = keep.tile([P, width, P, 4], BF16, name=RELEASES.get(key, "half%d" % key[1]), align_bytes=64)
+                elif n == SIDE:
+                    grouped[key] = keep.tile([P, width, P, 4], BF16, name=RELEASES[key], align_bytes=64)
                 else:
-                    grouped[key] = ring("grouped", n, 2, [P, 2 * PASSES, P, 4], BF16)
-            return grouped[key]
+                    grouped[key] = ring("grouped", n, 2, [P, width, P, 4], BF16)
+            return grouped[key][:, first % width : first % width + (count - 1) * step + 1 : step]
 
         def scale_turned(n, h, first, count=2):
-            passes = slice(first, first + count)
-            scales = scale_cols[:, passes, :].rearrange("p g (u e) -> p g u e", u=2)
-            tile = grouped_tile(n, first // 2)
-            g0 = first % 2 if n < HALVED else first
-            if n >= LAST - 1:
-                dst = tile[:, PASSES * h + first : PASSES * h + first + count]
+            scales = scale_cols[:, first : first + count, :].rearrange("p g (u e) -> p g u e", u=2)
+            dst = grouped_slots(n, slot_of(n, h, first), count, 1 if n == LAST else 2)
+            if (n, h, first) in by_matmul:
+                values = turned[n, h, first][:].rearrange("p g (u e) i -> p g i u e", u=2)
             else:
-                dst = tile[:].rearrange("p (g h) i t -> p h g i t", h=2)[:, h, g0 : g0 + count]
+                values = turned[n, h, first][:].bitcast(BF16).rearrange("p u g (i e) -> p g i u e", e=2)
             nc.vector.tensor_tensor(
                 out=dst.rearrange("p g i (u e) -> p g i u e", u=2),
-                in0=turned[n, h, first][:].bitcast(BF16).rearrange("p u g (i e) -> p g i u e", e=2),
+                in0=values,
                 in1=scales.unsqueeze(2).to_broadcast([P, count, P, 2, 2]),
                 op=ALU.mult,
             )
+            give_bank(("turn", n, h, first), bank_names if n == LAST else turn_names)
 
-        def turn_side(g):
-            words = side_wide[:, g * PASS : (g + 1) * PASS].bitcast(F32)
-            side_banks[g] = next_bank([P, 2, P], F32)
-            for u in range(2):
-                nc.tensor.transpose(side_banks[g][:, u, :], words[:, u : 2 * P : 2], ident[:])
+        def turn_side(g, names=bank_names):
+            side_banks[g] = take_bank(("side", g), [P, 2, 2, P], names)
+            for h in range(2):
+                words = side_wide[:, h * NODES + g * PASS : h * NODES + (g + 1) * PASS].bitcast(F32)
+                for u in range(2):
+                    nc.tensor.transpose(side_banks[g][:, u, h, :], words[:, u : 2 * P : 2], ident[:])
 
-        def scale_side(g):
-            values = side_banks[g][:].bitcast(BF16).rearrange("p u (i e) -> p u i e", e=2)
-            for t in range(4):
+        def scale_side(g, slots=range(4)):
+            if g not in side_planes:
+                side_planes[g] = ring("sideplanes", g, 3, [P, 2, 2 * P, 2], BF16)
+            values = side_banks[g][:].bitcast(BF16).rearrange("p u h (i e) -> p u (h i) e", e=2)
+            for t in slots:
                 nc.scalar.activation(
-                    out=side_planes[:, g, t // 2, :, t % 2],
+                    out=side_planes[g][:, t // 2, :, t % 2],
                     in_=values[:, t // 2, :, t % 2],
                     func=ACT.Copy,
                     scale=scale_cols[:, g, t : t + 1],
                 )
+            if slots[-1] == 3:
+                give_bank(("side", g))
 
-        def group_side(first, count):
-            part = slice(first, first + count)
+        def scale_side_on_vector(g):
+            scales = scale_cols[:, g : g + 1, :].rearrange("p g (u e) -> p g u e", u=2)
+            nc.vector.tensor_tensor(
+                out=grouped_slots(SIDE, 2 * g, 2).rearrange("p h i (u e) -> p (h i) u e", u=2),
+                in0=side_banks[g][:].bitcast(BF16).rearrange("p u h (i e) -> p (h i) u e", e=2),
+                in1=scales.to_broadcast([P, 2 * P, 2, 2]),
+                op=ALU.mult,
+            )
+            give_bank(("side", g))
+
+        def group_side(g):
             nc.scalar.copy(
-                out=side_grouped[:, part].bitcast(F32),
-                in_=side_planes[:, part].rearrange("p g u i e -> p g u (i e)").bitcast(F32).rearrange("p g u i -> p g i u"),
+                out=grouped_slots(SIDE, 2 * g, 2).rearrange("p h i t -> p (h i) t").bitcast(F32),
+                in_=side_planes[g][:].rearrange("p u i e -> p u (i e)").bitcast(F32).rearrange("p u i -> p i u"),
             )
 
-        def scale_on_scalar(g):
-            values = turned[LAST, 0, g][:].bitcast(BF16).rearrange("p u o (i e) -> p u (o i) e", e=2)
+        def scale_on_scalar(n, h, first, g):
+            if (n, h) not in side_planes:
+                side_planes[n, h] = ring("sideplanes", 0, 3, [P, 2, 2, P, 2], BF16)
+            values = turned[n, h, first][:].bitcast(BF16).rearrange("p u g (i e) -> p g u i e", e=2)
             for t in range(4):
                 nc.scalar.activation(
-                    out=last_planes[:, g % 2, t // 2, :, t % 2],
-                    in_=values[:, t // 2, :, t % 2],
+                    out=side_planes[n, h][:, g - first, t // 2, :, t % 2],
+                    in_=values[:, g - first, t // 2, :, t % 2],
                     func=ACT.Copy,
                     scale=scale_cols[:, g, t : t + 1],
                 )
+            if g == first + 1:
+                give_bank(("turn", n, h, first), bank_names)
 
-        def group_on_scalar(g):
+        def group_on_scalar(n, h, first):
             nc.scalar.copy(
-                out=grouped_tile(LAST, 0)[:, g].bitcast(F32),
-                in_=last_planes[:, g % 2].rearrange("p u i e -> p u (i e)").bitcast(F32).rearrange("p u i -> p i u"),
-            )
-
-        def quantize_side():
-            nc.vector.quantize_mx(
-                out=side_codes[:].rearrange("p g i -> p (g i)").bitcast(FP8X4),
-                scales=side_scales[:].rearrange("p g i -> p (g i)"),
-                in_=side_grouped[:].rearrange("p g i t -> p (g i t)"),
+                out=grouped_slots(n, slot_of(n, h, first), 2).bitcast(F32),
+                in_=side_planes[n, h][:].rearrange("p g u i e -> p g u (i e)").bitcast(F32).rearrange("p g u i -> p g i u"),
             )
 
         def quantize_rows(n, first=0, count=2 * PASSES):
@@ -251,69 +281,52 @@ def tile_net_pa_w4_kernel(tc, A_bytes, A_scale, features, Wg_words, Wg_scales, b
                 a_codes[n] = ring("acodes", n, 3, [P, 2 * PASSES, P], U32)
                 a_scales[n] = ring("ascales", n, 3, [P, 2 * PASSES, P], U8)
             part = slice(first, first + count)
-            rows = grouped_tile(n, first // PASSES)[:] if n < HALVED else grouped_tile(n, 0)[:, part]
             nc.vector.quantize_mx(
                 out=a_codes[n][:, part].rearrange("p g i -> p (g i)").bitcast(FP8X4),
                 scales=a_scales[n][:, part].rearrange("p g i -> p (g i)"),
-                in_=rows.rearrange("p g i t -> p (g i t)"),
+                in_=grouped_slots(n, first, count).rearrange("p g i t -> p (g i t)"),
             )
 
         def agg_tile(n):
             if n not in agg_bf:
-                name = "stage%d" % (n % 3) if 1 <= n <= LAST - 3 else "aggbf%d" % n
+                name = RELEASES.get(n, "aggbf%d" % n)
                 agg_bf[n] = keep.tile([P, 2, P, 4], BF16, name=name, align_bytes=64)
             return agg_bf[n]
 
-        def aggregate_tile(n, h, passes=range(PASSES), order=range(PASSES)):
-            side = (n, h) == (LAST, 1)
-            if (n, h) not in agg_banks:
-                agg_banks[n, h] = next_bank([P, 4, P], F32)
-            for g in passes:
-                slot = PASSES * h + g if n >= LAST - 1 else 2 * g + h
-                for t in range(4):
-                    nc.tensor.matmul_mx(
-                        out=agg_banks[n, h][:, t, :],
-                        lhsT=f_codes[g][:, t * P : (t + 1) * P].bitcast(FP8X4),
-                        lhsT_scale=f_scales[g][:, t * P : (t + 1) * P],
-                        rhs=(side_codes[:, g] if side else a_codes[n][:, slot]).bitcast(FP8X4),
-                        rhs_scale=side_scales[:, g] if side else a_scales[n][:, slot],
-                        start=(g == order[0] and t == 0),
-                        stop=(g == order[-1] and t == 3),
-                    )
-
-        def copy_agg_tile(n, h):
-            nc.scalar.copy(out=agg_tile(n)[:, h], in_=agg_banks[n, h][:].rearrange("p t i -> p i t"))
-
         def aggregate(n, half, passes=range(PASSES), order=range(PASSES)):
-            if n in BY_TILE:
-                return aggregate_tile(n, half, passes, order)
             if (n, half) not in agg_banks:
-                agg_banks[n, half] = next_bank([P, 2, 2 * P], F32)
+                agg_banks[n, half] = take_bank(("agg", n, half), [P, 4, P] if by_tile(n) else [P, 2, 2 * P])
+            slots = range(4) if by_tile(n) else range(2 * half, 2 * half + 2)
             for g in passes:
-                for tl in range(2):
-                    t = 2 * half + tl
+                if by_tile(n):
+                    codes, scales = a_codes[n][:, slot_of(n, half, g)], a_scales[n][:, slot_of(n, half, g)]
+                else:
+                    codes = a_codes[n][:, 2 * g : 2 * g + 2].rearrange("p h i -> p (h i)")
+                    scales = a_scales[n][:, 2 * g : 2 * g + 2].rearrange("p h i -> p (h i)")
+                for t in slots:
+                    f_words, f_bytes = features_operand(g, t)
                     nc.tensor.matmul_mx(
-                        out=agg_banks[n, half][:, tl, :],
-                        lhsT=f_codes[g][:, t * P : (t + 1) * P].bitcast(FP8X4),
-                        lhsT_scale=f_scales[g][:, t * P : (t + 1) * P],
-                        rhs=a_codes[n][:, 2 * g : 2 * g + 2].rearrange("p h i -> p (h i)").bitcast(FP8X4),
-                        rhs_scale=a_scales[n][:, 2 * g : 2 * g + 2].rearrange("p h i -> p (h i)"),
-                        start=(g == order[0] and tl == 0),
-                        stop=(g == order[-1] and tl == 1),
+                        out=agg_banks[n, half][:, t - slots[0], :],
+                        lhsT=f_words.bitcast(FP8X4),
+                        lhsT_scale=f_bytes,
+                        rhs=codes.bitcast(FP8X4),
+                        rhs_scale=scales,
+                        start=(g == order[0] and t == slots[0]),
+                        stop=(g == order[-1] and t == slots[-1]),
                     )
 
         def copy_agg(n, half):
-            if n in BY_TILE:
-                return copy_agg_tile(n, half)
-            nc.scalar.copy(
-                out=agg_tile(n)[:].rearrange("p h i t -> p (h i) t")[:, :, 2 * half : 2 * half + 2],
-                in_=agg_banks[n, half][:].rearrange("p t i -> p i t"),
-            )
+            if by_tile(n):
+                dst = agg_tile(n)[:, half]
+            else:
+                dst = agg_tile(n)[:].rearrange("p h i t -> p (h i) t")[:, :, 2 * half : 2 * half + 2]
+            nc.scalar.copy(out=dst, in_=agg_banks[n, half][:].rearrange("p t i -> p i t"))
+            give_bank(("agg", n, half))
 
         def quantize_agg(n, first=0, count=2):
             if n not in agg_codes:
-                agg_codes[n] = ring("aggcodes", n, 4, [P, 2 * P], U32)
-                agg_scales[n] = ring("aggscales", n, 4, [P, 2 * P], U8)
+                agg_codes[n] = ring("aggcodes", n, 8, [P, 2 * P], U32)
+                agg_scales[n] = ring("aggscales", n, 8, [P, 2 * P], U8)
             cols = slice(first * P, (first + count) * P)
             nc.vector.quantize_mx(
                 out=agg_codes[n][:, cols].bitcast(FP8X4),
@@ -321,67 +334,48 @@ def tile_net_pa_w4_kernel(tc, A_bytes, A_scale, features, Wg_words, Wg_scales, b
                 in_=agg_bf[n][:, first : first + count].rearrange("p h i t -> p (h i t)"),
             )
 
-        def project(n, h):
+        def project(n, h, first=0, last=D):
             cols = slice(h * P, (h + 1) * P)
-            product[n, h] = next_bank([P, D], F32)
+            product[n, h, first] = take_bank(("product", n, h, first), [P, last - first])
             nc.tensor.matmul_mx(
-                out=product[n, h][:],
+                out=product[n, h, first][:],
                 lhsT=agg_codes[n][:, cols].bitcast(FP8X4),
                 lhsT_scale=agg_scales[n][:, cols],
-                rhs=w_words[:].bitcast(FP4X4),
-                rhs_scale=w_scales[:],
+                rhs=w_words[:, 2 * first : 2 * last].bitcast(FP4X4),
+                rhs_scale=w_scales[:, first:last],
                 start=True,
                 stop=True,
             )
 
-        def finish_in_halves(n, h):
-            halves = [slice(c * D // 2, (c + 1) * D // 2) for c in range(2)]
-            banks = [next_bank([P, D // 2], F32) for c in range(2)]
-            sums = [keep.tile([P, D // 2], F32, name="lastsum%d" % c, align_bytes=64) for c in range(2)]
-            rows = [keep.tile([P, D // 2], F32, name="lastrows%d" % c, align_bytes=64) for c in range(2)]
-            for c in range(2):
-                nc.tensor.matmul_mx(
-                    out=banks[c][:],
-                    lhsT=agg_codes[n][:, h * P : (h + 1) * P].bitcast(FP8X4),
-                    lhsT_scale=agg_scales[n][:, h * P : (h + 1) * P],
-                    rhs=w_words[:, c * D : (c + 1) * D].bitcast(FP4X4),
-                    rhs_scale=w_scales[:, halves[c]],
-                    start=True,
-                    stop=True,
-                )
-            return halves, banks, sums, rows
+        def add_bias(n, h, first=0, last=D):
+            if (n, h) not in summed:
+                summed[n, h] = ring("summed", len(summed), 6, [P, D], F32)
+            nc.vector.tensor_tensor(
+                out=summed[n, h][:, first:last], in0=product[n, h, first][:], in1=bias_row[:, first:last], op=ALU.add
+            )
+            give_bank(("product", n, h, first))
 
-        def add_half(parts, c):
-            halves, banks, sums, rows = parts
-            nc.vector.tensor_tensor(out=sums[c][:], in0=banks[c][:], in1=bias_row[:, halves[c]], op=ALU.add)
+        rows = {}
 
-        def relu_store_half(n, h, parts, c, engine):
-            halves, banks, sums, rows = parts
-            if engine == "vector":
-                nc.vector.tensor_scalar(out=rows[c][:], in0=sums[c][:], scalar1=0.0, scalar2=None, op0=ALU.max)
-            else:
-                nc.scalar.activation(out=rows[c][:], in_=sums[c][:], func=ACT.Relu)
+        def rows_tile(n, h):
+            if (n, h) not in rows:
+                rows[n, h] = ring("rows", len(rows), 8, [P, D], F32)
+            return rows[n, h]
+
+        def store(n, h, first=0, last=D):
             r0 = (2 * n + h) * P
-            nc.sync.dma_start(out=out[r0 : r0 + P, halves[c]], in_=rows[c][:])
+            nc.sync.dma_start(out=out[r0 : r0 + P, first:last], in_=rows[n, h][:, first:last])
 
-        def add_bias(n, h):
-            summed[n, h] = ring("summed", 2 * n + h, 6, [P, D], F32)
-            nc.vector.tensor_tensor(out=summed[n, h][:], in0=product[n, h][:], in1=bias_row[:], op=ALU.add)
-
-        def store(n, h, rows):
-            r0 = (2 * n + h) * P
-            nc.sync.dma_start(out=out[r0 : r0 + P, :], in_=rows[:])
-
-        def relu_store(n, h, engine="scalar"):
-            rows = ring("rows", 2 * n + h, 8, [P, D], F32)
+        def relu_store(n, h, engine="scalar", first=0, last=D):
+            dst, src = rows_tile(n, h)[:, first:last], summed[n, h][:, first:last]
             if engine == "vector":
-                nc.vector.tensor_scalar(out=rows[:], in0=summed[n, h][:], scalar1=0.0, scalar2=None, op0=ALU.max)
+                nc.vector.tensor_scalar(out=dst, in0=src, scalar1=0.0, scalar2=None, op0=ALU.max)
             else:
-                nc.scalar.activation(out=rows[:], in_=summed[n, h][:], func=ACT.Relu)
-            store(n, h, rows)
+                nc.scalar.activation(out=dst, in_=src, func=ACT.Relu)
+            store(n, h, first, last)
 
         def project_turned(n, half):
-            product[n, half] = next_bank([P, 2, 2 * P], F32)
+            product[n, half] = take_bank(("product", n, half), [P, 2, 2 * P])
             for cl in range(2):
                 c = 2 * half + cl
                 nc.tensor.matmul_mx(
@@ -396,7 +390,7 @@ def tile_net_pa_w4_kernel(tc, A_bytes, A_scale, features, Wg_words, Wg_scales, b
 
         def relu_of_turned(n, half):
             if n not in relu_turned:
-                relu_turned[n] = ring("reluturned", n, 3, [P, 4, 2 * P], F32)
+                relu_turned[n] = ring("reluturned", len(relu_turned), 3, [P, 4, 2 * P], F32)
             for cl in range(2):
                 c = 2 * half + cl
                 nc.scalar.activation(
@@ -405,212 +399,261 @@ def tile_net_pa_w4_kernel(tc, A_bytes, A_scale, features, Wg_words, Wg_scales, b
                     func=ACT.Relu,
                     bias=bias_chunks[:, c : c + 1],
                 )
+            give_bank(("product", n, half))
 
         def turn_back(n, h):
-            back[n, h] = next_bank([P, 4, P], F32)
+            back[n, h] = take_bank(("back", n, h), [P, 4, P])
             for c in range(4):
                 nc.tensor.transpose(back[n, h][:, c, :], relu_turned[n][:, c, h * P : (h + 1) * P], ident[:])
 
         def store_back(n, h):
-            rows = ring("rows", 2 * n + h, 8, [P, D], F32)
-            nc.scalar.copy(out=rows[:], in_=back[n, h][:].rearrange("p c n -> p (c n)"))
-            store(n, h, rows)
+            nc.scalar.copy(out=rows_tile(n, h)[:], in_=back[n, h][:].rearrange("p c n -> p (c n)"))
+            give_bank(("back", n, h))
+            store(n, h)
 
         make_identity(nc, ident[:])
+        make_identity(nc, ident_bf[:])
         nc.vector.memset(w_scales[:].bitcast(I32), 0)
 
         load_a(0, 0, 0, PASS)
-        load_a(0, 0, PASS, NODES)
-        load_a(0, 1, 0, NODES // 2)
         nc.sync.dma_start(out=scale_cols[:], in_=A_scale.rearrange("o (g p t) -> p (o g) t", p=P, t=4))
-        load_a(0, 1, NODES // 2, NODES)
-        load_a(1, 0)
-        nc.sync.dma_start(out=bias_raw[:], in_=bg.rearrange("(p t) -> p t", t=4))
+        load_a(0, 0, PASS, NODES)
         load_f(0)
-        load_a(1, 1)
+        load_a(0, 1)
+        load_a(1, 0)
         load_f(1)
-        load_pair(2)
+        nc.sync.dma_start(out=bias_raw[:, :, 0:1], in_=bg.rearrange("(c p o) -> p c o", p=P, o=1))
+        load_a(1, 1)
         load_f(2)
         load_f(3)
-        nc.sync.dma_start(out=side_bytes[:], in_=A_bytes[NODES - P :, :])
+        load_pair(2)
+        load_pair(SIDE)
         load_pair(3)
         load_w()
-        for n in range(4, LAST):
+        for n in range(4, SIDE):
             load_pair(n)
-        load_a(LAST, 0)
 
         widen(0, PASS, "vector")
-        widen(PASS, 2 * PASS, "vector")
-        widen(2 * PASS, NODES, "vector")
-        widen(2 * QUARTER, 3 * QUARTER, "scalar")
-        widen(3 * QUARTER, 4 * QUARTER, "scalar")
+        for g in range(1, PASSES):
+            widen(g * PASS, (g + 1) * PASS, "scalar")
+        f_grouped[0] = keep.tile([P, 4, P, 4], BF16, name="stage0", align_bytes=64)
+        group_features(0, "gpsimd", 0, UNITS // 2)
+        widen(NODES, NODES + PASS, "scalar")
+        widen(NODES + PASS, NODES + QUARTER, "scalar")
+        widen(NODES + QUARTER, PAIR, "scalar")
+        widen(PAIR, PAIR + NODES, "scalar")
+        f_grouped[1] = keep.tile([P, 4, P, 4], BF16, name="fgrouped1", align_bytes=64)
+        group_features(1, "scalar", 0, UNITS // 2)
+        nc.scalar.copy(out=bias_chunks[:], in_=bias_raw[:, :, 0])
+        widen(PAIR + NODES, 2 * PAIR, "scalar")
         for g in range(PASSES):
             turn(0, 0, g, 1)
         for g in range(PASSES):
             scale_turned(0, 0, g, 1)
             turn(0, 1, g, 1)
-        widen(PAIR, PAIR + NODES, "gpsimd")
-        for g in (0, 1, 3):
-            features_tile(g, "fgrouped%d" % g)
-        nc.scalar.copy(out=bias_cols[:, :2], in_=bias_raw[:, :2])
-        spread_bias((0, 1))
-        group_features(0, "scalar")
-        for q in range(2, 4):
-            widen(PAIR + q * QUARTER, PAIR + (q + 1) * QUARTER, "scalar")
         for g in range(PASSES):
             scale_turned(0, 1, g, 1)
         turn(1, 0, 0)
         turn(1, 0, 2)
-        group_features(1, "scalar")
-        nc.scalar.copy(out=bias_cols[:, 2:], in_=bias_raw[:, 2:])
-
-        quantize_rows(0, 0, 4)
-        quantize_rows(0, 4, 4)
+        quantize_rows(0, 0, PASSES)
+        quantize_rows(0, PASSES, PASSES)
         quantize_features(0)
-        widen(2 * PAIR, 3 * PAIR - SHARE, "gpsimd")
-        group_features(3, "scalar", 0, SPLIT)
-        features_tile(2, "stage0")
-        group_features(2, "scalar")
+        quantize_features(1)
+
+        f_grouped[2] = keep.tile([P, 4, 2 * P, 4], BF16, name="stage0", align_bytes=64)
+        group_features(2, "gpsimd", 0, POOL_UNITS)
+        group_features(2, "scalar", POOL_UNITS, UNITS)
+        widen(2 * PAIR, 2 * PAIR + NODES, "scalar")
+        widen_side(0)
+        widen(2 * PAIR + NODES, 3 * PAIR, "scalar")
+        spread_bias((0, 1))
+        aggregate(0, 0, (0,))
+        aggregate(0, 1, (0,))
         turn(1, 1, 0)
         turn(1, 1, 2)
-        spread_bias((2, 3))
-        widen(3 * PAIR - SHARE, 3 * PAIR, "scalar")
-        copy_bias()
-        widen(3 * PAIR, 3 * PAIR + QUARTER, "scalar")
-        widen_side(0)
-        order = (0, 1, 3, 2)
-        aggregate(0, 0, (0,), order)
-        aggregate(0, 1, (0,), order)
+        aggregate(0, 0, (1,))
+        aggregate(0, 1, (1,))
         scale_turned(1, 0, 0)
         scale_turned(1, 0, 2)
+        turn(2, 0, 0)
+        turn_side(0)
+        scale_side(0)
+        turn(2, 0, 2)
+        spread_bias((2, 3))
         scale_turned(1, 1, 0)
         scale_turned(1, 1, 2)
-        turn(2, 0, 0)
-
-        quantize_features(1)
-        group_features(3, "vector", SPLIT, P)
-        quantize_rows(1, 0, 4)
-        quantize_features(3)
+        turn(2, 1, 0)
+        turn(2, 1, 2)
+        widen_side(1)
+        copy_bias()
         quantize_features(2)
-        quantize_rows(1, 4, 4)
-        widen(3 * PAIR + QUARTER, 4 * PAIR + QUARTER - SECOND_SHARE, "gpsimd")
-        for g in order[1:]:
-            for half in range(2):
-                aggregate(0, half, (g,), order)
-            if g == 1:
-                turn(2, 0, 2)
-                turn(2, 1, 0)
+        quantize_rows(1)
+
+        widen(3 * PAIR + QUARTER, 4 * PAIR + QUARTER - SHARE, "gpsimd")
+        aggregate(0, 0, (2, 3))
+        aggregate(0, 1, (2, 3))
+        turn_side(1)
         copy_agg(0, 0)
         copy_agg(0, 1)
         aggregate(1, 0)
-        turn(2, 1, 2)
+        widen(3 * PAIR, 3 * PAIR + QUARTER, "scalar")
+        scale_side(1)
+        widen_side(2)
+        scale_turned(2, 0, 0)
+        turn(3, 0, 0)
         aggregate(1, 1)
+        turn_side(2)
         copy_agg(1, 0)
         copy_agg(1, 1)
-        scale_turned(2, 0, 0)
         scale_turned(2, 0, 2)
-        turn(3, 0, 0)
-        turn_side(0)
-        widen(4 * PAIR + QUARTER - SECOND_SHARE, 4 * PAIR + QUARTER, "scalar")
-        bias_to_partitions()
-        scale_side(0)
         scale_turned(2, 1, 0)
         scale_turned(2, 1, 2)
 
-        for n in range(3, LAST):
-            if n == 3:
-                quantize_agg(0)
-            quantize_agg(n - 2)
-            quantize_rows(n - 1)
-            start = min((n + 1) * PAIR + QUARTER, LAST * PAIR)
-            stop = min(start + PAIR, LAST * PAIR) if n < LAST - 1 else start + NODES
-            share = SHARE if stop - start == PAIR else 0
-            widen(start, stop - share, "gpsimd")
-            turn(n, 0, 2)
-            if n == 3:
-                for half in range(2):
-                    project_turned(0, half)
-                    relu_of_turned(0, half)
-            turn(n, 1, 0)
-            turn(n, 1, 2)
-            if n == LAST - 1:
-                group_side(0, 4)
-            project_turned(n - 2, 0)
-            relu_of_turned(n - 2, 0)
-            scale_turned(n, 0, 0)
-            if n < LAST - 1:
-                widen_side(n - 2)
-            aggregate(n - 1, 0)
-            copy_agg(n - 1, 0)
-            aggregate(n - 1, 1)
-            copy_agg(n - 1, 1)
-            scale_turned(n, 0, 2)
-            for h in range(2):
-                turn_back(n - 3, h)
-                store_back(n - 3, h)
-            turn(n + 1, 0, 0)
-            if n < LAST - 1:
-                turn_side(n - 2)
-            project_turned(n - 2, 1)
-            relu_of_turned(n - 2, 1)
-            if n < LAST - 1:
-                scale_side(n - 2)
-            if share:
-                widen(stop - share, stop, "scalar")
-            if n == LAST - 1:
-                turn(LAST, 0, 3, 1)
-            scale_turned(n, 1, 0)
-            if n == LAST - 1:
-                quantize_side()
-                quantize_rows(n, 0, PASSES)
-            scale_turned(n, 1, 2)
+        quantize_agg(0)
+        quantize_rows(2)
+        widen(4 * PAIR + QUARTER, 5 * PAIR + QUARTER, "gpsimd")
+        turn(3, 0, 2)
+        project_turned(0, 0)
+        project_turned(0, 1)
+        turn(3, 1, 0)
+        widen_side(3)
+        scale_side(2)
+        widen(4 * PAIR + QUARTER - SHARE, 4 * PAIR + QUARTER, "scalar")
+        relu_of_turned(0, 0)
+        relu_of_turned(0, 1)
+        for g in range(3):
+            group_side(g)
+        aggregate(2, 0)
+        turn(3, 1, 2)
+        scale_turned(3, 0, 0)
+        turn_side(3, turn_names)
+        scale_turned(3, 0, 2)
+        turn(4, 0, 0)
+        aggregate(2, 1)
+        for h in range(2):
+            turn_back(0, h)
+        copy_agg(2, 0)
+        copy_agg(2, 1)
+        for h in range(2):
+            store_back(0, h)
+        scale_turned(3, 1, 0)
+        scale_side_on_vector(3)
+        scale_turned(3, 1, 2)
 
-        turn(LAST, 0, 2, 1)
-        free0, held0, held3, held2 = turn_names
-        ring0, ring1, ring2, ring3 = bank_names
-        bank_names.clear()
-        bank_names.extend([ring0, ring1, free0, ring2, ring3, ring0, held3, held0, ring1, ring2, free0, held2, ring3])
-        aggregate_tile(LAST, 1)
-        copy_agg_tile(LAST, 1)
-        scale_on_scalar(3)
-        quantize_agg(LAST - 2)
-        project(LAST - 2, 0)
-        project(LAST - 2, 1)
-        scale_turned(LAST, 0, 0)
-        add_bias(LAST - 2, 0)
-        quantize_rows(LAST - 1, PASSES, PASSES)
-        aggregate_tile(LAST - 1, 0)
-        turn_back(LAST - 3, 0)
-        relu_store(LAST - 2, 0)
-        copy_agg_tile(LAST - 1, 0)
-        group_on_scalar(3)
-        store_back(LAST - 3, 0)
-        quantize_agg(LAST, 1, 1)
-        scale_turned(LAST, 0, 2, 1)
-        quantize_rows(LAST, 0, 2)
-        add_bias(LAST - 2, 1)
-        quantize_agg(LAST - 1, 0, 1)
-        quantize_rows(LAST, 2, 2)
-        turn_back(LAST - 3, 1)
-        store_back(LAST - 3, 1)
-        aggregate_tile(LAST - 1, 1)
-        copy_agg_tile(LAST - 1, 1)
-        relu_store(LAST - 2, 1)
-        project(LAST, 1)
-        project(LAST - 1, 0)
-        add_bias(LAST, 1)
-        quantize_agg(LAST - 1, 1, 1)
-        add_bias(LAST - 1, 0)
-        aggregate_tile(LAST, 0)
-        project(LAST - 1, 1)
-        relu_store(LAST, 1)
-        copy_agg_tile(LAST, 0)
-        relu_store(LAST - 1, 0)
-        add_bias(LAST - 1, 1)
+        quantize_rows(SIDE)
+        quantize_agg(1)
+        quantize_rows(3)
+        widen(5 * PAIR + QUARTER, 6 * PAIR + QUARTER - SHARE, "gpsimd")
+        turn(4, 0, 2)
+        turn_by_matmul(4, 1, 0)
+        turn(4, 1, 2)
+        aggregate(SIDE, 0)
+        project_turned(1, 0)
+        project_turned(1, 1)
+        aggregate(SIDE, 1)
+        relu_of_turned(1, 0)
+        copy_agg(SIDE, 0)
+        relu_of_turned(1, 1)
+        aggregate(3, 0)
+        aggregate(3, 1)
+        copy_agg(SIDE, 1)
+        scale_turned(4, 0, 0)
+        turn(5, 0, 0)
+        for h in range(2):
+            turn_back(1, h)
+        copy_agg(3, 0)
+        widen(6 * PAIR + QUARTER - SHARE, 6 * PAIR + QUARTER, "scalar")
+        copy_agg(3, 1)
+        for h in range(2):
+            store_back(1, h)
+        scale_turned(4, 0, 2)
+        scale_turned(4, 1, 0)
+        scale_turned(4, 1, 2)
+
+        quantize_agg(2)
+        quantize_agg(SIDE)
+        quantize_rows(4)
+        widen(6 * PAIR + QUARTER, 7 * PAIR, "gpsimd")
+        turn(5, 0, 2)
+        project_turned(2, 0)
+        project_turned(2, 1)
+        turn(5, 1, 0)
+        turn(6, 0, 0)
+        project_turned(SIDE, 0)
+        project_turned(SIDE, 1)
+        relu_of_turned(2, 0)
+        relu_of_turned(2, 1)
+        scale_turned(5, 0, 0)
+        turn(5, 1, 2)
+        aggregate(4, 0)
+        aggregate(4, 1)
+        relu_of_turned(SIDE, 0)
+        relu_of_turned(SIDE, 1)
+        scale_turned(5, 0, 2)
+        scale_turned(5, 1, 0)
+        scale_turned(5, 1, 2)
+        scale_on_scalar(6, 0, 0, 0)
+        copy_agg(4, 0)
+        scale_on_scalar(6, 0, 0, 1)
+        copy_agg(4, 1)
+
+        quantize_agg(3)
+        quantize_rows(5)
+        turn(LAST, 0, 2)
+        for h in range(2):
+            turn_back(2, h)
+        project(3, 0)
+        turn(LAST, 1, 0)
+        aggregate(5, 0)
+        turn(LAST, 1, 2)
+        group_on_scalar(6, 0, 0)
+        for h in range(2):
+            store_back(2, h)
+        project(3, 1)
+        aggregate(5, 1)
+        scale_turned(LAST, 0, 2)
+        quantize_agg(4)
+        add_bias(3, 0)
+        quantize_rows(LAST, 0, PASSES)
+        project(4, 0)
+        copy_agg(5, 0)
+        relu_store(3, 0)
+        scale_turned(LAST, 1, 0)
+        add_bias(3, 1)
+        quantize_rows(LAST, PASSES, 2)
+        copy_agg(5, 1)
+        relu_store(3, 1)
+        scale_turned(LAST, 1, 2)
+        aggregate(LAST, 0)
+        for h in range(2):
+            turn_back(SIDE, h)
+        project(4, 1)
+        aggregate(LAST, 1, (0, 1))
+        copy_agg(LAST, 0)
+        quantize_agg(5)
+        quantize_rows(LAST, PASSES + 2, 2)
+        add_bias(4, 0)
+        add_bias(4, 1)
+        for h in range(2):
+            store_back(SIDE, h)
+        project(5, 0)
+        aggregate(LAST, 1, (2, 3))
+        project(5, 1)
+        relu_store(4, 0)
+        copy_agg(LAST, 1)
         quantize_agg(LAST, 0, 1)
-        parts = finish_in_halves(LAST, 0)
-        relu_store(LAST - 1, 1)
-        add_half(parts, 0)
-        add_half(parts, 1)
-        relu_store_half(LAST, 0, parts, 0, "vector")
-        relu_store_half(LAST, 0, parts, 1, "vector")
+        project(LAST, 0)
+        add_bias(5, 0)
+        add_bias(5, 1)
+        quantize_agg(LAST, 1, 1)
+        project(LAST, 1, 0, D // 2)
+        project(LAST, 1, D // 2, D)
+        relu_store(4, 1)
+        relu_store(5, 0)
+        add_bias(LAST, 0)
+        add_bias(LAST, 1, 0, D // 2)
+        add_bias(LAST, 1, D // 2, D)
+        relu_store(5, 1)
+        relu_store(LAST, 0)
+        relu_store(LAST, 1, "vector", 0, D // 2)
+        relu_store(LAST, 1, "vector", D // 2, D)

@@ -26,10 +26,13 @@ LAST = SIDE - 1
 TURN_BANKS = 4
 SHARE = 512
 UNITS = 128
-POOL_UNITS = 88
-HALVED = (0,)
+POOL_UNITS = 72
+EARLY_UNITS = 88
+FIRST_UNITS = 48
+HALVED = (0, SIDE)
 BY_TILE = (0, 1, LAST)
-RELEASES = {0: "stage1", 1: "stage2", (SIDE, 0): "sidegrouped", SIDE: "stage0"}
+RELEASES = {0: "stage1", 1: "stage2", SIDE: "stage0"}
+STARTS = [3 * PAIR + QUARTER, 4 * PAIR + PASS, 5 * PAIR + QUARTER, 6 * PAIR + QUARTER]
 FLOPS = 2 * NODES * NODES * D + 2 * NODES * D * D
 
 
@@ -108,7 +111,7 @@ def tile_net_pa_w4_kernel(tc, A_bytes, A_scale, features, Wg_words, Wg_scales, b
                 bias_banks.append(take_bank("bias", [P, 4, P]))
             for c in chunks:
                 column = bias_chunks[:, c : c + 1].to_broadcast([P, P])
-                nc.tensor.matmul(bias_banks[0][:, c, :], lhsT=column, rhs=ident[:], start=True, stop=True)
+                nc.tensor.transpose(bias_banks[0][:, c, :], column, ident[:])
 
         def copy_bias():
             nc.scalar.copy(out=bias_row[:], in_=bias_banks[0][:].rearrange("p c n -> p (c n)"))
@@ -148,7 +151,7 @@ def tile_net_pa_w4_kernel(tc, A_bytes, A_scale, features, Wg_words, Wg_scales, b
         agg_banks, agg_bf, agg_codes, agg_scales = {}, {}, {}, {}
         product, relu_turned, summed, back, side_banks, side_planes = {}, {}, {}, {}, {}, {}
 
-        starts = [0, PAIR, 2 * PAIR] + [n * PAIR + QUARTER for n in range(3, SIDE)] + [SIDE * PAIR]
+        starts = [0, PAIR, 2 * PAIR] + STARTS + [SIDE * PAIR]
 
         def wide_columns(first, last):
             n = max(m for m in range(SIDE) if starts[m] <= first)
@@ -165,8 +168,8 @@ def tile_net_pa_w4_kernel(tc, A_bytes, A_scale, features, Wg_words, Wg_scales, b
                 cols = slice(h * NODES + g * PASS, h * NODES + (g + 1) * PASS)
                 nc.scalar.copy(out=side_wide[:, cols], in_=side_bytes[:, cols].bitcast(FP8))
 
-        def turn(n, h, first, count=2):
-            bank = take_bank(("turn", n, h, first), [P, 2, count, P], turn_names)
+        def turn(n, h, first, count=2, names=turn_names):
+            bank = take_bank(("turn", n, h, first), [P, 2, count, P], names)
             turned[n, h, first] = bank
             for gl in range(count):
                 col = (2 * n + h) * NODES + (first + gl) * PASS
@@ -204,20 +207,22 @@ def tile_net_pa_w4_kernel(tc, A_bytes, A_scale, features, Wg_words, Wg_scales, b
                     grouped[key] = ring("grouped", n, 2, [P, width, P, 4], BF16)
             return grouped[key][:, first % width : first % width + (count - 1) * step + 1 : step]
 
-        def scale_turned(n, h, first, count=2):
+        def scale_turned(n, h, first, count=2, skip=0, last=True):
             scales = scale_cols[:, first : first + count, :].rearrange("p g (u e) -> p g u e", u=2)
             dst = grouped_slots(n, slot_of(n, h, first), count, 1 if n == LAST else 2)
             if (n, h, first) in by_matmul:
                 values = turned[n, h, first][:].rearrange("p g (u e) i -> p g i u e", u=2)
             else:
-                values = turned[n, h, first][:].bitcast(BF16).rearrange("p u g (i e) -> p g i u e", e=2)
+                bank = turned[n, h, first - skip][:, :, skip : skip + count]
+                values = bank.bitcast(BF16).rearrange("p u g (i e) -> p g i u e", e=2)
             nc.vector.tensor_tensor(
                 out=dst.rearrange("p g i (u e) -> p g i u e", u=2),
                 in0=values,
                 in1=scales.unsqueeze(2).to_broadcast([P, count, P, 2, 2]),
                 op=ALU.mult,
             )
-            give_bank(("turn", n, h, first), bank_names if n == LAST else turn_names)
+            if last:
+                give_bank(("turn", n, h, first - skip), bank_names if n == LAST else turn_names)
 
         def turn_side(g, names=bank_names):
             side_banks[g] = take_bank(("side", g), [P, 2, 2, P], names)
@@ -258,7 +263,7 @@ def tile_net_pa_w4_kernel(tc, A_bytes, A_scale, features, Wg_words, Wg_scales, b
 
         def scale_on_scalar(n, h, first, g):
             if (n, h) not in side_planes:
-                side_planes[n, h] = ring("sideplanes", 0, 3, [P, 2, 2, P, 2], BF16)
+                side_planes[n, h] = ring("sideplanes", n, 3, [P, 2, 2, P, 2], BF16)
             values = turned[n, h, first][:].bitcast(BF16).rearrange("p u g (i e) -> p g u i e", e=2)
             for t in range(4):
                 nc.scalar.activation(
@@ -268,11 +273,11 @@ def tile_net_pa_w4_kernel(tc, A_bytes, A_scale, features, Wg_words, Wg_scales, b
                     scale=scale_cols[:, g, t : t + 1],
                 )
             if g == first + 1:
-                give_bank(("turn", n, h, first), bank_names)
+                give_bank(("turn", n, h, first), bank_names if n == LAST else turn_names)
 
         def group_on_scalar(n, h, first):
             nc.scalar.copy(
-                out=grouped_slots(n, slot_of(n, h, first), 2).bitcast(F32),
+                out=grouped_slots(n, slot_of(n, h, first), 2, 1 if n == LAST else 2).bitcast(F32),
                 in_=side_planes[n, h][:].rearrange("p g u i e -> p g u (i e)").bitcast(F32).rearrange("p g u i -> p g i u"),
             )
 
@@ -418,14 +423,14 @@ def tile_net_pa_w4_kernel(tc, A_bytes, A_scale, features, Wg_words, Wg_scales, b
         load_a(0, 0, 0, PASS)
         nc.sync.dma_start(out=scale_cols[:], in_=A_scale.rearrange("o (g p t) -> p (o g) t", p=P, t=4))
         load_a(0, 0, PASS, NODES)
-        load_f(0)
         load_a(0, 1)
+        nc.sync.dma_start(out=bias_raw[:, :, 0:1], in_=bg.rearrange("(c p o) -> p c o", p=P, o=1))
+        load_f(0)
         load_a(1, 0)
         load_f(1)
-        nc.sync.dma_start(out=bias_raw[:, :, 0:1], in_=bg.rearrange("(c p o) -> p c o", p=P, o=1))
-        load_a(1, 1)
         load_f(2)
         load_f(3)
+        load_a(1, 1)
         load_pair(2)
         load_pair(SIDE)
         load_pair(3)
@@ -436,25 +441,29 @@ def tile_net_pa_w4_kernel(tc, A_bytes, A_scale, features, Wg_words, Wg_scales, b
         widen(0, PASS, "vector")
         for g in range(1, PASSES):
             widen(g * PASS, (g + 1) * PASS, "scalar")
-        f_grouped[0] = keep.tile([P, 4, P, 4], BF16, name="stage0", align_bytes=64)
-        group_features(0, "gpsimd", 0, UNITS // 2)
+        f_grouped[0] = keep.tile([P, 4, P, 4], BF16, name="fgrouped0", align_bytes=64)
+        group_features(0, "gpsimd", 0, FIRST_UNITS)
         widen(NODES, NODES + PASS, "scalar")
         widen(NODES + PASS, NODES + QUARTER, "scalar")
         widen(NODES + QUARTER, PAIR, "scalar")
-        widen(PAIR, PAIR + NODES, "scalar")
-        f_grouped[1] = keep.tile([P, 4, P, 4], BF16, name="fgrouped1", align_bytes=64)
-        group_features(1, "scalar", 0, UNITS // 2)
         nc.scalar.copy(out=bias_chunks[:], in_=bias_raw[:, :, 0])
-        widen(PAIR + NODES, 2 * PAIR, "scalar")
+        group_features(0, "scalar", FIRST_UNITS, UNITS // 2)
+        widen(PAIR, PAIR + NODES, "scalar")
         for g in range(PASSES):
             turn(0, 0, g, 1)
         for g in range(PASSES):
             scale_turned(0, 0, g, 1)
             turn(0, 1, g, 1)
+            if g:
+                spread_bias((g,))
+        spread_bias((0,))
+        f_grouped[1] = keep.tile([P, 4, P, 4], BF16, name="stage0", align_bytes=64)
+        group_features(1, "scalar", 0, UNITS // 2)
+        copy_bias()
         for g in range(PASSES):
             scale_turned(0, 1, g, 1)
-        turn(1, 0, 0)
-        turn(1, 0, 2)
+        turn_by_matmul(1, 0, 0)
+        turn_by_matmul(1, 0, 2)
         quantize_rows(0, 0, PASSES)
         quantize_rows(0, PASSES, PASSES)
         quantize_features(0)
@@ -462,46 +471,49 @@ def tile_net_pa_w4_kernel(tc, A_bytes, A_scale, features, Wg_words, Wg_scales, b
 
         f_grouped[2] = keep.tile([P, 4, 2 * P, 4], BF16, name="stage0", align_bytes=64)
         group_features(2, "gpsimd", 0, POOL_UNITS)
-        group_features(2, "scalar", POOL_UNITS, UNITS)
+        group_features(2, "scalar", POOL_UNITS, EARLY_UNITS)
+        widen(PAIR + NODES, PAIR + NODES + QUARTER, "scalar")
+        widen(PAIR + NODES + QUARTER, 2 * PAIR, "scalar")
         widen(2 * PAIR, 2 * PAIR + NODES, "scalar")
+        group_features(2, "scalar", EARLY_UNITS, UNITS)
         widen_side(0)
-        widen(2 * PAIR + NODES, 3 * PAIR, "scalar")
-        spread_bias((0, 1))
+        widen(2 * PAIR + NODES, 3 * PAIR - QUARTER, "scalar")
+        widen(3 * PAIR - QUARTER, 3 * PAIR, "scalar")
         aggregate(0, 0, (0,))
         aggregate(0, 1, (0,))
-        turn(1, 1, 0)
+        turn_by_matmul(1, 1, 0)
         turn(1, 1, 2)
         aggregate(0, 0, (1,))
         aggregate(0, 1, (1,))
         scale_turned(1, 0, 0)
         scale_turned(1, 0, 2)
         turn(2, 0, 0)
+        turn_by_matmul(2, 0, 2)
         turn_side(0)
-        scale_side(0)
-        turn(2, 0, 2)
-        spread_bias((2, 3))
+        scale_side(0, (0, 1))
+        widen_side(1)
+        scale_side(0, (2, 3))
         scale_turned(1, 1, 0)
         scale_turned(1, 1, 2)
         turn(2, 1, 0)
         turn(2, 1, 2)
-        widen_side(1)
-        copy_bias()
         quantize_features(2)
         quantize_rows(1)
 
-        widen(3 * PAIR + QUARTER, 4 * PAIR + QUARTER - SHARE, "gpsimd")
+        widen(starts[3], starts[4], "gpsimd")
         aggregate(0, 0, (2, 3))
         aggregate(0, 1, (2, 3))
         turn_side(1)
         copy_agg(0, 0)
         copy_agg(0, 1)
         aggregate(1, 0)
+        aggregate(1, 1)
         widen(3 * PAIR, 3 * PAIR + QUARTER, "scalar")
-        scale_side(1)
+        scale_side(1, (0, 1))
         widen_side(2)
+        scale_side(1, (2, 3))
         scale_turned(2, 0, 0)
         turn(3, 0, 0)
-        aggregate(1, 1)
         turn_side(2)
         copy_agg(1, 0)
         copy_agg(1, 1)
@@ -509,16 +521,16 @@ def tile_net_pa_w4_kernel(tc, A_bytes, A_scale, features, Wg_words, Wg_scales, b
         scale_turned(2, 1, 0)
         scale_turned(2, 1, 2)
 
+
         quantize_agg(0)
         quantize_rows(2)
-        widen(4 * PAIR + QUARTER, 5 * PAIR + QUARTER, "gpsimd")
+        widen(starts[4], starts[5], "gpsimd")
         turn(3, 0, 2)
         project_turned(0, 0)
         project_turned(0, 1)
         turn(3, 1, 0)
         widen_side(3)
         scale_side(2)
-        widen(4 * PAIR + QUARTER - SHARE, 4 * PAIR + QUARTER, "scalar")
         relu_of_turned(0, 0)
         relu_of_turned(0, 1)
         for g in range(3):
@@ -527,8 +539,6 @@ def tile_net_pa_w4_kernel(tc, A_bytes, A_scale, features, Wg_words, Wg_scales, b
         turn(3, 1, 2)
         scale_turned(3, 0, 0)
         turn_side(3, turn_names)
-        scale_turned(3, 0, 2)
-        turn(4, 0, 0)
         aggregate(2, 1)
         for h in range(2):
             turn_back(0, h)
@@ -536,124 +546,129 @@ def tile_net_pa_w4_kernel(tc, A_bytes, A_scale, features, Wg_words, Wg_scales, b
         copy_agg(2, 1)
         for h in range(2):
             store_back(0, h)
+        scale_turned(3, 0, 2)
         scale_turned(3, 1, 0)
-        scale_side_on_vector(3)
         scale_turned(3, 1, 2)
+        scale_side_on_vector(3)
 
-        quantize_rows(SIDE)
+        quantize_rows(SIDE, 0, PASSES)
+        quantize_rows(SIDE, PASSES, PASSES)
         quantize_agg(1)
         quantize_rows(3)
-        widen(5 * PAIR + QUARTER, 6 * PAIR + QUARTER - SHARE, "gpsimd")
-        turn(4, 0, 2)
-        turn_by_matmul(4, 1, 0)
-        turn(4, 1, 2)
+        widen(starts[5], starts[6] - SHARE, "gpsimd")
+        turn(4, 0, 0)
+        turn_by_matmul(4, 0, 2)
+        turn(4, 1, 0)
         aggregate(SIDE, 0)
         project_turned(1, 0)
         project_turned(1, 1)
+        turn(4, 1, 2)
         aggregate(SIDE, 1)
+        widen(starts[6] - SHARE, starts[6], "scalar")
         relu_of_turned(1, 0)
         copy_agg(SIDE, 0)
         relu_of_turned(1, 1)
+        scale_turned(4, 0, 0)
+        turn(5, 0, 0)
         aggregate(3, 0)
         aggregate(3, 1)
         copy_agg(SIDE, 1)
-        scale_turned(4, 0, 0)
-        turn(5, 0, 0)
-        for h in range(2):
-            turn_back(1, h)
-        copy_agg(3, 0)
-        widen(6 * PAIR + QUARTER - SHARE, 6 * PAIR + QUARTER, "scalar")
-        copy_agg(3, 1)
-        for h in range(2):
-            store_back(1, h)
+        scale_on_scalar(5, 0, 0, 0)
         scale_turned(4, 0, 2)
         scale_turned(4, 1, 0)
         scale_turned(4, 1, 2)
+        turn(5, 0, 2)
+        for h in range(2):
+            turn_back(1, h)
+        copy_agg(3, 0)
+        scale_on_scalar(5, 0, 0, 1)
+        for h in range(2):
+            store_back(1, h)
+        copy_agg(3, 1)
 
         quantize_agg(2)
         quantize_agg(SIDE)
         quantize_rows(4)
-        widen(6 * PAIR + QUARTER, 7 * PAIR, "gpsimd")
-        turn(5, 0, 2)
+        widen(starts[6], starts[7], "gpsimd")
+        turn(5, 1, 0)
+        project(SIDE, 0)
+        project(SIDE, 1)
+        turn(5, 1, 2)
+        turn(LAST, 0, 0)
         project_turned(2, 0)
         project_turned(2, 1)
-        turn(5, 1, 0)
-        turn(6, 0, 0)
-        project_turned(SIDE, 0)
-        project_turned(SIDE, 1)
-        relu_of_turned(2, 0)
-        relu_of_turned(2, 1)
-        scale_turned(5, 0, 0)
-        turn(5, 1, 2)
-        aggregate(4, 0)
-        aggregate(4, 1)
-        relu_of_turned(SIDE, 0)
-        relu_of_turned(SIDE, 1)
         scale_turned(5, 0, 2)
         scale_turned(5, 1, 0)
-        scale_turned(5, 1, 2)
-        scale_on_scalar(6, 0, 0, 0)
+        add_bias(SIDE, 0)
+        add_bias(SIDE, 1)
+        aggregate(4, 0)
+        turn(LAST, 0, 2)
+        group_on_scalar(5, 0, 0)
+        scale_on_scalar(LAST, 0, 0, 0)
+        relu_of_turned(2, 0)
+        relu_of_turned(2, 1)
+        aggregate(4, 1)
         copy_agg(4, 0)
-        scale_on_scalar(6, 0, 0, 1)
+        scale_turned(5, 1, 2)
+        scale_on_scalar(LAST, 0, 0, 1)
         copy_agg(4, 1)
+        group_on_scalar(LAST, 0, 0)
 
         quantize_agg(3)
         quantize_rows(5)
-        turn(LAST, 0, 2)
-        for h in range(2):
-            turn_back(2, h)
         project(3, 0)
         turn(LAST, 1, 0)
+        for h in range(2):
+            turn_back(2, h)
         aggregate(5, 0)
         turn(LAST, 1, 2)
-        group_on_scalar(6, 0, 0)
+        scale_turned(LAST, 0, 2)
+        add_bias(3, 0)
+        quantize_agg(4)
+        project(3, 1)
+        project(4, 0)
         for h in range(2):
             store_back(2, h)
-        project(3, 1)
-        aggregate(5, 1)
-        scale_turned(LAST, 0, 2)
-        quantize_agg(4)
-        add_bias(3, 0)
-        quantize_rows(LAST, 0, PASSES)
-        project(4, 0)
-        copy_agg(5, 0)
-        relu_store(3, 0)
-        scale_turned(LAST, 1, 0)
-        add_bias(3, 1)
-        quantize_rows(LAST, PASSES, 2)
-        copy_agg(5, 1)
-        relu_store(3, 1)
-        scale_turned(LAST, 1, 2)
-        aggregate(LAST, 0)
-        for h in range(2):
-            turn_back(SIDE, h)
         project(4, 1)
-        aggregate(LAST, 1, (0, 1))
-        copy_agg(LAST, 0)
-        quantize_agg(5)
-        quantize_rows(LAST, PASSES + 2, 2)
+        scale_turned(LAST, 1, 0)
+        aggregate(5, 1)
+        quantize_rows(LAST, 0, PASSES)
+        quantize_rows(LAST, PASSES, 2)
+        scale_turned(LAST, 1, 2, 1, 0, False)
+        add_bias(3, 1)
+        quantize_rows(LAST, PASSES + 2, 1)
+        relu_store(SIDE, 0)
+        copy_agg(5, 0)
+        relu_store(SIDE, 1)
+        aggregate(LAST, 0)
+        relu_store(3, 0)
+        copy_agg(5, 1)
         add_bias(4, 0)
         add_bias(4, 1)
-        for h in range(2):
-            store_back(SIDE, h)
+        scale_turned(LAST, 1, 3, 1, 1)
+        quantize_agg(5)
+        quantize_rows(LAST, PASSES + 3, 1)
+        aggregate(LAST, 1, (0, 1, 2))
         project(5, 0)
-        aggregate(LAST, 1, (2, 3))
+        aggregate(LAST, 1, (3,))
         project(5, 1)
-        relu_store(4, 0)
-        copy_agg(LAST, 1)
+        relu_store(3, 1)
+        copy_agg(LAST, 0)
+        relu_store(4, 0, "vector")
+        relu_store(4, 1)
         quantize_agg(LAST, 0, 1)
         project(LAST, 0)
         add_bias(5, 0)
+        copy_agg(LAST, 1)
         add_bias(5, 1)
         quantize_agg(LAST, 1, 1)
-        project(LAST, 1, 0, D // 2)
-        project(LAST, 1, D // 2, D)
-        relu_store(4, 1)
         relu_store(5, 0)
         add_bias(LAST, 0)
-        add_bias(LAST, 1, 0, D // 2)
-        add_bias(LAST, 1, D // 2, D)
+        project(LAST, 1, 0, D // 2)
+        project(LAST, 1, D // 2, D)
         relu_store(5, 1)
         relu_store(LAST, 0)
+        add_bias(LAST, 1, 0, D // 2)
+        add_bias(LAST, 1, D // 2, D)
         relu_store(LAST, 1, "vector", 0, D // 2)
         relu_store(LAST, 1, "vector", D // 2, D)

@@ -26,8 +26,8 @@ LAST = SIDE - 1
 TURN_BANKS = 4
 SHARE = 512
 UNITS = 128
-POOL_UNITS = 72
-EARLY_UNITS = 88
+POOL_UNITS = 68
+EARLY_UNITS = 86
 FIRST_UNITS = 48
 HALVED = (0, SIDE)
 BY_TILE = (0, 1, LAST)
@@ -58,6 +58,7 @@ def tile_net_pa_w4_kernel(tc, A_bytes, A_scale, features, Wg_words, Wg_scales, b
         w_words = keep.tile([P, 2 * D], U8, name="wwords", align_bytes=64)
         w_scales = keep.tile([P, D], U8, name="wscales", align_bytes=64)
         side_wide = keep.tile([P, PAIR], BF16, name="sidewide", align_bytes=64)
+        side_sums = keep.tile([P, 2, D], F32, name="sidesums", align_bytes=64)
         ident = keep.tile([P, P], F32, name="ident", align_bytes=64)
         ident_bf = keep.tile([P, P], BF16, name="identbf", align_bytes=64)
 
@@ -111,11 +112,13 @@ def tile_net_pa_w4_kernel(tc, A_bytes, A_scale, features, Wg_words, Wg_scales, b
                 bias_banks.append(take_bank("bias", [P, 4, P]))
             for c in chunks:
                 column = bias_chunks[:, c : c + 1].to_broadcast([P, P])
-                nc.tensor.transpose(bias_banks[0][:, c, :], column, ident[:])
+                nc.tensor.matmul(bias_banks[0][:, c, :], lhsT=column, rhs=ident[:], start=True, stop=True)
 
-        def copy_bias():
-            nc.scalar.copy(out=bias_row[:], in_=bias_banks[0][:].rearrange("p c n -> p (c n)"))
-            give_bank("bias")
+        def copy_bias(half):
+            cols = slice(half * D // 2, (half + 1) * D // 2)
+            nc.scalar.copy(out=bias_row[:, cols], in_=bias_banks[0][:].rearrange("p c n -> p (c n)")[:, cols])
+            if half:
+                give_bank("bias")
 
         def copy_on(engine, dst, src):
             if engine == "scalar":
@@ -360,6 +363,12 @@ def tile_net_pa_w4_kernel(tc, A_bytes, A_scale, features, Wg_words, Wg_scales, b
             )
             give_bank(("product", n, h, first))
 
+        def cap_side(h):
+            nc.vector.scalar_tensor_tensor(
+                out=side_sums[:, h], in0=product[SIDE, h, 0][:], scalar=-1.0, in1=bias_row[:], op0=ALU.mult, op1=ALU.min
+            )
+            give_bank(("product", SIDE, h, 0))
+
         rows = {}
 
         def rows_tile(n, h):
@@ -378,6 +387,15 @@ def tile_net_pa_w4_kernel(tc, A_bytes, A_scale, features, Wg_words, Wg_scales, b
             else:
                 nc.scalar.activation(out=dst, in_=src, func=ACT.Relu)
             store(n, h, first, last)
+
+        def relu_store_side():
+            both = keep.tile([P, 2, D], F32, name="aggbf3", align_bytes=64)
+            nc.gpsimd.tensor_tensor(
+                out=both[:], in0=bias_row[:].unsqueeze(1).to_broadcast([P, 2, D]), in1=side_sums[:], op=ALU.subtract
+            )
+            for h in range(2):
+                rows[SIDE, h] = both[:, h]
+                store(SIDE, h)
 
         def project_turned(n, half):
             product[n, half] = take_bank(("product", n, half), [P, 2, 2 * P])
@@ -417,7 +435,6 @@ def tile_net_pa_w4_kernel(tc, A_bytes, A_scale, features, Wg_words, Wg_scales, b
             store(n, h)
 
         make_identity(nc, ident[:])
-        make_identity(nc, ident_bf[:])
         nc.vector.memset(w_scales[:].bitcast(I32), 0)
 
         load_a(0, 0, 0, PASS)
@@ -454,16 +471,14 @@ def tile_net_pa_w4_kernel(tc, A_bytes, A_scale, features, Wg_words, Wg_scales, b
         for g in range(PASSES):
             scale_turned(0, 0, g, 1)
             turn(0, 1, g, 1)
-            if g:
-                spread_bias((g,))
-        spread_bias((0,))
         f_grouped[1] = keep.tile([P, 4, P, 4], BF16, name="stage0", align_bytes=64)
         group_features(1, "scalar", 0, UNITS // 2)
-        copy_bias()
         for g in range(PASSES):
             scale_turned(0, 1, g, 1)
-        turn_by_matmul(1, 0, 0)
-        turn_by_matmul(1, 0, 2)
+        turn(1, 0, 0)
+        turn(1, 0, 2)
+        spread_bias((0, 1))
+        copy_bias(0)
         quantize_rows(0, 0, PASSES)
         quantize_rows(0, PASSES, PASSES)
         quantize_features(0)
@@ -481,30 +496,32 @@ def tile_net_pa_w4_kernel(tc, A_bytes, A_scale, features, Wg_words, Wg_scales, b
         widen(3 * PAIR - QUARTER, 3 * PAIR, "scalar")
         aggregate(0, 0, (0,))
         aggregate(0, 1, (0,))
-        turn_by_matmul(1, 1, 0)
+        turn(1, 1, 0)
         turn(1, 1, 2)
         aggregate(0, 0, (1,))
         aggregate(0, 1, (1,))
         scale_turned(1, 0, 0)
         scale_turned(1, 0, 2)
         turn(2, 0, 0)
-        turn_by_matmul(2, 0, 2)
+        turn(2, 0, 2)
+        spread_bias((2, 3))
         turn_side(0)
+        copy_bias(1)
         scale_side(0, (0, 1))
         widen_side(1)
-        scale_side(0, (2, 3))
         scale_turned(1, 1, 0)
         scale_turned(1, 1, 2)
         turn(2, 1, 0)
-        turn(2, 1, 2)
         quantize_features(2)
         quantize_rows(1)
 
         widen(starts[3], starts[4], "gpsimd")
         aggregate(0, 0, (2, 3))
         aggregate(0, 1, (2, 3))
+        turn(2, 1, 2)
         turn_side(1)
         copy_agg(0, 0)
+        scale_side(0, (2, 3))
         copy_agg(0, 1)
         aggregate(1, 0)
         aggregate(1, 1)
@@ -529,6 +546,7 @@ def tile_net_pa_w4_kernel(tc, A_bytes, A_scale, features, Wg_words, Wg_scales, b
         project_turned(0, 0)
         project_turned(0, 1)
         turn(3, 1, 0)
+        turn(3, 1, 2)
         widen_side(3)
         scale_side(2)
         relu_of_turned(0, 0)
@@ -536,17 +554,18 @@ def tile_net_pa_w4_kernel(tc, A_bytes, A_scale, features, Wg_words, Wg_scales, b
         for g in range(3):
             group_side(g)
         aggregate(2, 0)
-        turn(3, 1, 2)
         scale_turned(3, 0, 0)
         turn_side(3, turn_names)
-        aggregate(2, 1)
+        aggregate(2, 1, (0, 1))
         for h in range(2):
             turn_back(0, h)
+        scale_turned(3, 0, 2)
+        turn(4, 0, 0)
+        aggregate(2, 1, (2, 3))
         copy_agg(2, 0)
         copy_agg(2, 1)
         for h in range(2):
             store_back(0, h)
-        scale_turned(3, 0, 2)
         scale_turned(3, 1, 0)
         scale_turned(3, 1, 2)
         scale_side_on_vector(3)
@@ -556,8 +575,7 @@ def tile_net_pa_w4_kernel(tc, A_bytes, A_scale, features, Wg_words, Wg_scales, b
         quantize_agg(1)
         quantize_rows(3)
         widen(starts[5], starts[6] - SHARE, "gpsimd")
-        turn(4, 0, 0)
-        turn_by_matmul(4, 0, 2)
+        turn(4, 0, 2)
         turn(4, 1, 0)
         aggregate(SIDE, 0)
         project_turned(1, 0)
@@ -599,8 +617,8 @@ def tile_net_pa_w4_kernel(tc, A_bytes, A_scale, features, Wg_words, Wg_scales, b
         project_turned(2, 1)
         scale_turned(5, 0, 2)
         scale_turned(5, 1, 0)
-        add_bias(SIDE, 0)
-        add_bias(SIDE, 1)
+        cap_side(0)
+        cap_side(1)
         aggregate(4, 0)
         turn(LAST, 0, 2)
         group_on_scalar(5, 0, 0)
@@ -616,6 +634,7 @@ def tile_net_pa_w4_kernel(tc, A_bytes, A_scale, features, Wg_words, Wg_scales, b
 
         quantize_agg(3)
         quantize_rows(5)
+        relu_store_side()
         project(3, 0)
         turn(LAST, 1, 0)
         for h in range(2):
@@ -624,24 +643,23 @@ def tile_net_pa_w4_kernel(tc, A_bytes, A_scale, features, Wg_words, Wg_scales, b
         turn(LAST, 1, 2)
         scale_turned(LAST, 0, 2)
         add_bias(3, 0)
+        scale_turned(LAST, 1, 0)
         quantize_agg(4)
         project(3, 1)
         project(4, 0)
         for h in range(2):
             store_back(2, h)
         project(4, 1)
-        scale_turned(LAST, 1, 0)
         aggregate(5, 1)
         quantize_rows(LAST, 0, PASSES)
         quantize_rows(LAST, PASSES, 2)
         scale_turned(LAST, 1, 2, 1, 0, False)
         add_bias(3, 1)
         quantize_rows(LAST, PASSES + 2, 1)
-        relu_store(SIDE, 0)
         copy_agg(5, 0)
-        relu_store(SIDE, 1)
         aggregate(LAST, 0)
         relu_store(3, 0)
+        relu_store(3, 1)
         copy_agg(5, 1)
         add_bias(4, 0)
         add_bias(4, 1)
@@ -652,9 +670,8 @@ def tile_net_pa_w4_kernel(tc, A_bytes, A_scale, features, Wg_words, Wg_scales, b
         project(5, 0)
         aggregate(LAST, 1, (3,))
         project(5, 1)
-        relu_store(3, 1)
+        relu_store(4, 0)
         copy_agg(LAST, 0)
-        relu_store(4, 0, "vector")
         relu_store(4, 1)
         quantize_agg(LAST, 0, 1)
         project(LAST, 0)

@@ -58,7 +58,6 @@ def tile_net_pa_w4_kernel(tc, A_bytes, A_scale, features, Wg_words, Wg_scales, b
         w_words = keep.tile([P, 2 * D], U8, name="wwords", align_bytes=64)
         w_scales = keep.tile([P, D], U8, name="wscales", align_bytes=64)
         side_wide = keep.tile([P, PAIR], BF16, name="sidewide", align_bytes=64)
-        side_sums = keep.tile([P, 2, D], F32, name="sidesums", align_bytes=64)
         ident = keep.tile([P, P], F32, name="ident", align_bytes=64)
         ident_bf = keep.tile([P, P], BF16, name="identbf", align_bytes=64)
 
@@ -363,12 +362,6 @@ def tile_net_pa_w4_kernel(tc, A_bytes, A_scale, features, Wg_words, Wg_scales, b
             )
             give_bank(("product", n, h, first))
 
-        def cap_side(h):
-            nc.vector.scalar_tensor_tensor(
-                out=side_sums[:, h], in0=product[SIDE, h, 0][:], scalar=-1.0, in1=bias_row[:], op0=ALU.mult, op1=ALU.min
-            )
-            give_bank(("product", SIDE, h, 0))
-
         rows = {}
 
         def rows_tile(n, h):
@@ -387,15 +380,6 @@ def tile_net_pa_w4_kernel(tc, A_bytes, A_scale, features, Wg_words, Wg_scales, b
             else:
                 nc.scalar.activation(out=dst, in_=src, func=ACT.Relu)
             store(n, h, first, last)
-
-        def relu_store_side():
-            both = keep.tile([P, 2, D], F32, name="aggbf3", align_bytes=64)
-            nc.gpsimd.tensor_tensor(
-                out=both[:], in0=bias_row[:].unsqueeze(1).to_broadcast([P, 2, D]), in1=side_sums[:], op=ALU.subtract
-            )
-            for h in range(2):
-                rows[SIDE, h] = both[:, h]
-                store(SIDE, h)
 
         def project_turned(n, half):
             product[n, half] = take_bank(("product", n, half), [P, 2, 2 * P])
@@ -617,8 +601,8 @@ def tile_net_pa_w4_kernel(tc, A_bytes, A_scale, features, Wg_words, Wg_scales, b
         project_turned(2, 1)
         scale_turned(5, 0, 2)
         scale_turned(5, 1, 0)
-        cap_side(0)
-        cap_side(1)
+        add_bias(SIDE, 0)
+        add_bias(SIDE, 1)
         aggregate(4, 0)
         turn(LAST, 0, 2)
         group_on_scalar(5, 0, 0)
@@ -634,7 +618,6 @@ def tile_net_pa_w4_kernel(tc, A_bytes, A_scale, features, Wg_words, Wg_scales, b
 
         quantize_agg(3)
         quantize_rows(5)
-        relu_store_side()
         project(3, 0)
         turn(LAST, 1, 0)
         for h in range(2):
@@ -656,10 +639,11 @@ def tile_net_pa_w4_kernel(tc, A_bytes, A_scale, features, Wg_words, Wg_scales, b
         scale_turned(LAST, 1, 2, 1, 0, False)
         add_bias(3, 1)
         quantize_rows(LAST, PASSES + 2, 1)
+        relu_store(SIDE, 0)
         copy_agg(5, 0)
+        relu_store(SIDE, 1)
         aggregate(LAST, 0)
         relu_store(3, 0)
-        relu_store(3, 1)
         copy_agg(5, 1)
         add_bias(4, 0)
         add_bias(4, 1)
@@ -670,8 +654,9 @@ def tile_net_pa_w4_kernel(tc, A_bytes, A_scale, features, Wg_words, Wg_scales, b
         project(5, 0)
         aggregate(LAST, 1, (3,))
         project(5, 1)
-        relu_store(4, 0)
+        relu_store(3, 1)
         copy_agg(LAST, 0)
+        relu_store(4, 0, "vector")
         relu_store(4, 1)
         quantize_agg(LAST, 0, 1)
         project(LAST, 0)

@@ -25,14 +25,14 @@ SIDE = 7
 LAST = SIDE - 1
 TURN_BANKS = 4
 SHARE = 512
-UNITS = 128
-POOL_UNITS = 68
-EARLY_UNITS = 86
-FIRST_UNITS = 48
+UNITS = 64
+EARLY_UNITS = 10
+FIRST_UNITS = 44
 HALVED = (0, SIDE)
 BY_TILE = (0, 1, LAST)
 RELEASES = {0: "stage1", 1: "stage2", SIDE: "stage0"}
 STARTS = [3 * PAIR + QUARTER, 4 * PAIR + PASS, 5 * PAIR + QUARTER, 6 * PAIR + QUARTER]
+FIRST_ORDER = (0, 1, 3, 2)
 FLOPS = 2 * NODES * NODES * D + 2 * NODES * D * D
 
 
@@ -45,16 +45,14 @@ def tile_net_pa_w4_kernel(tc, A_bytes, A_scale, features, Wg_words, Wg_scales, b
 
         a_bytes = keep.tile([P, SIDE * PAIR], U8, name="abytes", align_bytes=64)
         side_bytes = keep.tile([P, PAIR], U8, name="sidebytes", align_bytes=64)
-        scale_cols = keep.tile([P, PASSES, 4], F32, name="scalecols")
-        bias_raw = keep.tile([P, 4, 2], BF16, name="biasraw")
+        scale_cols = keep.tile([P, PASSES, 8], F32, name="scalecols", align_bytes=64)
+        bias_raw = keep.tile([P, P], BF16, name="biasraw", align_bytes=64)
+        bias_lines = keep.tile([P, P], F32, name="biaslines", align_bytes=64)
         bias_chunks = keep.tile([P, 4], F32, name="biaschunks")
         bias_row = keep.tile([P, D], F32, name="biasrow", align_bytes=64)
-        f_raw = [keep.tile([P, 4, D], BF16, name="fraw%d" % g, align_bytes=64) for g in range(2)]
-        f_raw_late = keep.tile([P, 4, 2 * D], BF16, name="frawlate", align_bytes=64)
-        f_codes = [keep.tile([P, 4, P], U32, name="fcodes%d" % g, align_bytes=64) for g in range(2)]
-        f_scales = [keep.tile([P, 4, P], U8, name="fscales%d" % g, align_bytes=64) for g in range(2)]
-        f_codes_late = keep.tile([P, 4, 2 * P], U32, name="fcodeslate", align_bytes=64)
-        f_scales_late = keep.tile([P, 4, 2 * P], U8, name="fscaleslate", align_bytes=64)
+        f_raw = [keep.tile([P, 4, D], BF16, name="fraw%d" % g, align_bytes=64) for g in range(PASSES)]
+        f_codes = [keep.tile([P, 4, P], U32, name="fcodes%d" % g, align_bytes=64) for g in range(PASSES)]
+        f_scales = [keep.tile([P, 4, P], U8, name="fscales%d" % g, align_bytes=64) for g in range(PASSES)]
         w_words = keep.tile([P, 2 * D], U8, name="wwords", align_bytes=64)
         w_scales = keep.tile([P, D], U8, name="wscales", align_bytes=64)
         side_wide = keep.tile([P, PAIR], BF16, name="sidewide", align_bytes=64)
@@ -93,8 +91,11 @@ def tile_net_pa_w4_kernel(tc, A_bytes, A_scale, features, Wg_words, Wg_scales, b
             )
 
         def load_f(g):
-            dst = f_raw[g][:] if g < 2 else f_raw_late[:, :, (g - 2) * D : (g - 1) * D]
-            nc.sync.dma_start(out=dst, in_=features.rearrange("(g p j) c -> g p j c", p=P, j=4)[g])
+            nc.sync.dma_start(out=f_raw[g][:], in_=features.rearrange("(g p j) c -> g p j c", p=P, j=4)[g])
+
+        def load_scales(first, last):
+            src = A_scale.rearrange("o (g p t) -> p (o g) t", p=P, t=4)
+            nc.sync.dma_start(out=scale_cols[:, first:last, 0:4], in_=src[:, first:last])
 
         def load_w():
             nc.sync.dma_start(out=w_words[:], in_=Wg_words.rearrange("g p w -> p (g w)"))
@@ -110,14 +111,21 @@ def tile_net_pa_w4_kernel(tc, A_bytes, A_scale, features, Wg_words, Wg_scales, b
             if not bias_banks:
                 bias_banks.append(take_bank("bias", [P, 4, P]))
             for c in chunks:
-                column = bias_chunks[:, c : c + 1].to_broadcast([P, P])
-                nc.tensor.matmul(bias_banks[0][:, c, :], lhsT=column, rhs=ident[:], start=True, stop=True)
+                pick = ident[:, c : c + 1].to_broadcast([P, P])
+                nc.tensor.matmul(bias_banks[0][:, c, :], lhsT=pick, rhs=bias_lines[:], start=True, stop=True)
 
-        def copy_bias(half):
-            cols = slice(half * D // 2, (half + 1) * D // 2)
-            nc.scalar.copy(out=bias_row[:, cols], in_=bias_banks[0][:].rearrange("p c n -> p (c n)")[:, cols])
-            if half:
-                give_bank("bias")
+        def bias_to_partitions():
+            bank = take_bank("chunks", [P, P])
+            nc.tensor.transpose(bank[:], bias_lines[:], ident[:])
+            return bank
+
+        def copy_chunks(bank):
+            nc.scalar.copy(out=bias_chunks[:], in_=bank[:, 0:4])
+            give_bank("chunks")
+
+        def copy_bias():
+            nc.scalar.copy(out=bias_row[:], in_=bias_banks[0][:].rearrange("p c n -> p (c n)"))
+            give_bank("bias")
 
         def copy_on(engine, dst, src):
             if engine == "scalar":
@@ -130,13 +138,13 @@ def tile_net_pa_w4_kernel(tc, A_bytes, A_scale, features, Wg_words, Wg_scales, b
         f_grouped = {}
 
         def group_features(g, engine, first, last):
-            raw = f_raw[g] if g < 2 else f_raw_late
+            raw = f_raw[g]
             dst = f_grouped[g][:].rearrange("p t (m i) j -> p m t i j", i=2)[:, first:last]
             src = raw[:].rearrange("p j (m i t) -> p m t i j", i=2, t=4)[:, first:last]
             copy_on(engine, dst, src)
 
         def quantize_features(g):
-            codes, scales = (f_codes[g], f_scales[g]) if g < 2 else (f_codes_late, f_scales_late)
+            codes, scales = f_codes[g], f_scales[g]
             nc.vector.quantize_mx(
                 out=codes[:].rearrange("p t m -> p (t m)").bitcast(FP8X4),
                 scales=scales[:].rearrange("p t m -> p (t m)"),
@@ -144,10 +152,7 @@ def tile_net_pa_w4_kernel(tc, A_bytes, A_scale, features, Wg_words, Wg_scales, b
             )
 
         def features_operand(g, t):
-            if g < 2:
-                return f_codes[g][:, t], f_scales[g][:, t]
-            cols = slice((g - 2) * P, (g - 1) * P)
-            return f_codes_late[:, t, cols], f_scales_late[:, t, cols]
+            return f_codes[g][:, t], f_scales[g][:, t]
 
         wide, grouped, a_codes, a_scales, turned = {}, {}, {}, {}, {}
         agg_banks, agg_bf, agg_codes, agg_scales = {}, {}, {}, {}
@@ -210,7 +215,7 @@ def tile_net_pa_w4_kernel(tc, A_bytes, A_scale, features, Wg_words, Wg_scales, b
             return grouped[key][:, first % width : first % width + (count - 1) * step + 1 : step]
 
         def scale_turned(n, h, first, count=2, skip=0, last=True):
-            scales = scale_cols[:, first : first + count, :].rearrange("p g (u e) -> p g u e", u=2)
+            scales = scale_cols[:, first : first + count, 0:4].rearrange("p g (u e) -> p g u e", u=2)
             dst = grouped_slots(n, slot_of(n, h, first), count, 1 if n == LAST else 2)
             if (n, h, first) in by_matmul:
                 values = turned[n, h, first][:].rearrange("p g (u e) i -> p g i u e", u=2)
@@ -248,7 +253,7 @@ def tile_net_pa_w4_kernel(tc, A_bytes, A_scale, features, Wg_words, Wg_scales, b
                 give_bank(("side", g))
 
         def scale_side_on_vector(g):
-            scales = scale_cols[:, g : g + 1, :].rearrange("p g (u e) -> p g u e", u=2)
+            scales = scale_cols[:, g : g + 1, 0:4].rearrange("p g (u e) -> p g u e", u=2)
             nc.vector.tensor_tensor(
                 out=grouped_slots(SIDE, 2 * g, 2).rearrange("p h i (u e) -> p (h i) u e", u=2),
                 in0=side_banks[g][:].bitcast(BF16).rearrange("p u h (i e) -> p (h i) u e", e=2),
@@ -419,13 +424,15 @@ def tile_net_pa_w4_kernel(tc, A_bytes, A_scale, features, Wg_words, Wg_scales, b
             store(n, h)
 
         make_identity(nc, ident[:])
+        nc.vector.memset(bias_raw[:], 0.0)
         nc.vector.memset(w_scales[:].bitcast(I32), 0)
 
         load_a(0, 0, 0, PASS)
-        nc.sync.dma_start(out=scale_cols[:], in_=A_scale.rearrange("o (g p t) -> p (o g) t", p=P, t=4))
+        load_scales(0, 1)
         load_a(0, 0, PASS, NODES)
+        nc.sync.dma_start(out=bias_raw[0:4, :], in_=bg.rearrange("(c n) -> c n", n=P))
+        load_scales(1, PASSES)
         load_a(0, 1)
-        nc.sync.dma_start(out=bias_raw[:, :, 0:1], in_=bg.rearrange("(c p o) -> p c o", p=P, o=1))
         load_f(0)
         load_a(1, 0)
         load_f(1)
@@ -442,13 +449,13 @@ def tile_net_pa_w4_kernel(tc, A_bytes, A_scale, features, Wg_words, Wg_scales, b
         widen(0, PASS, "vector")
         for g in range(1, PASSES):
             widen(g * PASS, (g + 1) * PASS, "scalar")
+        nc.scalar.copy(out=bias_lines[:], in_=bias_raw[:])
         f_grouped[0] = keep.tile([P, 4, P, 4], BF16, name="fgrouped0", align_bytes=64)
         group_features(0, "gpsimd", 0, FIRST_UNITS)
         widen(NODES, NODES + PASS, "scalar")
         widen(NODES + PASS, NODES + QUARTER, "scalar")
         widen(NODES + QUARTER, PAIR, "scalar")
-        nc.scalar.copy(out=bias_chunks[:], in_=bias_raw[:, :, 0])
-        group_features(0, "scalar", FIRST_UNITS, UNITS // 2)
+        group_features(0, "scalar", FIRST_UNITS, UNITS)
         widen(PAIR, PAIR + NODES, "scalar")
         for g in range(PASSES):
             turn(0, 0, g, 1)
@@ -456,25 +463,27 @@ def tile_net_pa_w4_kernel(tc, A_bytes, A_scale, features, Wg_words, Wg_scales, b
             scale_turned(0, 0, g, 1)
             turn(0, 1, g, 1)
         f_grouped[1] = keep.tile([P, 4, P, 4], BF16, name="stage0", align_bytes=64)
-        group_features(1, "scalar", 0, UNITS // 2)
+        group_features(1, "scalar", 0, UNITS)
         for g in range(PASSES):
             scale_turned(0, 1, g, 1)
         turn(1, 0, 0)
         turn(1, 0, 2)
+        chunks = bias_to_partitions()
         spread_bias((0, 1))
-        copy_bias(0)
+        copy_chunks(chunks)
         quantize_rows(0, 0, PASSES)
         quantize_rows(0, PASSES, PASSES)
         quantize_features(0)
         quantize_features(1)
 
-        f_grouped[2] = keep.tile([P, 4, 2 * P, 4], BF16, name="stage0", align_bytes=64)
-        group_features(2, "gpsimd", 0, POOL_UNITS)
-        group_features(2, "scalar", POOL_UNITS, EARLY_UNITS)
+        f_grouped[2] = keep.tile([P, 4, P, 4], BF16, name="stage0", align_bytes=64)
+        f_grouped[3] = keep.tile([P, 4, P, 4], BF16, name="fgrouped3", align_bytes=64)
+        group_features(2, "gpsimd", 0, UNITS)
+        group_features(3, "scalar", 0, EARLY_UNITS)
         widen(PAIR + NODES, PAIR + NODES + QUARTER, "scalar")
         widen(PAIR + NODES + QUARTER, 2 * PAIR, "scalar")
         widen(2 * PAIR, 2 * PAIR + NODES, "scalar")
-        group_features(2, "scalar", EARLY_UNITS, UNITS)
+        group_features(3, "scalar", EARLY_UNITS, UNITS)
         widen_side(0)
         widen(2 * PAIR + NODES, 3 * PAIR - QUARTER, "scalar")
         widen(3 * PAIR - QUARTER, 3 * PAIR, "scalar")
@@ -490,18 +499,20 @@ def tile_net_pa_w4_kernel(tc, A_bytes, A_scale, features, Wg_words, Wg_scales, b
         turn(2, 0, 2)
         spread_bias((2, 3))
         turn_side(0)
-        copy_bias(1)
+        copy_bias()
         scale_side(0, (0, 1))
         widen_side(1)
         scale_turned(1, 1, 0)
         scale_turned(1, 1, 2)
-        turn(2, 1, 0)
+        quantize_features(3)
         quantize_features(2)
         quantize_rows(1)
 
         widen(starts[3], starts[4], "gpsimd")
-        aggregate(0, 0, (2, 3))
-        aggregate(0, 1, (2, 3))
+        for g in (3, 2):
+            for h in range(2):
+                aggregate(0, h, (g,), FIRST_ORDER)
+        turn(2, 1, 0)
         turn(2, 1, 2)
         turn_side(1)
         copy_agg(0, 0)

@@ -27,7 +27,6 @@ TURN_BANKS = 4
 SHARE = 512
 UNITS = 64
 EARLY_UNITS = 10
-FIRST_UNITS = 44
 HALVED = (0, SIDE)
 BY_TILE = (0, 1, LAST)
 RELEASES = {0: "stage1", 1: "stage2", SIDE: "stage0"}
@@ -432,8 +431,9 @@ def tile_net_pa_w4_kernel(tc, A_bytes, A_scale, features, Wg_words, Wg_scales, b
         load_a(0, 0, PASS, NODES)
         nc.sync.dma_start(out=bias_raw[0:4, :], in_=bg.rearrange("(c n) -> c n", n=P))
         load_scales(1, PASSES)
-        load_a(0, 1)
+        load_a(0, 1, 0, QUARTER)
         load_f(0)
+        load_a(0, 1, QUARTER, NODES)
         load_a(1, 0)
         load_f(1)
         load_f(2)
@@ -451,11 +451,10 @@ def tile_net_pa_w4_kernel(tc, A_bytes, A_scale, features, Wg_words, Wg_scales, b
             widen(g * PASS, (g + 1) * PASS, "scalar")
         nc.scalar.copy(out=bias_lines[:], in_=bias_raw[:])
         f_grouped[0] = keep.tile([P, 4, P, 4], BF16, name="fgrouped0", align_bytes=64)
-        group_features(0, "gpsimd", 0, FIRST_UNITS)
+        group_features(0, "gpsimd", 0, UNITS)
         widen(NODES, NODES + PASS, "scalar")
         widen(NODES + PASS, NODES + QUARTER, "scalar")
         widen(NODES + QUARTER, PAIR, "scalar")
-        group_features(0, "scalar", FIRST_UNITS, UNITS)
         widen(PAIR, PAIR + NODES, "scalar")
         for g in range(PASSES):
             turn(0, 0, g, 1)

from contextlib import ExitStack

import concourse.mybir as mybir
from concourse.masks import make_identity

F32 = mybir.dt.float32
BF16 = mybir.dt.bfloat16
U32 = mybir.dt.uint32
I32 = mybir.dt.int32
U8 = mybir.dt.uint8
FP8 = mybir.dt.float8_e4m3fn
FP8X4 = mybir.dt.float8_e4m3fn_x4
FP4X4 = mybir.dt.float4_e2m1fn_x4
ALU = mybir.AluOpType
ACT = mybir.ActivationFunctionType

NODES = 2048
D = 512
P = 128
PASS = 512
QUARTER = 1024
PAIR = 4 * QUARTER
PASSES = NODES // PASS
SIDE = 7
LAST = SIDE - 1
TURN_BANKS = 4
SHARE = 512
UNITS = 64
EARLY_UNITS = 10
HALVED = (0, SIDE)
BY_TILE = (0, 1, LAST)
RELEASES = {0: "stage1", 1: "stage2", SIDE: "stage0"}
STARTS = [3 * PAIR + QUARTER, 4 * PAIR + PASS, 5 * PAIR + QUARTER, 6 * PAIR + QUARTER]
FIRST_ORDER = (0, 1, 3, 2)
FLOPS = 2 * NODES * NODES * D + 2 * NODES * D * D


def tile_net_pa_w4_kernel(tc, A_bytes, A_scale, features, Wg_words, Wg_scales, bg, out):
    nc = tc.nc
    with ExitStack() as ctx:
        keep = ctx.enter_context(tc.tile_pool(name="keep", bufs=1))
        psum = ctx.enter_context(tc.psum_pool(name="psum", bufs=1))
        ctx.enter_context(tc.manual_schedule())

        a_bytes = keep.tile([P, SIDE * PAIR], U8, name="abytes", align_bytes=64)
        side_bytes = keep.tile([P, PAIR], U8, name="sidebytes", align_bytes=64)
        scale_cols = keep.tile([P, PASSES, 8], F32, name="scalecols", align_bytes=64)
        bias_raw = keep.tile([P, P], BF16, name="biasraw", align_bytes=64)
        bias_lines = keep.tile([P, P], F32, name="biaslines", align_bytes=64)
        bias_chunks = keep.tile([P, 4], F32, name="biaschunks")
        bias_row = keep.tile([P, D], F32, name="biasrow", align_bytes=64)
        f_raw = [keep.tile([P, 4, D], BF16, name="fraw%d" % g, align_bytes=64) for g in range(PASSES)]
        f_codes = [keep.tile([P, 4, P], U32, name="fcodes%d" % g, align_bytes=64) for g in range(PASSES)]
        f_scales = [keep.tile([P, 4, P], U8, name="fscales%d" % g, align_bytes=64) for g in range(PASSES)]
        w_words = keep.tile([P, 2 * D], U8, name="wwords", align_bytes=64)
        w_scales = keep.tile([P, D], U8, name="wscales", align_bytes=64)
        side_wide = keep.tile([P, PAIR], BF16, name="sidewide", align_bytes=64)
        ident = keep.tile([P, P], F32, name="ident", align_bytes=64)
        ident_bf = keep.tile([P, P], BF16, name="identbf", align_bytes=64)

        bank_names = ["other%d" % b for b in range(8 - TURN_BANKS)]
        turn_names = ["turn%d" % b for b in range(TURN_BANKS)]

        held = {}

        def take_bank(key, shape, names=bank_names, dtype=F32):
            name = names[0]
            names.remove(name)
            held[key] = (name, names)
            return psum.tile(shape, dtype, name=name)

        def give_bank(key, names=None):
            name, home = held[key]
            (home if names is None else names).append(name)

        def ring(name, index, depth, shape, dtype):
            return keep.tile(shape, dtype, name="%s%d" % (name, index % depth), align_bytes=64)

        def load_a(n, h, first=0, last=NODES):
            r0 = (2 * n + h) * P
            nc.sync.dma_start(
                out=a_bytes[:, (2 * n + h) * NODES + first : (2 * n + h) * NODES + last], in_=A_bytes[r0 : r0 + P, first:last]
            )

        def load_pair(n):
            dst = side_bytes[:] if n == SIDE else a_bytes[:, n * PAIR : (n + 1) * PAIR]
            nc.sync.dma_start(
                out=dst.rearrange("p (h k) -> p h k", h=2),
                in_=A_bytes[2 * n * P : 2 * (n + 1) * P, :].rearrange("(h p) k -> p h k", p=P),
            )

        def load_f(g):
            nc.sync.dma_start(out=f_raw[g][:], in_=features.rearrange("(g p j) c -> g p j c", p=P, j=4)[g])

        def load_scales(first, last):
            src = A_scale.rearrange("o (g p t) -> p (o g) t", p=P, t=4)
            nc.sync.dma_start(out=scale_cols[:, first:last, 0:4], in_=src[:, first:last])

        def load_w():
            nc.sync.dma_start(out=w_words[:], in_=Wg_words.rearrange("g p w -> p (g w)"))
            for q in range(4):
                nc.sync.dma_start(
                    out=w_scales[32 * q : 32 * q + 4, :].bitcast(I32),
                    in_=Wg_scales.rearrange("g q n -> (g q) n")[4 * q : 4 * q + 4, :].bitcast(I32),
                )

        bias_banks = []

        def spread_bias(chunks):
            if not bias_banks:
                bias_banks.append(take_bank("bias", [P, 4, P]))
            for c in chunks:
                pick = ident[:, c : c + 1].to_broadcast([P, P])
                nc.tensor.matmul(bias_banks[0][:, c, :], lhsT=pick, rhs=bias_lines[:], start=True, stop=True)

        def bias_to_partitions():
            bank = take_bank("chunks", [P, P])
            nc.tensor.transpose(bank[:], bias_lines[:], ident[:])
            return bank

        def copy_chunks(bank):
            nc.scalar.copy(out=bias_chunks[:], in_=bank[:, 0:4])
            give_bank("chunks")

        def copy_bias():
            nc.scalar.copy(out=bias_row[:], in_=bias_banks[0][:].rearrange("p c n -> p (c n)"))
            give_bank("bias")

        def copy_on(engine, dst, src):
            if engine == "scalar":
                nc.scalar.copy(out=dst, in_=src)
            elif engine == "vector":
                nc.vector.tensor_copy(out=dst, in_=src)
            else:
                nc.gpsimd.tensor_copy(out=dst, in_=src)

        f_grouped = {}

        def group_features(g, engine, first, last):
            raw = f_raw[g]
            dst = f_grouped[g][:].rearrange("p t (m i) j -> p m t i j", i=2)[:, first:last]
            src = raw[:].rearrange("p j (m i t) -> p m t i j", i=2, t=4)[:, first:last]
            copy_on(engine, dst, src)

        def quantize_features(g):
            codes, scales = f_codes[g], f_scales[g]
            nc.vector.quantize_mx(
                out=codes[:].rearrange("p t m -> p (t m)").bitcast(FP8X4),
                scales=scales[:].rearrange("p t m -> p (t m)"),
                in_=f_grouped[g][:].rearrange("p t m j -> p (t m j)"),
            )

        def features_operand(g, t):
            return f_codes[g][:, t], f_scales[g][:, t]

        wide, grouped, a_codes, a_scales, turned = {}, {}, {}, {}, {}
        agg_banks, agg_bf, agg_codes, agg_scales = {}, {}, {}, {}
        product, relu_turned, summed, back, side_banks, side_planes = {}, {}, {}, {}, {}, {}

        starts = [0, PAIR, 2 * PAIR] + STARTS + [SIDE * PAIR]

        def wide_columns(first, last):
            n = max(m for m in range(SIDE) if starts[m] <= first)
            if n not in wide:
                name = "stage%d" % (n % 3) if n else "wide0"
                wide[n] = keep.tile([P, starts[n + 1] - starts[n]], BF16, name=name, align_bytes=64)
            return wide[n][:, first - starts[n] : last - starts[n]]

        def widen(first, last, engine):
            copy_on(engine, wide_columns(first, last), a_bytes[:, first:last].bitcast(FP8))

        def widen_side(g):
            for h in range(2):
                cols = slice(h * NODES + g * PASS, h * NODES + (g + 1) * PASS)
                nc.scalar.copy(out=side_wide[:, cols], in_=side_bytes[:, cols].bitcast(FP8))

        def turn(n, h, first, count=2, names=turn_names):
            bank = take_bank(("turn", n, h, first), [P, 2, count, P], names)
            turned[n, h, first] = bank
            for gl in range(count):
                col = (2 * n + h) * NODES + (first + gl) * PASS
                words = wide_columns(col, col + PASS).bitcast(F32)
                for u in range(2):
                    nc.tensor.transpose(bank[:, u, gl, :], words[:, u : 2 * P : 2], ident[:])

        by_matmul = []

        def turn_by_matmul(n, h, first):
            bank = take_bank(("turn", n, h, first), [P, 2, 4, P], turn_names, BF16)
            turned[n, h, first] = bank
            by_matmul.append((n, h, first))
            for gl in range(2):
                col = (2 * n + h) * NODES + (first + gl) * PASS
                values = wide_columns(col, col + PASS)
                for t in range(4):
                    nc.tensor.matmul(bank[:, gl, t, :], lhsT=values[:, t:PASS:4], rhs=ident_bf[:], start=True, stop=True)

        def by_tile(n):
            return n in BY_TILE

        def slot_of(n, h, g):
            return PASSES * h + g if n == LAST else 2 * g + h

        def grouped_slots(n, first, count, step=1):
            width = PASSES if n in HALVED else 2 * PASSES
            key = (n, first // width)
            if key not in grouped:
                if n in HALVED:
                    grouped[key] = keep.tile([P, width, P, 4], BF16, name=RELEASES.get(key, "half%d" % key[1]), align_bytes=64)
                elif n == SIDE:
                    grouped[key] = keep.tile([P, width, P, 4], BF16, name=RELEASES[key], align_bytes=64)
                else:
                    grouped[key] = ring("grouped", n, 2, [P, width, P, 4], BF16)
            return grouped[key][:, first % width : first % width + (count - 1) * step + 1 : step]

        def scale_turned(n, h, first, count=2, skip=0, last=True):
            scales = scale_cols[:, first : first + count, 0:4].rearrange("p g (u e) -> p g u e", u=2)
            dst = grouped_slots(n, slot_of(n, h, first), count, 1 if n == LAST else 2)
            if (n, h, first) in by_matmul:
                values = turned[n, h, first][:].rearrange("p g (u e) i -> p g i u e", u=2)
            else:
                bank = turned[n, h, first - skip][:, :, skip : skip + count]
                values = bank.bitcast(BF16).rearrange("p u g (i e) -> p g i u e", e=2)
            nc.vector.tensor_tensor(
                out=dst.rearrange("p g i (u e) -> p g i u e", u=2),
                in0=values,
                in1=scales.unsqueeze(2).to_broadcast([P, count, P, 2, 2]),
                op=ALU.mult,
            )
            if last:
                give_bank(("turn", n, h, first - skip), bank_names if n == LAST else turn_names)

        def turn_side(g, names=bank_names):
            side_banks[g] = take_bank(("side", g), [P, 2, 2, P], names)
            for h in range(2):
                words = side_wide[:, h * NODES + g * PASS : h * NODES + (g + 1) * PASS].bitcast(F32)
                for u in range(2):
                    nc.tensor.transpose(side_banks[g][:, u, h, :], words[:, u : 2 * P : 2], ident[:])

        def scale_side(g, slots=range(4)):
            if g not in side_planes:
                side_planes[g] = ring("sideplanes", g, 3, [P, 2, 2 * P, 2], BF16)
            values = side_banks[g][:].bitcast(BF16).rearrange("p u h (i e) -> p u (h i) e", e=2)
            for t in slots:
                nc.scalar.activation(
                    out=side_planes[g][:, t // 2, :, t % 2],
                    in_=values[:, t // 2, :, t % 2],
                    func=ACT.Copy,
                    scale=scale_cols[:, g, t : t + 1],
                )
            if slots[-1] == 3:
                give_bank(("side", g))

        def scale_side_on_vector(g):
            scales = scale_cols[:, g : g + 1, 0:4].rearrange("p g (u e) -> p g u e", u=2)
            nc.vector.tensor_tensor(
                out=grouped_slots(SIDE, 2 * g, 2).rearrange("p h i (u e) -> p (h i) u e", u=2),
                in0=side_banks[g][:].bitcast(BF16).rearrange("p u h (i e) -> p (h i) u e", e=2),
                in1=scales.to_broadcast([P, 2 * P, 2, 2]),
                op=ALU.mult,
            )
            give_bank(("side", g))

        def group_side(g):
            nc.scalar.copy(
                out=grouped_slots(SIDE, 2 * g, 2).rearrange("p h i t -> p (h i) t").bitcast(F32),
                in_=side_planes[g][:].rearrange("p u i e -> p u (i e)").bitcast(F32).rearrange("p u i -> p i u"),
            )

        def scale_on_scalar(n, h, first, g):
            if (n, h) not in side_planes:
                side_planes[n, h] = ring("sideplanes", n, 3, [P, 2, 2, P, 2], BF16)
            values = turned[n, h, first][:].bitcast(BF16).rearrange("p u g (i e) -> p g u i e", e=2)
            for t in range(4):
                nc.scalar.activation(
                    out=side_planes[n, h][:, g - first, t // 2, :, t % 2],
                    in_=values[:, g - first, t // 2, :, t % 2],
                    func=ACT.Copy,
                    scale=scale_cols[:, g, t : t + 1],
                )
            if g == first + 1:
                give_bank(("turn", n, h, first), bank_names if n == LAST else turn_names)

        def group_on_scalar(n, h, first):
            nc.scalar.copy(
                out=grouped_slots(n, slot_of(n, h, first), 2, 1 if n == LAST else 2).bitcast(F32),
                in_=side_planes[n, h][:].rearrange("p g u i e -> p g u (i e)").bitcast(F32).rearrange("p g u i -> p g i u"),
            )

        def quantize_rows(n, first=0, count=2 * PASSES):
            if n not in a_codes:
                a_codes[n] = ring("acodes", n, 3, [P, 2 * PASSES, P], U32)
                a_scales[n] = ring("ascales", n, 3, [P, 2 * PASSES, P], U8)
            part = slice(first, first + count)
            nc.vector.quantize_mx(
                out=a_codes[n][:, part].rearrange("p g i -> p (g i)").bitcast(FP8X4),
                scales=a_scales[n][:, part].rearrange("p g i -> p (g i)"),
                in_=grouped_slots(n, first, count).rearrange("p g i t -> p (g i t)"),
            )

        def agg_tile(n):
            if n not in agg_bf:
                name = RELEASES.get(n, "aggbf%d" % n)
                agg_bf[n] = keep.tile([P, 2, P, 4], BF16, name=name, align_bytes=64)
            return agg_bf[n]

        def aggregate(n, half, passes=range(PASSES), order=range(PASSES)):
            if (n, half) not in agg_banks:
                agg_banks[n, half] = take_bank(("agg", n, half), [P, 4, P] if by_tile(n) else [P, 2, 2 * P])
            slots = range(4) if by_tile(n) else range(2 * half, 2 * half + 2)
            for g in passes:
                if by_tile(n):
                    codes, scales = a_codes[n][:, slot_of(n, half, g)], a_scales[n][:, slot_of(n, half, g)]
                else:
                    codes = a_codes[n][:, 2 * g : 2 * g + 2].rearrange("p h i -> p (h i)")
                    scales = a_scales[n][:, 2 * g : 2 * g + 2].rearrange("p h i -> p (h i)")
                for t in slots:
                    f_words, f_bytes = features_operand(g, t)
                    nc.tensor.matmul_mx(
                        out=agg_banks[n, half][:, t - slots[0], :],
                        lhsT=f_words.bitcast(FP8X4),
                        lhsT_scale=f_bytes,
                        rhs=codes.bitcast(FP8X4),
                        rhs_scale=scales,
                        start=(g == order[0] and t == slots[0]),
                        stop=(g == order[-1] and t == slots[-1]),
                    )

        def copy_agg(n, half):
            if by_tile(n):
                dst = agg_tile(n)[:, half]
            else:
                dst = agg_tile(n)[:].rearrange("p h i t -> p (h i) t")[:, :, 2 * half : 2 * half + 2]
            nc.scalar.copy(out=dst, in_=agg_banks[n, half][:].rearrange("p t i -> p i t"))
            give_bank(("agg", n, half))

        def quantize_agg(n, first=0, count=2):
            if n not in agg_codes:
                agg_codes[n] = ring("aggcodes", n, 8, [P, 2 * P], U32)
                agg_scales[n] = ring("aggscales", n, 8, [P, 2 * P], U8)
            cols = slice(first * P, (first + count) * P)
            nc.vector.quantize_mx(
                out=agg_codes[n][:, cols].bitcast(FP8X4),
                scales=agg_scales[n][:, cols],
                in_=agg_bf[n][:, first : first + count].rearrange("p h i t -> p (h i t)"),
            )

        def project(n, h, first=0, last=D):
            cols = slice(h * P, (h + 1) * P)
            product[n, h, first] = take_bank(("product", n, h, first), [P, last - first])
            nc.tensor.matmul_mx(
                out=product[n, h, first][:],
                lhsT=agg_codes[n][:, cols].bitcast(FP8X4),
                lhsT_scale=agg_scales[n][:, cols],
                rhs=w_words[:, 2 * first : 2 * last].bitcast(FP4X4),
                rhs_scale=w_scales[:, first:last],
                start=True,
                stop=True,
            )

        def add_bias(n, h, first=0, last=D):
            if (n, h) not in summed:
                summed[n, h] = ring("summed", len(summed), 6, [P, D], F32)
            nc.vector.tensor_tensor(
                out=summed[n, h][:, first:last], in0=product[n, h, first][:], in1=bias_row[:, first:last], op=ALU.add
            )
            give_bank(("product", n, h, first))

        rows = {}

        def rows_tile(n, h):
            if (n, h) not in rows:
                rows[n, h] = ring("rows", len(rows), 8, [P, D], F32)
            return rows[n, h]

        def store(n, h, first=0, last=D):
            r0 = (2 * n + h) * P
            nc.sync.dma_start(out=out[r0 : r0 + P, first:last], in_=rows[n, h][:, first:last])

        def relu_store(n, h, engine="scalar", first=0, last=D):
            dst, src = rows_tile(n, h)[:, first:last], summed[n, h][:, first:last]
            if engine == "vector":
                nc.vector.tensor_scalar(out=dst, in0=src, scalar1=0.0, scalar2=None, op0=ALU.max)
            else:
                nc.scalar.activation(out=dst, in_=src, func=ACT.Relu)
            store(n, h, first, last)

        def project_turned(n, half):
            product[n, half] = take_bank(("product", n, half), [P, 2, 2 * P])
            for cl in range(2):
                c = 2 * half + cl
                nc.tensor.matmul_mx(
                    out=product[n, half][:, cl, :],
                    lhsT=w_words[:, 2 * c * P : 2 * (c + 1) * P].bitcast(FP4X4),
                    lhsT_scale=w_scales[:, c * P : (c + 1) * P],
                    rhs=agg_codes[n][:].bitcast(FP8X4),
                    rhs_scale=agg_scales[n][:],
                    start=True,
                    stop=True,
                )

        def relu_of_turned(n, half):
            if n not in relu_turned:
                relu_turned[n] = ring("reluturned", len(relu_turned), 3, [P, 4, 2 * P], F32)
            for cl in range(2):
                c = 2 * half + cl
                nc.scalar.activation(
                    out=relu_turned[n][:, c, :],
                    in_=product[n, half][:, cl, :],
                    func=ACT.Relu,
                    bias=bias_chunks[:, c : c + 1],
                )
            give_bank(("product", n, half))

        def turn_back(n, h):
            back[n, h] = take_bank(("back", n, h), [P, 4, P])
            for c in range(4):
                nc.tensor.transpose(back[n, h][:, c, :], relu_turned[n][:, c, h * P : (h + 1) * P], ident[:])

        def store_back(n, h):
            nc.scalar.copy(out=rows_tile(n, h)[:], in_=back[n, h][:].rearrange("p c n -> p (c n)"))
            give_bank(("back", n, h))
            store(n, h)

        make_identity(nc, ident[:])
        nc.vector.memset(bias_raw[:], 0.0)
        nc.vector.memset(w_scales[:].bitcast(I32), 0)

        load_a(0, 0, 0, PASS)
        load_scales(0, 1)
        load_a(0, 0, PASS, NODES)
        nc.sync.dma_start(out=bias_raw[0:4, :], in_=bg.rearrange("(c n) -> c n", n=P))
        load_scales(1, PASSES)
        load_a(0, 1, 0, QUARTER)
        load_f(0)
        load_a(0, 1, QUARTER, NODES)
        load_a(1, 0)
        load_f(1)
        load_f(2)
        load_f(3)
        load_a(1, 1)
        load_pair(2)
        load_pair(SIDE)
        load_pair(3)
        load_w()
        for n in range(4, SIDE):
            load_pair(n)

        widen(0, PASS, "vector")
        for g in range(1, PASSES):
            widen(g * PASS, (g + 1) * PASS, "scalar")
        nc.scalar.copy(out=bias_lines[:], in_=bias_raw[:])
        f_grouped[0] = keep.tile([P, 4, P, 4], BF16, name="fgrouped0", align_bytes=64)
        group_features(0, "gpsimd", 0, UNITS)
        widen(NODES, NODES + PASS, "scalar")
        widen(NODES + PASS, NODES + QUARTER, "scalar")
        widen(NODES + QUARTER, PAIR, "scalar")
        widen(PAIR, PAIR + NODES, "scalar")
        for g in range(PASSES):
            turn(0, 0, g, 1)
        for g in range(PASSES):
            scale_turned(0, 0, g, 1)
            turn(0, 1, g, 1)
        f_grouped[1] = keep.tile([P, 4, P, 4], BF16, name="stage0", align_bytes=64)
        group_features(1, "scalar", 0, UNITS)
        for g in range(PASSES):
            scale_turned(0, 1, g, 1)
        turn(1, 0, 0)
        turn(1, 0, 2)
        chunks = bias_to_partitions()
        spread_bias((0, 1))
        copy_chunks(chunks)
        quantize_rows(0, 0, PASSES)
        quantize_rows(0, PASSES, PASSES)
        quantize_features(0)
        quantize_features(1)

        f_grouped[2] = keep.tile([P, 4, P, 4], BF16, name="stage0", align_bytes=64)
        f_grouped[3] = keep.tile([P, 4, P, 4], BF16, name="fgrouped3", align_bytes=64)
        group_features(2, "gpsimd", 0, UNITS)
        group_features(3, "scalar", 0, EARLY_UNITS)
        widen(PAIR + NODES, PAIR + NODES + QUARTER, "scalar")
        widen(PAIR + NODES + QUARTER, 2 * PAIR, "scalar")
        widen(2 * PAIR, 2 * PAIR + NODES, "scalar")
        group_features(3, "scalar", EARLY_UNITS, UNITS)
        widen_side(0)
        widen(2 * PAIR + NODES, 3 * PAIR - QUARTER, "scalar")
        widen(3 * PAIR - QUARTER, 3 * PAIR, "scalar")
        aggregate(0, 0, (0,))
        aggregate(0, 1, (0,))
        turn(1, 1, 0)
        turn(1, 1, 2)
        aggregate(0, 0, (1,))
        aggregate(0, 1, (1,))
        scale_turned(1, 0, 0)
        scale_turned(1, 0, 2)
        turn(2, 0, 0)
        turn(2, 0, 2)
        spread_bias((2, 3))
        turn_side(0)
        copy_bias()
        scale_side(0, (0, 1))
        widen_side(1)
        scale_turned(1, 1, 0)
        scale_turned(1, 1, 2)
        quantize_features(3)
        quantize_features(2)
        quantize_rows(1)

        widen(starts[3], starts[4], "gpsimd")
        for g in (3, 2):
            for h in range(2):
                aggregate(0, h, (g,), FIRST_ORDER)
        turn(2, 1, 0)
        turn(2, 1, 2)
        turn_side(1)
        copy_agg(0, 0)
        scale_side(0, (2, 3))
        copy_agg(0, 1)
        aggregate(1, 0)
        aggregate(1, 1)
        widen(3 * PAIR, 3 * PAIR + QUARTER, "scalar")
        scale_side(1, (0, 1))
        widen_side(2)
        scale_side(1, (2, 3))
        scale_turned(2, 0, 0)
        turn(3, 0, 0)
        turn_side(2)
        copy_agg(1, 0)
        copy_agg(1, 1)
        scale_turned(2, 0, 2)
        scale_turned(2, 1, 0)
        scale_turned(2, 1, 2)


        quantize_agg(0)
        quantize_rows(2)
        widen(starts[4], starts[5], "gpsimd")
        turn(3, 0, 2)
        project_turned(0, 0)
        project_turned(0, 1)
        turn(3, 1, 0)
        turn(3, 1, 2)
        widen_side(3)
        scale_side(2)
        relu_of_turned(0, 0)
        relu_of_turned(0, 1)
        for g in range(3):
            group_side(g)
        aggregate(2, 0)
        scale_turned(3, 0, 0)
        turn_side(3, turn_names)
        aggregate(2, 1, (0, 1))
        for h in range(2):
            turn_back(0, h)
        scale_turned(3, 0, 2)
        turn(4, 0, 0)
        aggregate(2, 1, (2, 3))
        copy_agg(2, 0)
        copy_agg(2, 1)
        for h in range(2):
            store_back(0, h)
        scale_turned(3, 1, 0)
        scale_turned(3, 1, 2)
        scale_side_on_vector(3)

        quantize_rows(SIDE, 0, PASSES)
        quantize_rows(SIDE, PASSES, PASSES)
        quantize_agg(1)
        quantize_rows(3)
        widen(starts[5], starts[6] - SHARE, "gpsimd")
        turn(4, 0, 2)
        turn(4, 1, 0)
        aggregate(SIDE, 0)
        project_turned(1, 0)
        project_turned(1, 1)
        turn(4, 1, 2)
        aggregate(SIDE, 1)
        widen(starts[6] - SHARE, starts[6], "scalar")
        relu_of_turned(1, 0)
        copy_agg(SIDE, 0)
        relu_of_turned(1, 1)
        scale_turned(4, 0, 0)
        turn(5, 0, 0)
        aggregate(3, 0)
        aggregate(3, 1)
        copy_agg(SIDE, 1)
        scale_on_scalar(5, 0, 0, 0)
        scale_turned(4, 0, 2)
        scale_turned(4, 1, 0)
        scale_turned(4, 1, 2)
        turn(5, 0, 2)
        for h in range(2):
            turn_back(1, h)
        copy_agg(3, 0)
        scale_on_scalar(5, 0, 0, 1)
        for h in range(2):
            store_back(1, h)
        copy_agg(3, 1)

        quantize_agg(2)
        quantize_agg(SIDE)
        quantize_rows(4)
        widen(starts[6], starts[7], "gpsimd")
        turn(5, 1, 0)
        project(SIDE, 0)
        project(SIDE, 1)
        turn(5, 1, 2)
        turn(LAST, 0, 0)
        project_turned(2, 0)
        project_turned(2, 1)
        scale_turned(5, 0, 2)
        scale_turned(5, 1, 0)
        add_bias(SIDE, 0)
        add_bias(SIDE, 1)
        aggregate(4, 0)
        turn(LAST, 0, 2)
        group_on_scalar(5, 0, 0)
        scale_on_scalar(LAST, 0, 0, 0)
        relu_of_turned(2, 0)
        relu_of_turned(2, 1)
        aggregate(4, 1)
        copy_agg(4, 0)
        scale_turned(5, 1, 2)
        scale_on_scalar(LAST, 0, 0, 1)
        copy_agg(4, 1)
        group_on_scalar(LAST, 0, 0)

        quantize_agg(3)
        quantize_rows(5)
        project(3, 0)
        turn(LAST, 1, 0)
        for h in range(2):
            turn_back(2, h)
        aggregate(5, 0)
        turn(LAST, 1, 2)
        scale_turned(LAST, 0, 2)
        add_bias(3, 0)
        scale_turned(LAST, 1, 0)
        quantize_agg(4)
        project(3, 1)
        project(4, 0)
        for h in range(2):
            store_back(2, h)
        project(4, 1)
        aggregate(5, 1)
        quantize_rows(LAST, 0, PASSES)
        quantize_rows(LAST, PASSES, 2)
        scale_turned(LAST, 1, 2, 1, 0, False)
        add_bias(3, 1)
        quantize_rows(LAST, PASSES + 2, 1)
        relu_store(SIDE, 0)
        copy_agg(5, 0)
        relu_store(SIDE, 1)
        aggregate(LAST, 0)
        relu_store(3, 0)
        copy_agg(5, 1)
        add_bias(4, 0)
        add_bias(4, 1)
        scale_turned(LAST, 1, 3, 1, 1)
        quantize_agg(5)
        quantize_rows(LAST, PASSES + 3, 1)
        aggregate(LAST, 1, (0, 1, 2))
        project(5, 0)
        aggregate(LAST, 1, (3,))
        project(5, 1)
        relu_store(3, 1)
        copy_agg(LAST, 0)
        relu_store(4, 0, "vector")
        relu_store(4, 1)
        quantize_agg(LAST, 0, 1)
        project(LAST, 0)
        add_bias(5, 0)
        copy_agg(LAST, 1)
        add_bias(5, 1)
        quantize_agg(LAST, 1, 1)
        relu_store(5, 0)
        add_bias(LAST, 0)
        project(LAST, 1, 0, D // 2)
        project(LAST, 1, D // 2, D)
        relu_store(5, 1)
        relu_store(LAST, 0)
        add_bias(LAST, 1, 0, D // 2)
        add_bias(LAST, 1, D // 2, D)
        relu_store(LAST, 1, "vector", 0, D // 2)
        relu_store(LAST, 1, "vector", D // 2, D)
